import numpy as np
import ml_dtypes


def mxq(x, axis, fmt="e4m3"):
    dtype, down = {"e4m3": (ml_dtypes.float8_e4m3fn, 7), "e5m2": (ml_dtypes.float8_e5m2, 14)}[fmt]
    v = np.moveaxis(np.asarray(x, np.float32).astype(ml_dtypes.bfloat16).astype(np.float64), axis, -1)
    blocks = v.reshape(v.shape[:-1] + (-1, 32))
    amax = np.abs(blocks).max(-1, keepdims=True)
    byte = np.maximum(np.where(amax > 0, np.frexp(amax)[1] - 1 + 127, 0) - down, 1)
    scale = np.exp2(byte - 127.0)
    codes = (blocks / scale).astype(np.float32).astype(dtype).astype(np.float64)
    return np.moveaxis((codes * scale).reshape(v.shape), -1, axis)


WIDE = False


def mx_kscale(k):
    if not WIDE:
        return np.ones(k)
    levels = np.array([10, -10, 5, -5, 0])
    if k % 512:
        return np.exp2(np.random.permutation(np.resize(levels, k // 32))).repeat(32)
    a = np.empty((k // 512, 16))
    for p in range(k // 512):
        a[p, :8] = np.random.permutation(np.resize(levels, 8))
        for g in range(8):
            far = levels[np.abs(levels - a[p, g]) >= 10]
            a[p, g + 8] = far[np.random.randint(len(far))]
    return np.exp2(a.ravel()).repeat(32)


BF16 = ml_dtypes.bfloat16


def bf(x):
    return np.asarray(x, np.float32).astype(BF16)


def f64(x):
    return np.asarray(x).astype(np.float64)


B, T, DM, DH, L = 4, 512, 1024, 1024, 512


def sigmoid(x):
    return 1.0 / (1.0 + np.exp(-x))


def draw0():
    s, t = mx_kscale(DM), mx_kscale(DH)
    return {"q": bf(np.random.standard_normal((B, T, DM)) * s),
            "num": bf(np.random.standard_normal((B, T, DH)) * 1.9 * np.sqrt(T) * t),
            "den": bf(0.5 * T * (0.5 + np.random.random((B, T, DH)))),
            "Wq": bf(np.random.standard_normal((DH, DM)) / np.sqrt(DM) / s),
            "Wo": bf(np.random.standard_normal((DM, DH)) * 5.0 / np.sqrt(DH) / t)}


def core(q, num, den, Wq, Wo):
    Q = mxq(f64(q), 2, "e4m3") @ mxq(f64(Wq), 1, "e4m3").T
    Yt = sigmoid(Q) * f64(num) / f64(den)
    return mxq(Yt, 2, "e4m3") @ mxq(f64(Wo), 1, "e4m3").T


def e4m3fn_bytes(y):
    return np.clip(np.asarray(y, np.float64), -448.0, 448.0).astype(np.float32).astype(ml_dtypes.float8_e4m3fn).view(np.uint8)


def e4m3fn_values(b):
    return np.asarray(b, np.uint8).view(ml_dtypes.float8_e4m3fn).astype(np.float64)


def setup_inputs():
    d = draw0()
    x0 = np.asarray(d['q']).astype(np.float64)
    s = (np.max(np.abs(x0), axis=(0, 1), keepdims=True) / 448.0).astype(np.float32)
    out = {}
    for k, v in d.items():
        if k == 'q':
            out['q_bytes'] = e4m3fn_bytes(x0 / s.astype(np.float64))
            out['q_scale'] = s
        else:
            out[k] = v
    return out


def reference(q_bytes, q_scale, num, den, Wq, Wo):
    return core(e4m3fn_values(q_bytes) * q_scale.astype(np.float64), num, den, Wq, Wo)

@@ -1,0 +1,417 @@
+from contextlib import ExitStack
+
+import concourse.mybir as mybir
+from concourse.masks import make_identity
+
+F32 = mybir.dt.float32
+BF16 = mybir.dt.bfloat16
+U32 = mybir.dt.uint32
+U8 = mybir.dt.uint8
+FP8 = mybir.dt.float8_e4m3fn
+FP8X4 = mybir.dt.float8_e4m3fn_x4
+ACT = mybir.ActivationFunctionType
+ALU = mybir.AluOpType
+
+P = 128
+T, DM, DH, DO = 2048, 1024, 1024, 1024
+CH = 256
+NC = T // CH
+FLOPS = 2 * T * DM * DH + 2 * T * DH * DO
+
+
+def tile_aftfull_pb_kernel(tc, q_bytes, q_scale, num, den, Wq, Wo, out):
+    nc = tc.nc
+    with ExitStack() as ctx:
+        sb = ctx.enter_context(tc.tile_pool(name="sb", bufs=1))
+        ps = ctx.enter_context(tc.psum_pool(name="ps", bufs=1))
+
+        q_v = q_bytes.flatten_outer_dims().rearrange("(c p i) d -> c p i d", p=P, i=2)
+        num_v = num.flatten_outer_dims().rearrange("(c p i) d -> c p i d", p=P, i=2)
+        den_v = den.flatten_outer_dims().rearrange("(c p i) d -> c p i d", p=P, i=2)
+        out_v = out.flatten_outer_dims().rearrange("(c p i) d -> c p i d", p=P, i=2)
+        wq_v = Wq.rearrange("(g m t) k -> g m t k", m=P, t=4)
+        wo_v = Wo.rearrange("(j m) k -> j m k", m=P)
+
+        ident = sb.tile([P, P], F32, name="ident")
+        make_identity(nc, ident[:])
+        sc = sb.tile([P, 2, 4], F32, name="sc")
+
+        raw = {}
+        banks = {}
+        wts = {}
+        wq_c = {}
+        wo_c = {}
+        qb = {}
+        qx = {}
+        qt = {}
+        qc = {}
+        dent = {}
+        numt = {}
+        w = {}
+        rr = {}
+        s = {}
+        y = {}
+        yc = {}
+        o = {}
+
+        def load_sc():
+            nc.sync.dma_start(out=sc[:], in_=q_scale.rearrange("a b (g p t) -> p (a b g) t", p=P, t=4))
+
+        def load_w(key, src):
+            raw[key] = sb.tile([P, DM], BF16, name="wraw", tag="wraw", bufs=8)
+            nc.sync.dma_start(out=raw[key][:], in_=src)
+
+        def load_wq(G, t):
+            load_w(("q", G, t), wq_v[G][:, t, :])
+
+        def load_wo(j):
+            load_w(("o", j), wo_v[j])
+
+        def load_q(c):
+            qb[c] = sb.tile([P, 2, DM], U8, name="qb", tag="qb", bufs=4)
+            nc.sync.dma_start(out=qb[c][:], in_=q_v[c])
+
+        def load_den(c, i):
+            dent[c, i] = sb.tile([P, DH], BF16, name="dent", tag="dent", bufs=6)
+            nc.sync.dma_start(out=dent[c, i][:], in_=den_v[c][:, i, :])
+
+        def load_num(c):
+            numt[c] = sb.tile([P, 2, DH], BF16, name="numt", tag="numt", bufs=4)
+            nc.sync.dma_start(out=numt[c][:], in_=num_v[c])
+
+        def w_transpose(key):
+            words = raw[key][:].bitcast(F32)
+            bank = ps.tile([P, 2, 2, P], F32, name="bank_t", tag="bank_t", bufs=4)
+            for g in range(2):
+                for u in range(2):
+                    nc.tensor.transpose(bank[:, g, u, :], words[:, 256 * g + u : 256 * (g + 1) : 2], ident[:])
+            banks[key] = bank
+
+        def w_copy(key, dst, on_scalar):
+            copy = nc.scalar.copy if on_scalar else nc.vector.tensor_copy
+            copy(
+                out=dst.bitcast(F32),
+                in_=banks[key][:].rearrange("p g u m -> p g m u"),
+            )
+
+        def wq_transpose(G, t):
+            w_transpose(("q", G, t))
+
+        def wq_copy(G, t, on_scalar=False):
+            h = t // 2
+            if t % 2 == 0:
+                wts[G, h] = sb.tile([P, 2, 2, P, 4], BF16, name="wt", tag="wt", bufs=2, align_bytes=64)
+            w_copy(("q", G, t), wts[G, h][:, t % 2, :, :, :], on_scalar)
+
+        def wq_quant(G, h):
+            codes = sb.tile([P, 2, 2, P], U32, name=f"wqc{G}{h}", align_bytes=64)
+            scales = sb.tile([P, 2, 2, P], U8, name=f"wqs{G}{h}", align_bytes=64)
+            nc.vector.quantize_mx(
+                out=codes[:].rearrange("p a g m -> p (a g m)").bitcast(FP8X4),
+                scales=scales[:].rearrange("p a g m -> p (a g m)"),
+                in_=wts[G, h][:].rearrange("p a g m f -> p (a g m f)"),
+            )
+            wq_c[G, h] = (codes, scales)
+
+        def wo_transpose(j):
+            w_transpose(("o", j))
+
+        def wo_copy(j, on_scalar=False):
+            oh, jj = divmod(j, 4)
+            if jj == 0:
+                wts[oh] = sb.tile([P, 2, 512, 4], BF16, name="wot", tag="wot", bufs=1, align_bytes=64)
+            w_copy(("o", j), wts[oh][:, :, jj * P : (jj + 1) * P, :], on_scalar)
+
+        def wo_quant(oh):
+            codes = sb.tile([P, 2, 512], U32, name=f"woc{oh}", align_bytes=64)
+            scales = sb.tile([P, 2, 512], U8, name=f"wos{oh}", align_bytes=64)
+            for g in range(2):
+                nc.vector.quantize_mx(
+                    out=codes[:, g, :].bitcast(FP8X4),
+                    scales=scales[:, g, :],
+                    in_=wts[oh][:, g, :, :].rearrange("p o f -> p (o f)"),
+                )
+            wo_c[oh] = (codes, scales)
+
+        def cast(c, on_scalar=False):
+            qx[c] = sb.tile([P, 2, DM], BF16, name="qx", tag="qx", bufs=2)
+            copy = nc.scalar.copy if on_scalar else nc.vector.tensor_copy
+            copy(out=qx[c][:], in_=qb[c][:].bitcast(FP8))
+
+        def q_transpose(c, g):
+            words = qx[c][:].rearrange("p i k -> p (i k)").bitcast(F32)
+            bank = ps.tile([P, 2, 2, P], F32, name="bank_t", tag="bank_t", bufs=4)
+            for i in range(2):
+                s0 = 512 * i + 256 * g
+                for u in range(2):
+                    nc.tensor.transpose(bank[:, u, i, :], words[:, s0 + u : s0 + 256 : 2], ident[:])
+            banks["x", c, g] = bank
+
+        def q_scale_up(c, g):
+            if g == 0:
+                qt[c] = sb.tile([P, 2, CH, 4], BF16, name="qt", tag="qt", bufs=2, align_bytes=64)
+            nc.vector.tensor_tensor(
+                out=qt[c][:, g, :, :].rearrange("p n (u e) -> p n u e", u=2),
+                in0=banks["x", c, g][:].rearrange("p u i n -> p (u i n)").bitcast(BF16).rearrange("p (u n e) -> p n u e", u=2, e=2),
+                in1=sc[:, g, :].rearrange("p (u e) -> p u e", u=2).unsqueeze(1).to_broadcast([P, CH, 2, 2]),
+                op=ALU.mult,
+            )
+
+        def q_quant(c):
+            codes = sb.tile([P, 2, CH], U32, name="qcod", tag="qcod", bufs=3, align_bytes=64)
+            scales = sb.tile([P, 2, CH], U8, name="qscl", tag="qscl", bufs=3, align_bytes=64)
+            nc.vector.quantize_mx(
+                out=codes[:].rearrange("p g n -> p (g n)").bitcast(FP8X4),
+                scales=scales[:].rearrange("p g n -> p (g n)"),
+                in_=qt[c][:].rearrange("p g n f -> p (g n f)"),
+            )
+            qc[c] = (codes, scales)
+
+        def rsqrt(c, i):
+            w[c, i] = sb.tile([P, DH], F32, name="w", tag="w", bufs=16)
+            nc.scalar.activation(out=w[c, i][:], in_=dent[c, i][:], func=ACT.Abs_reciprocal_sqrt)
+
+        def square(c, i, on_gpsimd=False):
+            x = w[c, i][:]
+            if on_gpsimd:
+                nc.gpsimd.tensor_tensor(out=x, in0=x, in1=x, op=ALU.mult)
+            else:
+                nc.scalar.activation(out=x, in_=x, func=ACT.Square)
+
+        def ratio(c, i, on_vector=False):
+            rr[c, i] = sb.tile([P, 2, 4, P], F32, name="r", tag="r", bufs=4)
+            eng = nc.vector if on_vector else nc.gpsimd
+            eng.tensor_tensor(
+                out=rr[c, i][:].rearrange("p g t m -> p g m t"),
+                in0=numt[c][:, i, :].rearrange("p (g m t) -> p g m t", g=2, t=4),
+                in1=w[c, i][:].rearrange("p (g m t) -> p g m t", g=2, t=4),
+                op=ALU.mult,
+            )
+
+        def m1(c, G, tp):
+            codes, scales = qc[c]
+            wc, ws = wq_c[G, tp]
+            bank = ps.tile([P, 2, CH], F32, name="bank_m", tag="bank_m", bufs=4)
+            for tt in range(2):
+                for g in range(2):
+                    nc.tensor.matmul_mx(
+                        out=bank[:, tt, :],
+                        lhsT=wc[:, tt, g, :].bitcast(FP8X4),
+                        lhsT_scale=ws[:, tt, g, :],
+                        rhs=codes[:, g, :].bitcast(FP8X4),
+                        rhs_scale=scales[:, g, :],
+                        start=(g == 0),
+                        stop=(g == 1),
+                    )
+            banks["m1", c, G, tp] = bank
+
+        def sig(c, G, tp):
+            if tp == 0:
+                s[c, G] = sb.tile([P, 4, CH], F32, name="s", tag="s", bufs=3)
+            nc.scalar.activation(out=s[c, G][:, 2 * tp : 2 * tp + 2, :], in_=banks["m1", c, G, tp][:], func=ACT.Sigmoid)
+
+        def r_transpose(c, G, i):
+            bank = ps.tile([P, 4, P], F32, name="bank_t", tag="bank_t", bufs=4)
+            for t in range(4):
+                nc.tensor.transpose(bank[:, t, :], rr[c, i][:, G, t, :], ident[:])
+            banks["r", c, G, i] = bank
+
+        def fin(c, G, i):
+            if i == 0:
+                y[c, G] = sb.tile([P, CH, 4], BF16, name="y", tag="y", bufs=3, align_bytes=64)
+            nc.vector.tensor_tensor(
+                out=y[c, G][:, i * P : (i + 1) * P, :],
+                in0=banks["r", c, G, i][:].rearrange("p t n -> p n t"),
+                in1=s[c, G][:, :, i * P : (i + 1) * P].rearrange("p t n -> p n t"),
+                op=ALU.mult,
+            )
+
+        def y_quant(c, G):
+            codes = sb.tile([P, CH], U32, name="ycod", tag="ycod", bufs=4, align_bytes=64)
+            scales = sb.tile([P, CH], U8, name="yscl", tag="yscl", bufs=4, align_bytes=64)
+            nc.vector.quantize_mx(out=codes[:].bitcast(FP8X4), scales=scales[:], in_=y[c, G][:].rearrange("p n t -> p (n t)"))
+            yc[c, G] = (codes, scales)
+
+        def m2(c, i, oh):
+            bank = ps.tile([P, 512], F32, name="bank_m", tag="bank_m", bufs=4)
+            for G in range(2):
+                codes, scales = yc[c, G]
+                nc.tensor.matmul_mx(
+                    out=bank[:],
+                    lhsT=codes[:, i * P : (i + 1) * P].bitcast(FP8X4),
+                    lhsT_scale=scales[:, i * P : (i + 1) * P],
+                    rhs=wo_c[oh][0][:, G, :].bitcast(FP8X4),
+                    rhs_scale=wo_c[oh][1][:, G, :],
+                    start=(G == 0),
+                    stop=(G == 1),
+                )
+            banks["m2", c, i, oh] = bank
+
+        def copy_out(c, i, oh, on_vector=False):
+            if oh == 0:
+                o[c, i] = sb.tile([P, DO], F32, name="o", tag="o", bufs=4)
+            copy = nc.vector.tensor_copy if on_vector else nc.scalar.copy
+            copy(out=o[c, i][:, 512 * oh : 512 * (oh + 1)], in_=banks["m2", c, i, oh][:])
+
+        def store(c, i):
+            nc.sync.dma_start(out=out_v[c][:, i, :], in_=o[c, i][:])
+
+        with tc.manual_schedule():
+
+            load_den(0, 0)
+            load_wq(0, 0)
+            load_q(0)
+            load_sc()
+            load_wq(0, 1)
+            load_den(0, 1)
+            load_wq(0, 2)
+            load_den(1, 0)
+            load_wq(0, 3)
+            rsqrt(0, 0)
+            load_den(1, 1)
+            load_wq(1, 0)
+            rsqrt(0, 1)
+            load_den(2, 0)
+            load_wq(1, 1)
+            rsqrt(1, 0)
+            load_den(2, 1)
+            load_wq(1, 2)
+            rsqrt(1, 1)
+            load_den(3, 0)
+            load_wq(1, 3)
+            load_q(1)
+            rsqrt(2, 0)
+            load_den(3, 1)
+            load_num(0)
+            rsqrt(2, 1)
+            load_den(4, 0)
+            load_wo(0)
+            load_wo(1)
+            rsqrt(3, 0)
+            load_den(4, 1)
+            load_wo(2)
+            rsqrt(3, 1)
+            load_den(5, 0)
+            load_wo(3)
+            rsqrt(4, 0)
+            load_den(5, 1)
+            load_num(1)
+            rsqrt(4, 1)
+            load_den(6, 0)
+            load_wo(4)
+            rsqrt(5, 0)
+            load_den(6, 1)
+            load_wo(5)
+            rsqrt(5, 1)
+            load_den(7, 0)
+            load_wo(6)
+            rsqrt(6, 0)
+            load_den(7, 1)
+            load_wo(7)
+            rsqrt(6, 1)
+            load_q(2)
+            load_num(2)
+            rsqrt(7, 0)
+            rsqrt(7, 1)
+            load_q(3)
+            load_num(3)
+            load_q(4)
+            load_q(5)
+
+            for c in range(4):
+                for i in range(2):
+                    square(c, i, on_gpsimd=True)
+
+            wq_transpose(0, 0)
+            wq_copy(0, 0)
+            cast(0)
+            wq_transpose(0, 1)
+            wq_copy(0, 1)
+            q_transpose(0, 0)
+            q_transpose(0, 1)
+            wq_transpose(0, 2)
+            q_scale_up(0, 0)
+            wq_quant(0, 0)
+            q_scale_up(0, 1)
+            wq_copy(0, 2)
+            wq_transpose(0, 3)
+            q_quant(0)
+            wq_copy(0, 3)
+            for t in range(4):
+                wq_transpose(1, t)
+                if t == 2:
+                    cast(1)
+                    wq_quant(0, 1)
+                wq_copy(1, t)
+            for g in range(2):
+                q_transpose(1, g)
+            wq_quant(1, 0)
+            q_scale_up(1, 0)
+            wq_quant(1, 1)
+            q_scale_up(1, 1)
+            ratio(0, 0, on_vector=True)
+            q_quant(1)
+            ratio(0, 1, on_vector=True)
+            cast(2)
+            for j in range(4):
+                wo_transpose(j)
+                wo_copy(j)
+
+            for n in range(NC + 1):
+                if n < NC:
+                    for G in range(2):
+                        for tp in range(2):
+                            m1(n, G, tp)
+                            sig(n, G, tp)
+                if n == NC - 1:
+                    for G in range(2):
+                        for i in range(2):
+                            r_transpose(n, G, i)
+                            fin(n, G, i)
+                        y_quant(n, G)
+                if n == 0:
+                    wo_quant(0)
+                if n > 0:
+                    for i in range(2):
+                        for oh in range(2):
+                            m2(n - 1, i, oh)
+                            copy_out(n - 1, i, oh, on_vector=(n == NC and oh == 1))
+                        store(n - 1, i)
+                if 4 <= n + 1 < NC:
+                    for i in range(2):
+                        square(n + 1, i)
+                if n < NC - 1:
+                    r_transpose(n, 0, 0)
+                    r_transpose(n, 0, 1)
+                    r_transpose(n, 1, 0)
+                    r_transpose(n, 1, 1)
+                    fin(n, 0, 0)
+                    fin(n, 0, 1)
+                    fin(n, 1, 0)
+                    y_quant(n, 0)
+                    fin(n, 1, 1)
+                    if n == 0:
+                        for j in range(4, 8):
+                            wo_transpose(j)
+                            wo_copy(j, on_scalar=True)
+                            if j == 4:
+                                y_quant(n, 1)
+                        wo_quant(1)
+                    for i in range(2):
+                        ratio(n + 1, i, on_vector=True)
+                    if n + 2 < NC:
+                        q_transpose(n + 2, 0)
+                        q_transpose(n + 2, 1)
+                        q_scale_up(n + 2, 0)
+                        if n > 0:
+                            y_quant(n, 1)
+                        q_scale_up(n + 2, 1)
+                        if n + 3 < NC:
+                            cast(n + 3, on_scalar=True)
+                        q_quant(n + 2)
+                    else:
+                        y_quant(n, 1)
+                    if n + 4 < NC:
+                        load_num(n + 4)
+                    if n + 6 < NC:
+                        load_q(n + 6)

@@ -36,23 +36,15 @@ def tile_aftfull_pb_kernel(tc, q_bytes, q_scale, num, den, Wq, Wo, out):
         make_identity(nc, ident[:])
         sc = sb.tile([P, 2, 4], F32, name="sc")
 
-        raw = {}
-        banks = {}
-        wts = {}
-        wq_c = {}
-        wo_c = {}
-        qb = {}
-        qx = {}
-        qt = {}
-        qc = {}
-        dent = {}
-        numt = {}
-        w = {}
-        rr = {}
-        s = {}
-        y = {}
-        yc = {}
-        o = {}
+        raw, banks, wts, wq_c, wo_c = {}, {}, {}, {}, {}
+        qb, qx, qt, qc = {}, {}, {}, {}
+        dent, numt, w, rr, s, y, yc, o = {}, {}, {}, {}, {}, {}, {}, {}
+
+        def turn_bank(shape):
+            return ps.tile(shape, F32, name="bank_t", tag="bank_t", bufs=4)
+
+        def sum_bank(shape):
+            return ps.tile(shape, F32, name="bank_m", tag="bank_m", bufs=4)
 
         def load_sc():
             nc.sync.dma_start(out=sc[:], in_=q_scale.rearrange("a b (g p t) -> p (a b g) t", p=P, t=4))
@@ -68,79 +60,75 @@ def tile_aftfull_pb_kernel(tc, q_bytes, q_scale, num, den, Wq, Wo, out):
             load_w(("o", j), wo_v[j])
 
         def load_q(c):
-            qb[c] = sb.tile([P, 2, DM], U8, name="qb", tag="qb", bufs=4)
-            nc.sync.dma_start(out=qb[c][:], in_=q_v[c])
+            qb[c] = sb.tile([P, 2 * DM], U8, name="qb", tag="qb", bufs=NC)
+            nc.sync.dma_start(out=qb[c][:], in_=q_v[c].rearrange("p i d -> p (i d)"))
 
         def load_den(c, i):
-            dent[c, i] = sb.tile([P, DH], BF16, name="dent", tag="dent", bufs=6)
+            dent[c, i] = sb.tile([P, DH], BF16, name="dent", tag="dent", bufs=4)
             nc.sync.dma_start(out=dent[c, i][:], in_=den_v[c][:, i, :])
 
         def load_num(c):
-            numt[c] = sb.tile([P, 2, DH], BF16, name="numt", tag="numt", bufs=4)
+            numt[c] = sb.tile([P, 2, DH], BF16, name="numt", tag="numt", bufs=6)
             nc.sync.dma_start(out=numt[c][:], in_=num_v[c])
 
-        def w_transpose(key):
-            words = raw[key][:].bitcast(F32)
-            bank = ps.tile([P, 2, 2, P], F32, name="bank_t", tag="bank_t", bufs=4)
+        def grouped():
+            return sb.tile([P, 2048], BF16, name="grouped", tag="grouped", bufs=3, align_bytes=64)
+
+        def shared(c):
+            return sb.tile([P, 2048], BF16, name="shared", tag=f"shared{c % 2}", bufs=1, align_bytes=64)
+
+        def wq_transpose(G, t):
+            words = raw["q", G, t][:].bitcast(F32)
+            bank = turn_bank([P, 2, 2, P])
             for g in range(2):
                 for u in range(2):
                     nc.tensor.transpose(bank[:, g, u, :], words[:, 256 * g + u : 256 * (g + 1) : 2], ident[:])
-            banks[key] = bank
+            banks["wq", G, t] = bank
 
-        def w_copy(key, dst, on_scalar):
-            copy = nc.scalar.copy if on_scalar else nc.vector.tensor_copy
-            copy(
-                out=dst.bitcast(F32),
-                in_=banks[key][:].rearrange("p g u m -> p g m u"),
-            )
+        def wq_copy(G, t, eng):
+            u, e = divmod(t, 2)
+            if e == 0:
+                wts["q", G, u] = grouped()
+            dst = wts["q", G, u][:, 1024 * e : 1024 * (e + 1)].bitcast(F32)
+            eng(out=dst.rearrange("p (g m u) -> p g m u", g=2, u=2), in_=banks["wq", G, t][:].rearrange("p g u m -> p g m u"))
 
-        def wq_transpose(G, t):
-            w_transpose(("q", G, t))
-
-        def wq_copy(G, t, on_scalar=False):
-            h = t // 2
-            if t % 2 == 0:
-                wts[G, h] = sb.tile([P, 2, 2, P, 4], BF16, name="wt", tag="wt", bufs=2, align_bytes=64)
-            w_copy(("q", G, t), wts[G, h][:, t % 2, :, :, :], on_scalar)
-
-        def wq_quant(G, h):
-            codes = sb.tile([P, 2, 2, P], U32, name=f"wqc{G}{h}", align_bytes=64)
-            scales = sb.tile([P, 2, 2, P], U8, name=f"wqs{G}{h}", align_bytes=64)
+        def wq_quant(G, u):
+            codes = sb.tile([P, 2, 2, P], U32, name=f"wqc{G}{u}", align_bytes=64)
+            scales = sb.tile([P, 2, 2, P], U8, name=f"wqs{G}{u}", align_bytes=64)
             nc.vector.quantize_mx(
-                out=codes[:].rearrange("p a g m -> p (a g m)").bitcast(FP8X4),
-                scales=scales[:].rearrange("p a g m -> p (a g m)"),
-                in_=wts[G, h][:].rearrange("p a g m f -> p (a g m f)"),
+                out=codes[:].rearrange("p e g m -> p (e g m)").bitcast(FP8X4),
+                scales=scales[:].rearrange("p e g m -> p (e g m)"),
+                in_=wts["q", G, u][:],
             )
-            wq_c[G, h] = (codes, scales)
+            wq_c[G, u] = (codes, scales)
 
-        def wo_transpose(j):
-            w_transpose(("o", j))
+        def wo_transpose(oh, g, h):
+            bank = turn_bank([P, 2, 2, P])
+            for j in range(2):
+                words = raw["o", 4 * oh + 2 * h + j][:].bitcast(F32)
+                for u in range(2):
+                    nc.tensor.transpose(bank[:, u, j, :], words[:, 256 * g + u : 256 * (g + 1) : 2], ident[:])
+            banks["wo", oh, g, h] = bank
 
-        def wo_copy(j, on_scalar=False):
-            oh, jj = divmod(j, 4)
-            if jj == 0:
-                wts[oh] = sb.tile([P, 2, 512, 4], BF16, name="wot", tag="wot", bufs=1, align_bytes=64)
-            w_copy(("o", j), wts[oh][:, :, jj * P : (jj + 1) * P, :], on_scalar)
+        def wo_copy(oh, g, h, eng):
+            if h == 0:
+                wts["o", oh, g] = grouped()
+            dst = wts["o", oh, g][:, 1024 * h : 1024 * (h + 1)].bitcast(F32)
+            eng(out=dst.rearrange("p (n u) -> p n u", u=2), in_=banks["wo", oh, g, h][:].rearrange("p u j m -> p (j m) u"))
 
-        def wo_quant(oh):
-            codes = sb.tile([P, 2, 512], U32, name=f"woc{oh}", align_bytes=64)
-            scales = sb.tile([P, 2, 512], U8, name=f"wos{oh}", align_bytes=64)
-            for g in range(2):
-                nc.vector.quantize_mx(
-                    out=codes[:, g, :].bitcast(FP8X4),
-                    scales=scales[:, g, :],
-                    in_=wts[oh][:, g, :, :].rearrange("p o f -> p (o f)"),
-                )
-            wo_c[oh] = (codes, scales)
+        def wo_quant(oh, g):
+            codes = sb.tile([P, 512], U32, name=f"woc{oh}{g}", align_bytes=64)
+            scales = sb.tile([P, 512], U8, name=f"wos{oh}{g}", align_bytes=64)
+            nc.vector.quantize_mx(out=codes[:].bitcast(FP8X4), scales=scales[:], in_=wts["o", oh, g][:])
+            wo_c[oh, g] = (codes, scales)
 
-        def cast(c, on_scalar=False):
-            qx[c] = sb.tile([P, 2, DM], BF16, name="qx", tag="qx", bufs=2)
-            copy = nc.scalar.copy if on_scalar else nc.vector.tensor_copy
-            copy(out=qx[c][:], in_=qb[c][:].bitcast(FP8))
+        def cast(c, eng):
+            qx[c] = sb.tile([P, 2 * DM], BF16, name="qx", tag="qx", bufs=2)
+            eng(out=qx[c][:], in_=qb[c][:].bitcast(FP8))
 
         def q_transpose(c, g):
-            words = qx[c][:].rearrange("p i k -> p (i k)").bitcast(F32)
-            bank = ps.tile([P, 2, 2, P], F32, name="bank_t", tag="bank_t", bufs=4)
+            words = qx[c][:].bitcast(F32)
+            bank = turn_bank([P, 2, 2, P])
             for i in range(2):
                 s0 = 512 * i + 256 * g
                 for u in range(2):
@@ -149,9 +137,9 @@ def tile_aftfull_pb_kernel(tc, q_bytes, q_scale, num, den, Wq, Wo, out):
 
         def q_scale_up(c, g):
             if g == 0:
-                qt[c] = sb.tile([P, 2, CH, 4], BF16, name="qt", tag="qt", bufs=2, align_bytes=64)
+                qt[c] = sb.tile([P, 2048], BF16, name="qt", tag="qt", bufs=2, align_bytes=64)
             nc.vector.tensor_tensor(
-                out=qt[c][:, g, :, :].rearrange("p n (u e) -> p n u e", u=2),
+                out=qt[c][:, 1024 * g : 1024 * (g + 1)].rearrange("p (n u e) -> p n u e", u=2, e=2),
                 in0=banks["x", c, g][:].rearrange("p u i n -> p (u i n)").bitcast(BF16).rearrange("p (u n e) -> p n u e", u=2, e=2),
                 in1=sc[:, g, :].rearrange("p (u e) -> p u e", u=2).unsqueeze(1).to_broadcast([P, CH, 2, 2]),
                 op=ALU.mult,
@@ -163,255 +151,236 @@ def tile_aftfull_pb_kernel(tc, q_bytes, q_scale, num, den, Wq, Wo, out):
             nc.vector.quantize_mx(
                 out=codes[:].rearrange("p g n -> p (g n)").bitcast(FP8X4),
                 scales=scales[:].rearrange("p g n -> p (g n)"),
-                in_=qt[c][:].rearrange("p g n f -> p (g n f)"),
+                in_=qt[c][:],
             )
             qc[c] = (codes, scales)
 
         def rsqrt(c, i):
-            w[c, i] = sb.tile([P, DH], F32, name="w", tag="w", bufs=16)
-            nc.scalar.activation(out=w[c, i][:], in_=dent[c, i][:], func=ACT.Abs_reciprocal_sqrt)
+            w[c, i] = sb.tile([P, DH], F32, name="w", tag="w", bufs=2 * NC)
+            nc.scalar.activation(
+                out=w[c, i][:].rearrange("p (g t m) -> p g t m", g=2, t=4),
+                in_=dent[c, i][:].rearrange("p (g m t) -> p g t m", g=2, t=4),
+                func=ACT.Abs_reciprocal_sqrt,
+            )
 
-        def square(c, i, on_gpsimd=False):
-            x = w[c, i][:]
-            if on_gpsimd:
-                nc.gpsimd.tensor_tensor(out=x, in0=x, in1=x, op=ALU.mult)
-            else:
-                nc.scalar.activation(out=x, in_=x, func=ACT.Square)
+        def square(c, i):
+            nc.scalar.activation(out=w[c, i][:], in_=w[c, i][:], func=ACT.Square)
 
-        def ratio(c, i, on_vector=False):
-            rr[c, i] = sb.tile([P, 2, 4, P], F32, name="r", tag="r", bufs=4)
-            eng = nc.vector if on_vector else nc.gpsimd
+        def ratio(c, i, eng, dst):
+            rr[c, i] = dst
             eng.tensor_tensor(
-                out=rr[c, i][:].rearrange("p g t m -> p g m t"),
-                in0=numt[c][:, i, :].rearrange("p (g m t) -> p g m t", g=2, t=4),
-                in1=w[c, i][:].rearrange("p (g m t) -> p g m t", g=2, t=4),
+                out=dst.rearrange("p (g t m) -> p g t m", g=2, t=4),
+                in0=numt[c][:, i, :].rearrange("p (g m t) -> p g t m", g=2, t=4),
+                in1=w[c, i][:].rearrange("p (g t m) -> p g t m", g=2, t=4),
                 op=ALU.mult,
             )
 
-        def m1(c, G, tp):
+        def m1(c, G, u):
             codes, scales = qc[c]
-            wc, ws = wq_c[G, tp]
-            bank = ps.tile([P, 2, CH], F32, name="bank_m", tag="bank_m", bufs=4)
-            for tt in range(2):
+            wc, ws = wq_c[G, u]
+            bank = sum_bank([P, 2, CH])
+            for e in range(2):
                 for g in range(2):
                     nc.tensor.matmul_mx(
-                        out=bank[:, tt, :],
-                        lhsT=wc[:, tt, g, :].bitcast(FP8X4),
-                        lhsT_scale=ws[:, tt, g, :],
+                        out=bank[:, e, :],
+                        lhsT=wc[:, e, g, :].bitcast(FP8X4),
+                        lhsT_scale=ws[:, e, g, :],
                         rhs=codes[:, g, :].bitcast(FP8X4),
                         rhs_scale=scales[:, g, :],
                         start=(g == 0),
                         stop=(g == 1),
                     )
-            banks["m1", c, G, tp] = bank
+            banks["m1", c, G, u] = bank
 
-        def sig(c, G, tp):
-            if tp == 0:
-                s[c, G] = sb.tile([P, 4, CH], F32, name="s", tag="s", bufs=3)
-            nc.scalar.activation(out=s[c, G][:, 2 * tp : 2 * tp + 2, :], in_=banks["m1", c, G, tp][:], func=ACT.Sigmoid)
+        def sig(c, G, u):
+            if u == 0:
+                s[c, G] = sb.tile([P, 2, CH, 2], F32, name="s", tag="s", bufs=4)
+            nc.scalar.activation(out=s[c, G][:, u, :, :], in_=banks["m1", c, G, u][:].rearrange("p e n -> p n e"), func=ACT.Sigmoid)
 
         def r_transpose(c, G, i):
-            bank = ps.tile([P, 4, P], F32, name="bank_t", tag="bank_t", bufs=4)
+            bank = turn_bank([P, 4, P])
             for t in range(4):
-                nc.tensor.transpose(bank[:, t, :], rr[c, i][:, G, t, :], ident[:])
+                s0 = 512 * G + P * t
+                nc.tensor.transpose(bank[:, t, :], rr[c, i][:, s0 : s0 + P], ident[:])
             banks["r", c, G, i] = bank
 
         def fin(c, G, i):
-            if i == 0:
-                y[c, G] = sb.tile([P, CH, 4], BF16, name="y", tag="y", bufs=3, align_bytes=64)
+            if (G, i) == (0, 0):
+                y[c] = shared(c)
+            s0 = 1024 * i + 512 * G
             nc.vector.tensor_tensor(
-                out=y[c, G][:, i * P : (i + 1) * P, :],
-                in0=banks["r", c, G, i][:].rearrange("p t n -> p n t"),
-                in1=s[c, G][:, :, i * P : (i + 1) * P].rearrange("p t n -> p n t"),
+                out=y[c][:, s0 : s0 + 512].rearrange("p (n u e) -> p n u e", u=2, e=2),
+                in0=banks["r", c, G, i][:].rearrange("p (u e) n -> p n u e", u=2),
+                in1=s[c, G][:, :, i * P : (i + 1) * P, :].rearrange("p u n e -> p n u e"),
                 op=ALU.mult,
             )
 
-        def y_quant(c, G):
-            codes = sb.tile([P, CH], U32, name="ycod", tag="ycod", bufs=4, align_bytes=64)
-            scales = sb.tile([P, CH], U8, name="yscl", tag="yscl", bufs=4, align_bytes=64)
-            nc.vector.quantize_mx(out=codes[:].bitcast(FP8X4), scales=scales[:], in_=y[c, G][:].rearrange("p n t -> p (n t)"))
-            yc[c, G] = (codes, scales)
+        def y_quant(c, i0, i1):
+            if i0 == 0:
+                codes = sb.tile([P, 512], U32, name="ycod", tag="ycod", bufs=3, align_bytes=64)
+                scales = sb.tile([P, 512], U8, name="yscl", tag="yscl", bufs=3, align_bytes=64)
+                yc[c] = (codes, scales)
+            codes, scales = yc[c]
+            nc.vector.quantize_mx(
+                out=codes[:, 256 * i0 : 256 * i1].bitcast(FP8X4),
+                scales=scales[:, 256 * i0 : 256 * i1],
+                in_=y[c][:, 1024 * i0 : 1024 * i1],
+            )
 
         def m2(c, i, oh):
-            bank = ps.tile([P, 512], F32, name="bank_m", tag="bank_m", bufs=4)
+            bank = sum_bank([P, 512])
+            codes, scales = yc[c]
             for G in range(2):
-                codes, scales = yc[c, G]
+                s0 = 256 * i + P * G
                 nc.tensor.matmul_mx(
                     out=bank[:],
-                    lhsT=codes[:, i * P : (i + 1) * P].bitcast(FP8X4),
-                    lhsT_scale=scales[:, i * P : (i + 1) * P],
-                    rhs=wo_c[oh][0][:, G, :].bitcast(FP8X4),
-                    rhs_scale=wo_c[oh][1][:, G, :],
+                    lhsT=codes[:, s0 : s0 + P].bitcast(FP8X4),
+                    lhsT_scale=scales[:, s0 : s0 + P],
+                    rhs=wo_c[oh, G][0][:].bitcast(FP8X4),
+                    rhs_scale=wo_c[oh, G][1][:],
                     start=(G == 0),
                     stop=(G == 1),
                 )
             banks["m2", c, i, oh] = bank
 
-        def copy_out(c, i, oh, on_vector=False):
+        def copy_out(c, i, oh, eng):
             if oh == 0:
                 o[c, i] = sb.tile([P, DO], F32, name="o", tag="o", bufs=4)
-            copy = nc.vector.tensor_copy if on_vector else nc.scalar.copy
-            copy(out=o[c, i][:, 512 * oh : 512 * (oh + 1)], in_=banks["m2", c, i, oh][:])
+            eng(out=o[c, i][:, 512 * oh : 512 * (oh + 1)], in_=banks["m2", c, i, oh][:])
 
         def store(c, i):
             nc.sync.dma_start(out=out_v[c][:, i, :], in_=o[c, i][:])
 
+        def store_half(c, i, oh):
+            nc.sync.dma_start(out=out_v[c][:, i, 512 * oh : 512 * (oh + 1)], in_=o[c, i][:, 512 * oh : 512 * (oh + 1)])
+
+        on_v, on_s = nc.vector.tensor_copy, nc.scalar.copy
+
         with tc.manual_schedule():
 
-            load_den(0, 0)
-            load_wq(0, 0)
-            load_q(0)
-            load_sc()
-            load_wq(0, 1)
-            load_den(0, 1)
-            load_wq(0, 2)
-            load_den(1, 0)
-            load_wq(0, 3)
-            rsqrt(0, 0)
-            load_den(1, 1)
-            load_wq(1, 0)
-            rsqrt(0, 1)
-            load_den(2, 0)
-            load_wq(1, 1)
-            rsqrt(1, 0)
-            load_den(2, 1)
-            load_wq(1, 2)
-            rsqrt(1, 1)
-            load_den(3, 0)
-            load_wq(1, 3)
-            load_q(1)
-            rsqrt(2, 0)
-            load_den(3, 1)
-            load_num(0)
-            rsqrt(2, 1)
-            load_den(4, 0)
-            load_wo(0)
-            load_wo(1)
-            rsqrt(3, 0)
-            load_den(4, 1)
-            load_wo(2)
-            rsqrt(3, 1)
-            load_den(5, 0)
-            load_wo(3)
-            rsqrt(4, 0)
-            load_den(5, 1)
-            load_num(1)
-            rsqrt(4, 1)
-            load_den(6, 0)
-            load_wo(4)
-            rsqrt(5, 0)
-            load_den(6, 1)
-            load_wo(5)
-            rsqrt(5, 1)
-            load_den(7, 0)
-            load_wo(6)
-            rsqrt(6, 0)
-            load_den(7, 1)
-            load_wo(7)
-            rsqrt(6, 1)
-            load_q(2)
-            load_num(2)
-            rsqrt(7, 0)
-            rsqrt(7, 1)
-            load_q(3)
-            load_num(3)
-            load_q(4)
-            load_q(5)
+            def stage1(c):
+                for G in range(2):
+                    for u in range(2):
+                        m1(c, G, u)
+                        sig(c, G, u)
 
-            for c in range(4):
+            def den_step(n):
+                if n < 2 * NC:
+                    load_den(*divmod(n, 2))
+                if n >= 2:
+                    rsqrt(*divmod(n - 2, 2))
+
+            def r_transposes(c):
                 for i in range(2):
-                    square(c, i, on_gpsimd=True)
+                    for G in range(2):
+                        r_transpose(c, G, i)
 
-            wq_transpose(0, 0)
-            wq_copy(0, 0)
-            cast(0)
-            wq_transpose(0, 1)
-            wq_copy(0, 1)
+            def ratio_v(c, i):
+                ratio(c, i, nc.vector, w[c, i][:])
+
+            load_q(0)
+            den_step(0)
+            load_q(1)
+            load_sc()
+            den_step(1)
+            cast(0, on_v)
+            cast(1, on_v)
             q_transpose(0, 0)
             q_transpose(0, 1)
-            wq_transpose(0, 2)
             q_scale_up(0, 0)
-            wq_quant(0, 0)
             q_scale_up(0, 1)
-            wq_copy(0, 2)
-            wq_transpose(0, 3)
-            q_quant(0)
-            wq_copy(0, 3)
-            for t in range(4):
-                wq_transpose(1, t)
-                if t == 2:
-                    cast(1)
-                    wq_quant(0, 1)
-                wq_copy(1, t)
-            for g in range(2):
-                q_transpose(1, g)
-            wq_quant(1, 0)
-            q_scale_up(1, 0)
-            wq_quant(1, 1)
-            q_scale_up(1, 1)
-            ratio(0, 0, on_vector=True)
-            q_quant(1)
-            ratio(0, 1, on_vector=True)
-            cast(2)
-            for j in range(4):
-                wo_transpose(j)
-                wo_copy(j)
-
-            for n in range(NC + 1):
-                if n < NC:
-                    for G in range(2):
-                        for tp in range(2):
-                            m1(n, G, tp)
-                            sig(n, G, tp)
-                if n == NC - 1:
-                    for G in range(2):
-                        for i in range(2):
-                            r_transpose(n, G, i)
-                            fin(n, G, i)
-                        y_quant(n, G)
+            q_transpose(1, 0)
+            q_transpose(1, 1)
+            for n in range(8):
+                G, t = divmod(n, 4)
+                load_wq(G, t)
+                den_step(2 + n)
+                wq_transpose(G, t)
                 if n == 0:
-                    wo_quant(0)
-                if n > 0:
-                    for i in range(2):
+                    q_scale_up(1, 0)
+                    q_quant(0)
+                    q_scale_up(1, 1)
+                wq_copy(G, t, on_v)
+                if n in (2, 4, 6):
+                    wq_quant(*divmod(n // 2 - 1, 2))
+            load_q(2)
+            for n in range(10, 14):
+                load_wo(n - 10)
+                den_step(n)
+            cast(2, on_v)
+            wq_quant(1, 1)
+            for G in range(2):
+                for u in range(2):
+                    m1(0, G, u)
+            load_num(0)
+            for n in range(14, 2 * NC + 2):
+                load_wo(n - 10)
+                den_step(n)
+            square(0, 0)
+            square(0, 1)
+            load_q(3)
+            load_num(1)
+            for c in range(4, NC):
+                load_num(c - 2)
+                load_q(c)
+            for oh in range(2):
+                for g in range(2):
+                    for h in range(2):
+                        wo_transpose(oh, g, h)
+                        wo_copy(oh, g, h, on_v)
+                        if h == 0 and (oh, g) > (0, 0):
+                            wo_quant(*divmod(2 * oh + g - 1, 2))
+            ratio_v(0, 0)
+            wo_quant(1, 1)
+            ratio_v(0, 1)
+            for G in range(2):
+                for u in range(2):
+                    sig(0, G, u)
+            r_transposes(0)
+            square(1, 0)
+            square(1, 1)
+            square(2, 0)
+
+            for n in range(NC):
+                last = n == NC - 1
+                for i in range(2):
+                    if n > 0:
                         for oh in range(2):
                             m2(n - 1, i, oh)
-                            copy_out(n - 1, i, oh, on_vector=(n == NC and oh == 1))
+                            copy_out(n - 1, i, oh, on_s)
                         store(n - 1, i)
-                if 4 <= n + 1 < NC:
-                    for i in range(2):
-                        square(n + 1, i)
-                if n < NC - 1:
-                    r_transpose(n, 0, 0)
-                    r_transpose(n, 0, 1)
-                    r_transpose(n, 1, 0)
-                    r_transpose(n, 1, 1)
-                    fin(n, 0, 0)
-                    fin(n, 0, 1)
-                    fin(n, 1, 0)
-                    y_quant(n, 0)
-                    fin(n, 1, 1)
-                    if n == 0:
-                        for j in range(4, 8):
-                            wo_transpose(j)
-                            wo_copy(j, on_scalar=True)
-                            if j == 4:
-                                y_quant(n, 1)
-                        wo_quant(1)
-                    for i in range(2):
-                        ratio(n + 1, i, on_vector=True)
-                    if n + 2 < NC:
-                        q_transpose(n + 2, 0)
-                        q_transpose(n + 2, 1)
-                        q_scale_up(n + 2, 0)
-                        if n > 0:
-                            y_quant(n, 1)
-                        q_scale_up(n + 2, 1)
-                        if n + 3 < NC:
-                            cast(n + 3, on_scalar=True)
-                        q_quant(n + 2)
-                    else:
-                        y_quant(n, 1)
-                    if n + 4 < NC:
-                        load_num(n + 4)
-                    if n + 6 < NC:
-                        load_q(n + 6)
+                if n + 6 < NC:
+                    load_num(n + 6)
+                for i in range(2):
+                    for G in range(2):
+                        fin(n, G, i)
+                    if last and i == 1:
+                        y_quant(n, 0, 1)
+                if n + 2 < NC:
+                    square(n + 2, 1)
+                    q_transpose(n + 2, 0)
+                    q_transpose(n + 2, 1)
+                if n == 0:
+                    ratio_v(1, 0)
+                    ratio_v(1, 1)
+                if not last:
+                    q_quant(n + 1)
+                if n + 3 < NC:
+                    cast(n + 3, on_v)
+                y_quant(n, 1 if last else 0, 2)
+                if not last:
+                    stage1(n + 1)
+                if n + 2 < NC:
+                    ratio(n + 2, 0, nc.gpsimd, shared(n)[:].bitcast(F32))
+                    ratio(n + 2, 1, nc.gpsimd, w[n + 2, 1][:])
+                    q_scale_up(n + 2, 0)
+                    q_scale_up(n + 2, 1)
+                if n + 3 < NC:
+                    square(n + 3, 0)
+                if not last:
+                    r_transposes(n + 1)
+            for i in range(2):
+                for oh in range(2):
+                    m2(NC - 1, i, oh)
+                    copy_out(NC - 1, i, oh, (on_s, on_v)[oh])
+                    store_half(NC - 1, i, oh)

@@ -29,8 +29,8 @@ def tile_aftfull_pb_kernel(tc, q_bytes, q_scale, num, den, Wq, Wo, out):
         num_v = num.flatten_outer_dims().rearrange("(c p i) d -> c p i d", p=P, i=2)
         den_v = den.flatten_outer_dims().rearrange("(c p i) d -> c p i d", p=P, i=2)
         out_v = out.flatten_outer_dims().rearrange("(c p i) d -> c p i d", p=P, i=2)
-        wq_v = Wq.rearrange("(g m t) k -> g m t k", m=P, t=4)
-        wo_v = Wo.rearrange("(j m) k -> j m k", m=P)
+        wq_v = Wq.rearrange("(g m u e) k -> g u m e k", m=P, u=2, e=2)
+        wo_v = Wo.rearrange("(oh m h j) k -> oh h m j k", m=P, h=2, j=2)
 
         ident = sb.tile([P, P], F32, name="ident")
         make_identity(nc, ident[:])
@@ -50,45 +50,53 @@ def tile_aftfull_pb_kernel(tc, q_bytes, q_scale, num, den, Wq, Wo, out):
             nc.sync.dma_start(out=sc[:], in_=q_scale.rearrange("a b (g p t) -> p (a b g) t", p=P, t=4))
 
         def load_w(key, src):
-            raw[key] = sb.tile([P, DM], BF16, name="wraw", tag="wraw", bufs=8)
-            nc.sync.dma_start(out=raw[key][:], in_=src)
+            raw[key] = sb.tile([P, 2 * DM], BF16, name="wraw", tag="wraw", bufs=4)
+            nc.sync.dma_start(out=raw[key][:], in_=src.rearrange("m j k -> m (j k)"))
 
-        def load_wq(G, t):
-            load_w(("q", G, t), wq_v[G][:, t, :])
+        def load_wq(G, u):
+            load_w(("q", G, u), wq_v[G][u])
 
-        def load_wo(j):
-            load_w(("o", j), wo_v[j])
+        def load_wo(oh, h):
+            load_w(("o", oh, h), wo_v[oh][h])
 
         def load_q(c):
-            qb[c] = sb.tile([P, 2 * DM], U8, name="qb", tag="qb", bufs=NC)
+            qb[c] = sb.tile([P, 2 * DM], U8, name="qb", tag="qb", bufs=3)
             nc.sync.dma_start(out=qb[c][:], in_=q_v[c].rearrange("p i d -> p (i d)"))
 
-        def load_den(c, i):
-            dent[c, i] = sb.tile([P, DH], BF16, name="dent", tag="dent", bufs=4)
-            nc.sync.dma_start(out=dent[c, i][:], in_=den_v[c][:, i, :])
+        def load_den_half(c, i):
+            half = sb.tile([P, DH], BF16, name="den_half", tag="den_half", bufs=2)
+            nc.sync.dma_start(out=half[:], in_=den_v[c][:, i, :])
+            dent[c, i] = half[:]
+
+        def load_den(c):
+            both = sb.tile([P, 2 * DH], BF16, name="den_both", tag="den_both", bufs=3)
+            nc.sync.dma_start(out=both[:], in_=den_v[c].rearrange("p i d -> p (i d)"))
+            for i in range(2):
+                dent[c, i] = both[:, DH * i : DH * (i + 1)]
 
         def load_num(c):
-            numt[c] = sb.tile([P, 2, DH], BF16, name="numt", tag="numt", bufs=6)
-            nc.sync.dma_start(out=numt[c][:], in_=num_v[c])
+            numt[c] = sb.tile([P, 2 * DH], BF16, name="numt", tag="numt", bufs=3)
+            nc.sync.dma_start(out=numt[c][:], in_=num_v[c].rearrange("p i d -> p (i d)"))
 
         def grouped():
-            return sb.tile([P, 2048], BF16, name="grouped", tag="grouped", bufs=3, align_bytes=64)
+            return sb.tile([P, 2048], BF16, name="grouped", tag="grouped", bufs=4, align_bytes=64)
 
         def shared(c):
             return sb.tile([P, 2048], BF16, name="shared", tag=f"shared{c % 2}", bufs=1, align_bytes=64)
 
         def wq_transpose(G, t):
-            words = raw["q", G, t][:].bitcast(F32)
+            words = raw["q", G, t // 2][:].bitcast(F32)
             bank = turn_bank([P, 2, 2, P])
             for g in range(2):
+                s0 = 512 * (t % 2) + 256 * g
                 for u in range(2):
-                    nc.tensor.transpose(bank[:, g, u, :], words[:, 256 * g + u : 256 * (g + 1) : 2], ident[:])
+                    nc.tensor.transpose(bank[:, g, u, :], words[:, s0 + u : s0 + 256 : 2], ident[:])
             banks["wq", G, t] = bank
 
         def wq_copy(G, t, eng):
             u, e = divmod(t, 2)
             if e == 0:
-                wts["q", G, u] = grouped()
+                wts["q", G, u] = shared(1 - G) if G == u else grouped()
             dst = wts["q", G, u][:, 1024 * e : 1024 * (e + 1)].bitcast(F32)
             eng(out=dst.rearrange("p (g m u) -> p g m u", g=2, u=2), in_=banks["wq", G, t][:].rearrange("p g u m -> p g m u"))
 
@@ -104,17 +112,18 @@ def tile_aftfull_pb_kernel(tc, q_bytes, q_scale, num, den, Wq, Wo, out):
 
         def wo_transpose(oh, g, h):
             bank = turn_bank([P, 2, 2, P])
+            words = raw["o", oh, h][:].bitcast(F32)
             for j in range(2):
-                words = raw["o", 4 * oh + 2 * h + j][:].bitcast(F32)
+                s0 = 512 * j + 256 * g
                 for u in range(2):
-                    nc.tensor.transpose(bank[:, u, j, :], words[:, 256 * g + u : 256 * (g + 1) : 2], ident[:])
+                    nc.tensor.transpose(bank[:, j, u, :], words[:, s0 + u : s0 + 256 : 2], ident[:])
             banks["wo", oh, g, h] = bank
 
         def wo_copy(oh, g, h, eng):
             if h == 0:
                 wts["o", oh, g] = grouped()
-            dst = wts["o", oh, g][:, 1024 * h : 1024 * (h + 1)].bitcast(F32)
-            eng(out=dst.rearrange("p (n u) -> p n u", u=2), in_=banks["wo", oh, g, h][:].rearrange("p u j m -> p (j m) u"))
+            dst = wts["o", oh, g][:].bitcast(F32).rearrange("p (m h x) -> p m h x", h=2, x=4)
+            eng(out=dst[:, :, h, :], in_=banks["wo", oh, g, h][:].rearrange("p j u m -> p m (j u)"))
 
         def wo_quant(oh, g):
             codes = sb.tile([P, 512], U32, name=f"woc{oh}{g}", align_bytes=64)
@@ -122,9 +131,10 @@ def tile_aftfull_pb_kernel(tc, q_bytes, q_scale, num, den, Wq, Wo, out):
             nc.vector.quantize_mx(out=codes[:].bitcast(FP8X4), scales=scales[:], in_=wts["o", oh, g][:])
             wo_c[oh, g] = (codes, scales)
 
-        def cast(c, eng):
-            qx[c] = sb.tile([P, 2 * DM], BF16, name="qx", tag="qx", bufs=2)
-            eng(out=qx[c][:], in_=qb[c][:].bitcast(FP8))
+        def cast(c, eng, lo=0, hi=2 * DM):
+            if c not in qx:
+                qx[c] = sb.tile([P, 2 * DM], BF16, name="qx", tag="qx", bufs=2)
+            eng(out=qx[c][:, lo:hi], in_=qb[c][:, lo:hi].bitcast(FP8))
 
         def q_transpose(c, g):
             words = qx[c][:].bitcast(F32)
@@ -137,7 +147,7 @@ def tile_aftfull_pb_kernel(tc, q_bytes, q_scale, num, den, Wq, Wo, out):
 
         def q_scale_up(c, g):
             if g == 0:
-                qt[c] = sb.tile([P, 2048], BF16, name="qt", tag="qt", bufs=2, align_bytes=64)
+                qt[c] = sb.tile([P, 2048], BF16, name="qt", tag="qt", bufs=3, align_bytes=64)
             nc.vector.tensor_tensor(
                 out=qt[c][:, 1024 * g : 1024 * (g + 1)].rearrange("p (n u e) -> p n u e", u=2, e=2),
                 in0=banks["x", c, g][:].rearrange("p u i n -> p (u i n)").bitcast(BF16).rearrange("p (u n e) -> p n u e", u=2, e=2),
@@ -156,22 +166,26 @@ def tile_aftfull_pb_kernel(tc, q_bytes, q_scale, num, den, Wq, Wo, out):
             qc[c] = (codes, scales)
 
         def rsqrt(c, i):
-            w[c, i] = sb.tile([P, DH], F32, name="w", tag="w", bufs=2 * NC)
+            w[c, i] = sb.tile([P, DH], F32, name="w", tag="w", bufs=2 * NC)[:]
             nc.scalar.activation(
-                out=w[c, i][:].rearrange("p (g t m) -> p g t m", g=2, t=4),
-                in_=dent[c, i][:].rearrange("p (g m t) -> p g t m", g=2, t=4),
+                out=w[c, i].rearrange("p (g t m) -> p g t m", g=2, t=4),
+                in_=dent[c, i].rearrange("p (g m t) -> p g t m", g=2, t=4),
                 func=ACT.Abs_reciprocal_sqrt,
             )
 
         def square(c, i):
-            nc.scalar.activation(out=w[c, i][:], in_=w[c, i][:], func=ACT.Square)
+            nc.scalar.activation(out=w[c, i], in_=w[c, i], func=ACT.Square)
+
+        def square_g(c, i, dst):
+            nc.gpsimd.tensor_tensor(out=dst, in0=w[c, i], in1=w[c, i], op=ALU.mult)
+            w[c, i] = dst
 
         def ratio(c, i, eng, dst):
             rr[c, i] = dst
             eng.tensor_tensor(
-                out=dst.rearrange("p (g t m) -> p g t m", g=2, t=4),
-                in0=numt[c][:, i, :].rearrange("p (g m t) -> p g t m", g=2, t=4),
-                in1=w[c, i][:].rearrange("p (g t m) -> p g t m", g=2, t=4),
+                out=dst.rearrange("p (g t m) -> p g t m", t=4, m=P),
+                in0=numt[c][:, DH * i : DH * (i + 1)].rearrange("p (g m t) -> p g t m", t=4, m=P),
+                in1=w[c, i].rearrange("p (g t m) -> p g t m", t=4, m=P),
                 op=ALU.mult,
             )
 
@@ -194,7 +208,7 @@ def tile_aftfull_pb_kernel(tc, q_bytes, q_scale, num, den, Wq, Wo, out):
 
         def sig(c, G, u):
             if u == 0:
-                s[c, G] = sb.tile([P, 2, CH, 2], F32, name="s", tag="s", bufs=4)
+                s[c, G] = sb.tile([P, 2, CH, 2], F32, name="s", tag="s", bufs=6)
             nc.scalar.activation(out=s[c, G][:, u, :, :], in_=banks["m1", c, G, u][:].rearrange("p e n -> p n e"), func=ACT.Sigmoid)
 
         def r_transpose(c, G, i):
@@ -258,129 +272,201 @@ def tile_aftfull_pb_kernel(tc, q_bytes, q_scale, num, den, Wq, Wo, out):
 
         with tc.manual_schedule():
 
+            def stage1_matmuls(c):
+                for G in range(2):
+                    for u in range(2):
+                        m1(c, G, u)
+
+            def sigmoids(c):
+                for G in range(2):
+                    for u in range(2):
+                        sig(c, G, u)
+
             def stage1(c):
                 for G in range(2):
                     for u in range(2):
                         m1(c, G, u)
                         sig(c, G, u)
 
-            def den_step(n):
-                if n < 2 * NC:
-                    load_den(*divmod(n, 2))
-                if n >= 2:
-                    rsqrt(*divmod(n - 2, 2))
+            def rsqrts(c):
+                rsqrt(c, 0)
+                rsqrt(c, 1)
 
             def r_transposes(c):
                 for i in range(2):
                     for G in range(2):
                         r_transpose(c, G, i)
 
-            def ratio_v(c, i):
-                ratio(c, i, nc.vector, w[c, i][:])
+            def q_transposes(c):
+                q_transpose(c, 0)
+                q_transpose(c, 1)
 
+            def q_scales(c):
+                q_scale_up(c, 0)
+                q_scale_up(c, 1)
+
+            def wq_turn(G, u):
+                for e in range(2):
+                    wq_transpose(G, 2 * u + e)
+                    wq_copy(G, 2 * u + e, on_v)
+
+            def wo_turn(oh, g, eng):
+                for h in range(2):
+                    wo_transpose(oh, g, h)
+                    wo_copy(oh, g, h, eng)
+
+            def ratios_g(c, first_dst):
+                ratio(c, 0, nc.gpsimd, first_dst)
+                ratio(c, 1, nc.gpsimd, w[c, 1])
+
+            load_den_half(0, 0)
             load_q(0)
-            den_step(0)
-            load_q(1)
+            load_den_half(0, 1)
+            load_den(1)
             load_sc()
-            den_step(1)
+            load_wq(0, 0)
+            load_den(2)
+            load_q(1)
+            rsqrts(0)
             cast(0, on_v)
-            cast(1, on_v)
-            q_transpose(0, 0)
-            q_transpose(0, 1)
-            q_scale_up(0, 0)
-            q_scale_up(0, 1)
-            q_transpose(1, 0)
-            q_transpose(1, 1)
-            for n in range(8):
-                G, t = divmod(n, 4)
-                load_wq(G, t)
-                den_step(2 + n)
-                wq_transpose(G, t)
-                if n == 0:
-                    q_scale_up(1, 0)
-                    q_quant(0)
-                    q_scale_up(1, 1)
-                wq_copy(G, t, on_v)
-                if n in (2, 4, 6):
-                    wq_quant(*divmod(n // 2 - 1, 2))
+            square_g(0, 0, w[0, 0])
+            square_g(0, 1, w[0, 1])
+            q_transposes(0)
+            q_scales(0)
+            rsqrts(1)
+            load_den(3)
+            for n in range(1, 4):
+                load_wq(*divmod(n, 2))
+                rsqrts(1 + n)
+                load_den(3 + n)
             load_q(2)
-            for n in range(10, 14):
-                load_wo(n - 10)
-                den_step(n)
-            cast(2, on_v)
-            wq_quant(1, 1)
-            for G in range(2):
-                for u in range(2):
-                    m1(0, G, u)
+            rsqrts(5)
+            load_den(7)
+            rsqrts(6)
+            rsqrts(7)
             load_num(0)
-            for n in range(14, 2 * NC + 2):
-                load_wo(n - 10)
-                den_step(n)
-            square(0, 0)
-            square(0, 1)
+            load_wo(0, 0)
+            load_wo(0, 1)
             load_q(3)
+            load_wo(1, 0)
+            load_wo(1, 1)
             load_num(1)
-            for c in range(4, NC):
-                load_num(c - 2)
-                load_q(c)
-            for oh in range(2):
-                for g in range(2):
-                    for h in range(2):
-                        wo_transpose(oh, g, h)
-                        wo_copy(oh, g, h, on_v)
-                        if h == 0 and (oh, g) > (0, 0):
-                            wo_quant(*divmod(2 * oh + g - 1, 2))
-            ratio_v(0, 0)
-            wo_quant(1, 1)
-            ratio_v(0, 1)
-            for G in range(2):
-                for u in range(2):
-                    sig(0, G, u)
-            r_transposes(0)
-            square(1, 0)
-            square(1, 1)
-            square(2, 0)
+            wq_turn(0, 0)
+            cast(1, on_v)
+            q_quant(0)
+            wq_quant(0, 0)
+            square_g(1, 0, shared(1)[:].bitcast(F32))
+            square_g(1, 1, w[1, 1])
+            wq_turn(0, 1)
+            q_transposes(1)
+            q_scales(1)
+            wq_turn(1, 0)
+            wq_turn(1, 1)
+            cast(2, on_v)
+            q_quant(1)
+            wq_quant(0, 1)
+            wq_quant(1, 0)
+            wq_quant(1, 1)
+            ratios_g(0, shared(0)[:].bitcast(F32))
 
-            for n in range(NC):
-                last = n == NC - 1
-                for i in range(2):
-                    if n > 0:
-                        for oh in range(2):
-                            m2(n - 1, i, oh)
-                            copy_out(n - 1, i, oh, on_s)
-                        store(n - 1, i)
-                if n + 6 < NC:
-                    load_num(n + 6)
-                for i in range(2):
-                    for G in range(2):
-                        fin(n, G, i)
-                    if last and i == 1:
-                        y_quant(n, 0, 1)
-                if n + 2 < NC:
-                    square(n + 2, 1)
-                    q_transpose(n + 2, 0)
-                    q_transpose(n + 2, 1)
-                if n == 0:
-                    ratio_v(1, 0)
-                    ratio_v(1, 1)
-                if not last:
-                    q_quant(n + 1)
+            def stage1_half(c, G):
+                for u in range(2):
+                    m1(c, G, u)
+                    sig(c, G, u)
+
+            def stage2(c, i, oh, eng):
+                m2(c, i, oh)
+                copy_out(c, i, oh, eng)
+
+            q_transposes(2)
+            stage1(0)
+            for c in range(2, 4):
+                load_q(c + 2)
+                load_num(c)
+            q_scales(2)
+            wo_turn(0, 0, on_v)
+            stage1_half(1, 0)
+            wo_turn(0, 1, on_s)
+            stage1_half(1, 1)
+            q_quant(2)
+            cast(3, on_v)
+            wo_quant(0, 0)
+            wo_quant(0, 1)
+            ratios_g(1, wts["o", 0, 1][:].bitcast(F32))
+            r_transposes(0)
+            square(2, 0)
+            halves = [(i, k) for i in range(2) for k in range(2)]
+            for i, G in halves:
+                fin(0, G, i)
+            stage1_half(2, 0)
+            q_transposes(3)
+            square(2, 1)
+            stage1_half(2, 1)
+            q_scales(3)
+            wo_turn(1, 0, on_s)
+            wo_turn(1, 1, on_s)
+            y_quant(0, 0, 2)
+            cast(4, on_v)
+            q_quant(3)
+            stage2(0, 0, 0, on_s)
+            stage2(0, 1, 0, on_s)
+            r_transposes(1)
+            wo_quant(1, 0)
+            wo_quant(1, 1)
+            ratios_g(2, wts["o", 1, 1][:].bitcast(F32))
+            square(3, 0)
+            square(3, 1)
+            load_q(6)
+            load_num(4)
+
+            for n in range(1, NC - 1):
+                for k, (i, G) in enumerate(halves):
+                    fin(n, G, i)
+                    if n > 1 or k % 2 == 1:
+                        stage2(n - 1, *halves[k], on_v if k == 3 and n < NC - 2 else on_s)
+                    if k % 2 == 1:
+                        store(n - 1, k // 2)
                 if n + 3 < NC:
-                    cast(n + 3, on_v)
-                y_quant(n, 1 if last else 0, 2)
-                if not last:
-                    stage1(n + 1)
-                if n + 2 < NC:
-                    ratio(n + 2, 0, nc.gpsimd, shared(n)[:].bitcast(F32))
-                    ratio(n + 2, 1, nc.gpsimd, w[n + 2, 1][:])
-                    q_scale_up(n + 2, 0)
-                    q_scale_up(n + 2, 1)
-                if n + 3 < NC:
+                    q_transposes(n + 3)
+                if 1 < n + 0 < NC - 3:
                     square(n + 3, 0)
-                if not last:
+                if n + 2 < NC:
+                    stage1(n + 2)
+                if n + 3 < NC:
+                    q_scales(n + 3)
+                if n + 4 < NC:
+                    cast(n + 4, on_s, 0, 1024)
+                if n == 1:
+                    square(4, 0)
+                if n + 3 < NC:
+                    square(n + 3, 1)
+                if n + 2 < NC:
                     r_transposes(n + 1)
+                if n + 4 < NC:
+                    cast(n + 4, on_v, 1024, 2 * DM)
+                if n + 3 < NC:
+                    y_quant(n, 0, 2)
+                    q_quant(n + 3)
+                    ratios_g(n + 2, qt[n + 3][:].bitcast(F32))
+                elif n + 2 < NC:
+                    y_quant(n, 0, 2)
+                    ratio(NC - 1, 0, nc.gpsimd, y[n][:].bitcast(F32))
+                if n + 6 < NC:
+                    load_q(n + 6)
+                if n + 4 < NC:
+                    load_num(n + 4)
+            a, b = NC - 2, NC - 1
+            y_quant(a, 0, 2)
+            ratio(b, 1, nc.vector, w[b, 1])
+            for i in range(2):
+                for G in range(2):
+                    r_transpose(b, G, i)
+                    fin(b, G, i)
+                for oh in range(2):
+                    stage2(a, i, oh, on_s)
+                store(a, i)
+                y_quant(b, i, i + 1)
             for i in range(2):
                 for oh in range(2):
-                    m2(NC - 1, i, oh)
-                    copy_out(NC - 1, i, oh, (on_s, on_v)[oh])
-                    store_half(NC - 1, i, oh)
+                    stage2(b, i, oh, (on_s, on_v)[oh])
+                    store_half(b, i, oh)

@@ -36,15 +36,28 @@ def tile_aftfull_pb_kernel(tc, q_bytes, q_scale, num, den, Wq, Wo, out):
         make_identity(nc, ident[:])
         sc = sb.tile([P, 2, 4], F32, name="sc")
 
+        one = sb.tile([P, 1], F32, name="one")
+        nc.vector.memset(one[:], 1.0)
+        sorted_words = {}
         raw, banks, wts, wq_c, wo_c = {}, {}, {}, {}, {}
         qb, qx, qt, qc = {}, {}, {}, {}
         dent, numt, w, rr, s, y, yc, o = {}, {}, {}, {}, {}, {}, {}, {}
 
-        def turn_bank(shape):
-            return ps.tile(shape, F32, name="bank_t", tag="bank_t", bufs=4)
+        rings = {"turn": [0, 1, 2, 3], "sum": [4, 5, 6, 7]}
 
-        def sum_bank(shape):
-            return ps.tile(shape, F32, name="bank_m", tag="bank_m", bufs=4)
+        def next_bank(ring):
+            k = rings[ring][0]
+            rings[ring] = rings[ring][1:] + [k]
+            return k
+
+        def bank_tile(shape, k):
+            return ps.tile(shape, F32, name="bank", tag=f"bank{k}", bufs=1)
+
+        def turn_bank(shape, k=None):
+            return bank_tile(shape, next_bank("turn") if k is None else k)
+
+        def sum_bank(shape, k=None):
+            return bank_tile(shape, next_bank("sum") if k is None else k)
 
         def load_sc():
             nc.sync.dma_start(out=sc[:], in_=q_scale.rearrange("a b (g p t) -> p (a b g) t", p=P, t=4))
@@ -78,11 +91,8 @@ def tile_aftfull_pb_kernel(tc, q_bytes, q_scale, num, den, Wq, Wo, out):
             numt[c] = sb.tile([P, 2 * DH], BF16, name="numt", tag="numt", bufs=3)
             nc.sync.dma_start(out=numt[c][:], in_=num_v[c].rearrange("p i d -> p (i d)"))
 
-        def grouped():
-            return sb.tile([P, 2048], BF16, name="grouped", tag="grouped", bufs=4, align_bytes=64)
-
-        def shared(c):
-            return sb.tile([P, 2048], BF16, name="shared", tag=f"shared{c % 2}", bufs=1, align_bytes=64)
+        def grouped(slot):
+            return sb.tile([P, 2048], BF16, name="grouped", tag=slot, bufs=1, align_bytes=64)
 
         def wq_transpose(G, t):
             words = raw["q", G, t // 2][:].bitcast(F32)
@@ -96,7 +106,7 @@ def tile_aftfull_pb_kernel(tc, q_bytes, q_scale, num, den, Wq, Wo, out):
         def wq_copy(G, t, eng):
             u, e = divmod(t, 2)
             if e == 0:
-                wts["q", G, u] = shared(1 - G) if G == u else grouped()
+                wts["q", G, u] = grouped(f"stage{2 * G + u}")
             dst = wts["q", G, u][:, 1024 * e : 1024 * (e + 1)].bitcast(F32)
             eng(out=dst.rearrange("p (g m u) -> p g m u", g=2, u=2), in_=banks["wq", G, t][:].rearrange("p g u m -> p g m u"))
 
@@ -110,8 +120,8 @@ def tile_aftfull_pb_kernel(tc, q_bytes, q_scale, num, den, Wq, Wo, out):
             )
             wq_c[G, u] = (codes, scales)
 
-        def wo_transpose(oh, g, h):
-            bank = turn_bank([P, 2, 2, P])
+        def wo_transpose(oh, g, h, k=None):
+            bank = turn_bank([P, 2, 2, P], k)
             words = raw["o", oh, h][:].bitcast(F32)
             for j in range(2):
                 s0 = 512 * j + 256 * g
@@ -121,7 +131,7 @@ def tile_aftfull_pb_kernel(tc, q_bytes, q_scale, num, den, Wq, Wo, out):
 
         def wo_copy(oh, g, h, eng):
             if h == 0:
-                wts["o", oh, g] = grouped()
+                wts["o", oh, g] = grouped(("stage1", "stage2", "y1", "stage3")[2 * oh + g])
             dst = wts["o", oh, g][:].bitcast(F32).rearrange("p (m h x) -> p m h x", h=2, x=4)
             eng(out=dst[:, :, h, :], in_=banks["wo", oh, g, h][:].rearrange("p j u m -> p m (j u)"))
 
@@ -131,18 +141,41 @@ def tile_aftfull_pb_kernel(tc, q_bytes, q_scale, num, den, Wq, Wo, out):
             nc.vector.quantize_mx(out=codes[:].bitcast(FP8X4), scales=scales[:], in_=wts["o", oh, g][:])
             wo_c[oh, g] = (codes, scales)
 
-        def cast(c, eng, lo=0, hi=2 * DM):
+        def widened(c):
             if c not in qx:
                 qx[c] = sb.tile([P, 2 * DM], BF16, name="qx", tag="qx", bufs=2)
-            eng(out=qx[c][:, lo:hi], in_=qb[c][:, lo:hi].bitcast(FP8))
+            return qx[c]
 
-        def q_transpose(c, g):
+        def cast_s(c, i):
+            cols = slice(DM * i, DM * (i + 1))
+            nc.scalar.copy(out=widened(c)[:, cols], in_=qb[c][:, cols].bitcast(FP8))
+            sorted_words[c, i] = False
+
+        def cast_v(c, i0, i1):
+            cols = slice(DM * i0, DM * i1)
+            nc.vector.tensor_scalar(
+                out=widened(c)[:, cols].rearrange("p (u x e) -> p x u e", u=2, e=2),
+                in0=qb[c][:, cols].bitcast(FP8),
+                scalar1=one[:],
+                scalar2=None,
+                op0=ALU.mult,
+            )
+            for i in range(i0, i1):
+                sorted_words[c, i] = (512 * i0 + 256 * (i - i0), 256 * (i1 - i0))
+
+        def q_transpose(c, g, k=None):
             words = qx[c][:].bitcast(F32)
-            bank = turn_bank([P, 2, 2, P])
+            bank = turn_bank([P, 2, 2, P], k)
             for i in range(2):
-                s0 = 512 * i + 256 * g
                 for u in range(2):
-                    nc.tensor.transpose(bank[:, u, i, :], words[:, s0 + u : s0 + 256 : 2], ident[:])
+                    if sorted_words[c, i]:
+                        first, plane = sorted_words[c, i]
+                        s0 = first + plane * u + P * g
+                        src = words[:, s0 : s0 + P]
+                    else:
+                        s0 = 512 * i + 256 * g
+                        src = words[:, s0 + u : s0 + 256 : 2]
+                    nc.tensor.transpose(bank[:, u, i, :], src, ident[:])
             banks["x", c, g] = bank
 
         def q_scale_up(c, g):
@@ -189,10 +222,10 @@ def tile_aftfull_pb_kernel(tc, q_bytes, q_scale, num, den, Wq, Wo, out):
                 op=ALU.mult,
             )
 
-        def m1(c, G, u):
+        def m1(c, G, u, k=None):
             codes, scales = qc[c]
             wc, ws = wq_c[G, u]
-            bank = sum_bank([P, 2, CH])
+            bank = sum_bank([P, 2, CH], k)
             for e in range(2):
                 for g in range(2):
                     nc.tensor.matmul_mx(
@@ -211,8 +244,8 @@ def tile_aftfull_pb_kernel(tc, q_bytes, q_scale, num, den, Wq, Wo, out):
                 s[c, G] = sb.tile([P, 2, CH, 2], F32, name="s", tag="s", bufs=6)
             nc.scalar.activation(out=s[c, G][:, u, :, :], in_=banks["m1", c, G, u][:].rearrange("p e n -> p n e"), func=ACT.Sigmoid)
 
-        def r_transpose(c, G, i):
-            bank = turn_bank([P, 4, P])
+        def r_transpose(c, G, i, k=None):
+            bank = turn_bank([P, 4, P], k)
             for t in range(4):
                 s0 = 512 * G + P * t
                 nc.tensor.transpose(bank[:, t, :], rr[c, i][:, s0 : s0 + P], ident[:])
@@ -220,7 +253,7 @@ def tile_aftfull_pb_kernel(tc, q_bytes, q_scale, num, den, Wq, Wo, out):
 
         def fin(c, G, i):
             if (G, i) == (0, 0):
-                y[c] = shared(c)
+                y[c] = grouped(f"y{c % 2}")
             s0 = 1024 * i + 512 * G
             nc.vector.tensor_tensor(
                 out=y[c][:, s0 : s0 + 512].rearrange("p (n u e) -> p n u e", u=2, e=2),
@@ -241,8 +274,8 @@ def tile_aftfull_pb_kernel(tc, q_bytes, q_scale, num, den, Wq, Wo, out):
                 in_=y[c][:, 1024 * i0 : 1024 * i1],
             )
 
-        def m2(c, i, oh):
-            bank = sum_bank([P, 512])
+        def m2(c, i, oh, lo=0, hi=512):
+            bank = sum_bank([P, hi - lo])
             codes, scales = yc[c]
             for G in range(2):
                 s0 = 256 * i + P * G
@@ -250,23 +283,26 @@ def tile_aftfull_pb_kernel(tc, q_bytes, q_scale, num, den, Wq, Wo, out):
                     out=bank[:],
                     lhsT=codes[:, s0 : s0 + P].bitcast(FP8X4),
                     lhsT_scale=scales[:, s0 : s0 + P],
-                    rhs=wo_c[oh, G][0][:].bitcast(FP8X4),
-                    rhs_scale=wo_c[oh, G][1][:],
+                    rhs=wo_c[oh, G][0][:, lo:hi].bitcast(FP8X4),
+                    rhs_scale=wo_c[oh, G][1][:, lo:hi],
                     start=(G == 0),
                     stop=(G == 1),
                 )
             banks["m2", c, i, oh] = bank
 
-        def copy_out(c, i, oh, eng):
-            if oh == 0:
+        def copy_out(c, i, oh, eng, lo=0, hi=512):
+            if (c, i) not in o:
                 o[c, i] = sb.tile([P, DO], F32, name="o", tag="o", bufs=4)
-            eng(out=o[c, i][:, 512 * oh : 512 * (oh + 1)], in_=banks["m2", c, i, oh][:])
+            eng(out=o[c, i][:, 512 * oh + lo : 512 * oh + hi], in_=banks["m2", c, i, oh][:])
 
         def store(c, i):
             nc.sync.dma_start(out=out_v[c][:, i, :], in_=o[c, i][:])
 
+        def store_cols(c, i, lo, hi):
+            nc.sync.dma_start(out=out_v[c][:, i, lo:hi], in_=o[c, i][:, lo:hi])
+
         def store_half(c, i, oh):
-            nc.sync.dma_start(out=out_v[c][:, i, 512 * oh : 512 * (oh + 1)], in_=o[c, i][:, 512 * oh : 512 * (oh + 1)])
+            store_cols(c, i, 512 * oh, 512 * (oh + 1))
 
         on_v, on_s = nc.vector.tensor_copy, nc.scalar.copy
 
@@ -315,59 +351,6 @@ def tile_aftfull_pb_kernel(tc, q_bytes, q_scale, num, den, Wq, Wo, out):
                     wo_transpose(oh, g, h)
                     wo_copy(oh, g, h, eng)
 
-            def ratios_g(c, first_dst):
-                ratio(c, 0, nc.gpsimd, first_dst)
-                ratio(c, 1, nc.gpsimd, w[c, 1])
-
-            load_den_half(0, 0)
-            load_q(0)
-            load_den_half(0, 1)
-            load_den(1)
-            load_sc()
-            load_wq(0, 0)
-            load_den(2)
-            load_q(1)
-            rsqrts(0)
-            cast(0, on_v)
-            square_g(0, 0, w[0, 0])
-            square_g(0, 1, w[0, 1])
-            q_transposes(0)
-            q_scales(0)
-            rsqrts(1)
-            load_den(3)
-            for n in range(1, 4):
-                load_wq(*divmod(n, 2))
-                rsqrts(1 + n)
-                load_den(3 + n)
-            load_q(2)
-            rsqrts(5)
-            load_den(7)
-            rsqrts(6)
-            rsqrts(7)
-            load_num(0)
-            load_wo(0, 0)
-            load_wo(0, 1)
-            load_q(3)
-            load_wo(1, 0)
-            load_wo(1, 1)
-            load_num(1)
-            wq_turn(0, 0)
-            cast(1, on_v)
-            q_quant(0)
-            wq_quant(0, 0)
-            square_g(1, 0, shared(1)[:].bitcast(F32))
-            square_g(1, 1, w[1, 1])
-            wq_turn(0, 1)
-            q_transposes(1)
-            q_scales(1)
-            wq_turn(1, 0)
-            wq_turn(1, 1)
-            cast(2, on_v)
-            q_quant(1)
-            wq_quant(0, 1)
-            wq_quant(1, 0)
-            wq_quant(1, 1)
-            ratios_g(0, shared(0)[:].bitcast(F32))
 
             def stage1_half(c, G):
                 for u in range(2):
@@ -378,47 +361,133 @@ def tile_aftfull_pb_kernel(tc, q_bytes, q_scale, num, den, Wq, Wo, out):
                 m2(c, i, oh)
                 copy_out(c, i, oh, eng)
 
-            q_transposes(2)
-            stage1(0)
+            def ratios_g(c, freed):
+                ratio(c, 0, nc.gpsimd, freed[:].bitcast(F32))
+                ratio(c, 1, nc.gpsimd, w[c, 1])
+
+            def stage1_group(c, G, u):
+                m1(c, G, u)
+                sig(c, G, u)
+
+            def words(tile):
+                return tile[:].bitcast(F32)
+
+            def ratio_g(c, i, dst=None):
+                ratio(c, i, nc.gpsimd, w[c, i] if dst is None else dst)
+
+            load_q(0)
+            load_den_half(0, 0)
+            load_q(1)
+            load_den_half(0, 1)
+            load_sc()
+            load_den(1)
+            rsqrts(0)
+            cast_v(0, 0, 2)
+            cast_v(1, 0, 2)
+            square_g(0, 0, w[0, 0])
+            square_g(0, 1, w[0, 1])
+            for c in range(2):
+                q_transposes(c)
+                q_scales(c)
+            for n in range(4):
+                load_wq(*divmod(n, 2))
+                rsqrts(1 + n)
+                load_den(2 + n)
+            load_q(2)
+            rsqrts(5)
+            load_den(6)
+            load_num(0)
+            rsqrts(6)
+            load_den(7)
+            rsqrts(7)
+            load_wo(0, 0)
+            load_wo(0, 1)
+            load_q(3)
+            load_wo(1, 0)
+            load_wo(1, 1)
+            load_num(1)
+            wq_turn(0, 0)
+            q_quant(0)
+            q_quant(1)
+            wq_quant(0, 0)
+            square_g(1, 0, words(wts["q", 0, 0]))
+            wq_turn(0, 1)
+            wq_turn(1, 0)
+            wq_turn(1, 1)
+            wq_quant(0, 1)
+            wq_quant(1, 0)
+            cast_v(2, 0, 2)
+            wq_quant(1, 1)
+            ratios_g(0, wts["q", 1, 1])
             for c in range(2, 4):
                 load_q(c + 2)
                 load_num(c)
+            def wo_unit(oh, g, h, k, eng):
+                wo_transpose(oh, g, h, k)
+                wo_copy(oh, g, h, eng)
+
+            m1(0, 0, 0)
+            m1(0, 0, 1)
+            m1(0, 1, 0)
+            q_transpose(2, 0, 0)
+            q_transpose(2, 1, 1)
+            m1(0, 1, 1)
             q_scales(2)
-            wo_turn(0, 0, on_v)
-            stage1_half(1, 0)
-            wo_turn(0, 1, on_s)
+            m1(1, 0, 0, 2)
+            wo_unit(0, 0, 0, 3, on_v)
+            wo_unit(0, 0, 1, 0, on_v)
+            m1(1, 0, 1, 1)
+            wo_unit(0, 1, 0, 3, on_v)
+            wo_unit(0, 1, 1, 0, on_v)
+            sigmoids(0)
+            sig(1, 0, 0)
+            sig(1, 0, 1)
             stage1_half(1, 1)
             q_quant(2)
-            cast(3, on_v)
+            cast_v(3, 0, 2)
             wo_quant(0, 0)
             wo_quant(0, 1)
-            ratios_g(1, wts["o", 0, 1][:].bitcast(F32))
-            r_transposes(0)
+            r_transpose(0, 0, 0, 3)
+            r_transpose(0, 1, 0, 0)
+            stage1_group(2, 0, 0)
+            square(1, 1)
+            ratios_g(1, wts["o", 0, 1])
+            r_transpose(0, 0, 1, 2)
+            r_transpose(0, 1, 1, 1)
+            for i in range(2):
+                for G in range(2):
+                    fin(0, G, i)
+            stage1_group(2, 0, 1)
+            q_transpose(3, 0, 3)
+            q_transpose(3, 1, 0)
+            stage1_group(2, 1, 0)
             square(2, 0)
-            halves = [(i, k) for i in range(2) for k in range(2)]
-            for i, G in halves:
-                fin(0, G, i)
-            stage1_half(2, 0)
-            q_transposes(3)
-            square(2, 1)
-            stage1_half(2, 1)
             q_scales(3)
-            wo_turn(1, 0, on_s)
-            wo_turn(1, 1, on_s)
+            wo_unit(1, 0, 0, 2, on_v)
+            wo_unit(1, 0, 1, 1, on_v)
+            wo_transpose(1, 1, 0, 3)
+            stage1_group(2, 1, 1)
+            wo_copy(1, 1, 0, on_s)
+            wo_unit(1, 1, 1, 0, on_s)
             y_quant(0, 0, 2)
-            cast(4, on_v)
-            q_quant(3)
             stage2(0, 0, 0, on_s)
             stage2(0, 1, 0, on_s)
-            r_transposes(1)
+            cast_v(4, 0, 2)
+            q_quant(3)
+            r_transpose(1, 0, 0, 2)
+            r_transpose(1, 1, 0, 1)
+            r_transpose(1, 0, 1, 3)
+            r_transpose(1, 1, 1, 0)
             wo_quant(1, 0)
             wo_quant(1, 1)
-            ratios_g(2, wts["o", 1, 1][:].bitcast(F32))
+            square(2, 1)
+            ratios_g(2, wts["o", 1, 1])
             square(3, 0)
             square(3, 1)
             load_q(6)
             load_num(4)
-
+            rings["turn"] = [2, 1, 3, 0]
+            halves = [(i, k) for i in range(2) for k in range(2)]
             for n in range(1, NC - 1):
                 for k, (i, G) in enumerate(halves):
                     fin(n, G, i)
@@ -435,19 +504,23 @@ def tile_aftfull_pb_kernel(tc, q_bytes, q_scale, num, den, Wq, Wo, out):
                 if n + 3 < NC:
                     q_scales(n + 3)
                 if n + 4 < NC:
-                    cast(n + 4, on_s, 0, 1024)
+                    cast_s(n + 4, 0)
                 if n == 1:
                     square(4, 0)
                 if n + 3 < NC:
                     square(n + 3, 1)
+                if n == NC - 3:
+                    ratio(n + 1, 1, nc.vector, w[n + 1, 1])
                 if n + 2 < NC:
                     r_transposes(n + 1)
                 if n + 4 < NC:
-                    cast(n + 4, on_v, 1024, 2 * DM)
+                    cast_v(n + 4, 1, 2)
                 if n + 3 < NC:
                     y_quant(n, 0, 2)
                     q_quant(n + 3)
-                    ratios_g(n + 2, qt[n + 3][:].bitcast(F32))
+                    ratio(n + 2, 0, nc.gpsimd, words(qt[n + 3]))
+                    if n + 4 < NC:
+                        ratio(n + 2, 1, nc.gpsimd, w[n + 2, 1])
                 elif n + 2 < NC:
                     y_quant(n, 0, 2)
                     ratio(NC - 1, 0, nc.gpsimd, y[n][:].bitcast(F32))
@@ -464,7 +537,7 @@ def tile_aftfull_pb_kernel(tc, q_bytes, q_scale, num, den, Wq, Wo, out):
                     fin(b, G, i)
                 for oh in range(2):
                     stage2(a, i, oh, on_s)
-                store(a, i)
+                    store_half(a, i, oh)
                 y_quant(b, i, i + 1)
             for i in range(2):
                 for oh in range(2):

@@ -433,51 +433,56 @@ def tile_aftfull_pb_kernel(tc, q_bytes, q_scale, num, den, Wq, Wo, out):
             q_transpose(2, 1, 1)
             m1(0, 1, 1)
             q_scales(2)
-            m1(1, 0, 0, 2)
             wo_unit(0, 0, 0, 3, on_v)
+            m1(1, 0, 0, 2)
             wo_unit(0, 0, 1, 0, on_v)
             m1(1, 0, 1, 1)
-            wo_unit(0, 1, 0, 3, on_v)
-            wo_unit(0, 1, 1, 0, on_v)
-            sigmoids(0)
-            sig(1, 0, 0)
-            sig(1, 0, 1)
-            stage1_half(1, 1)
+            wo_transpose(0, 1, 0, 3)
+            for c in range(2):
+                for u in range(2):
+                    sig(c, 0, u)
+            m1(1, 1, 0)
+            m1(1, 1, 1)
+            wo_transpose(0, 1, 1, 0)
+            for c in range(2):
+                for u in range(2):
+                    sig(c, 1, u)
             q_quant(2)
             cast_v(3, 0, 2)
             wo_quant(0, 0)
-            wo_quant(0, 1)
-            r_transpose(0, 0, 0, 3)
-            r_transpose(0, 1, 0, 0)
-            stage1_group(2, 0, 0)
             square(1, 1)
-            ratios_g(1, wts["o", 0, 1])
-            r_transpose(0, 0, 1, 2)
-            r_transpose(0, 1, 1, 1)
+            ratios_g(1, wts["o", 0, 0])
+            wo_copy(0, 1, 0, on_v)
+            wo_copy(0, 1, 1, on_v)
+            r_transpose(0, 0, 0, 2)
+            r_transpose(0, 1, 0, 1)
+            stage1_half(2, 0)
+            r_transpose(0, 0, 1, 3)
+            r_transpose(0, 1, 1, 0)
             for i in range(2):
                 for G in range(2):
                     fin(0, G, i)
-            stage1_group(2, 0, 1)
-            q_transpose(3, 0, 3)
-            q_transpose(3, 1, 0)
+            q_transpose(3, 0, 2)
+            q_transpose(3, 1, 1)
             stage1_group(2, 1, 0)
             square(2, 0)
             q_scales(3)
-            wo_unit(1, 0, 0, 2, on_v)
-            wo_unit(1, 0, 1, 1, on_v)
-            wo_transpose(1, 1, 0, 3)
-            stage1_group(2, 1, 1)
-            wo_copy(1, 1, 0, on_s)
-            wo_unit(1, 1, 1, 0, on_s)
+            wo_unit(1, 0, 0, 3, on_s)
+            wo_unit(1, 0, 1, 0, on_s)
+            m1(2, 1, 1)
+            wo_unit(1, 1, 0, 2, on_s)
+            wo_unit(1, 1, 1, 1, on_s)
+            sig(2, 1, 1)
             y_quant(0, 0, 2)
+            wo_quant(0, 1)
             stage2(0, 0, 0, on_s)
             stage2(0, 1, 0, on_s)
             cast_v(4, 0, 2)
             q_quant(3)
-            r_transpose(1, 0, 0, 2)
-            r_transpose(1, 1, 0, 1)
-            r_transpose(1, 0, 1, 3)
-            r_transpose(1, 1, 1, 0)
+            r_transpose(1, 0, 0, 3)
+            r_transpose(1, 1, 0, 0)
+            r_transpose(1, 0, 1, 2)
+            r_transpose(1, 1, 1, 1)
             wo_quant(1, 0)
             wo_quant(1, 1)
             square(2, 1)
@@ -486,7 +491,7 @@ def tile_aftfull_pb_kernel(tc, q_bytes, q_scale, num, den, Wq, Wo, out):
             square(3, 1)
             load_q(6)
             load_num(4)
-            rings["turn"] = [2, 1, 3, 0]
+            rings["turn"] = [3, 0, 2, 1]
             halves = [(i, k) for i in range(2) for k in range(2)]
             for n in range(1, NC - 1):
                 for k, (i, G) in enumerate(halves):
@@ -513,10 +518,11 @@ def tile_aftfull_pb_kernel(tc, q_bytes, q_scale, num, den, Wq, Wo, out):
                     ratio(n + 1, 1, nc.vector, w[n + 1, 1])
                 if n + 2 < NC:
                     r_transposes(n + 1)
+                if n + 3 < NC:
+                    y_quant(n, 0, 2)
                 if n + 4 < NC:
                     cast_v(n + 4, 1, 2)
                 if n + 3 < NC:
-                    y_quant(n, 0, 2)
                     q_quant(n + 3)
                     ratio(n + 2, 0, nc.gpsimd, words(qt[n + 3]))
                     if n + 4 < NC:
@@ -537,9 +543,12 @@ def tile_aftfull_pb_kernel(tc, q_bytes, q_scale, num, den, Wq, Wo, out):
                     fin(b, G, i)
                 for oh in range(2):
                     stage2(a, i, oh, on_s)
-                    store_half(a, i, oh)
+                store(a, i)
                 y_quant(b, i, i + 1)
             for i in range(2):
                 for oh in range(2):
                     stage2(b, i, oh, (on_s, on_v)[oh])
-                    store_half(b, i, oh)
+                    if i == 1:
+                        store_half(b, i, oh)
+                if i == 0:
+                    store(b, 0)

@@ -464,8 +464,8 @@ def tile_aftfull_pb_kernel(tc, q_bytes, q_scale, num, den, Wq, Wo, out):
                     fin(0, G, i)
             q_transpose(3, 0, 2)
             q_transpose(3, 1, 1)
-            stage1_group(2, 1, 0)
             square(2, 0)
+            stage1_group(2, 1, 0)
             q_scales(3)
             wo_unit(1, 0, 0, 3, on_s)
             wo_unit(1, 0, 1, 0, on_s)
@@ -487,8 +487,6 @@ def tile_aftfull_pb_kernel(tc, q_bytes, q_scale, num, den, Wq, Wo, out):
             wo_quant(1, 1)
             square(2, 1)
             ratios_g(2, wts["o", 1, 1])
-            square(3, 0)
-            square(3, 1)
             load_q(6)
             load_num(4)
             rings["turn"] = [3, 0, 2, 1]
@@ -502,18 +500,16 @@ def tile_aftfull_pb_kernel(tc, q_bytes, q_scale, num, den, Wq, Wo, out):
                         store(n - 1, k // 2)
                 if n + 3 < NC:
                     q_transposes(n + 3)
-                if 1 < n + 0 < NC - 3:
-                    square(n + 3, 0)
+                if n + 2 < NC:
+                    square(n + 2, 0)
                 if n + 2 < NC:
                     stage1(n + 2)
                 if n + 3 < NC:
                     q_scales(n + 3)
                 if n + 4 < NC:
                     cast_s(n + 4, 0)
-                if n == 1:
-                    square(4, 0)
-                if n + 3 < NC:
-                    square(n + 3, 1)
+                if n + 2 < NC:
+                    square(n + 2, 1)
                 if n == NC - 3:
                     ratio(n + 1, 1, nc.vector, w[n + 1, 1])
                 if n + 2 < NC:

@@ -94,6 +94,9 @@ def tile_aftfull_pb_kernel(tc, q_bytes, q_scale, num, den, Wq, Wo, out):
         def grouped(slot):
             return sb.tile([P, 2048], BF16, name="grouped", tag=slot, bufs=1, align_bytes=64)
 
+        def wide(slot):
+            return sb.tile([P, 4096], BF16, name="wide", tag=f"wide{slot}", bufs=1, align_bytes=64)
+
         def wq_transpose(G, t):
             words = raw["q", G, t // 2][:].bitcast(F32)
             bank = turn_bank([P, 2, 2, P])
@@ -106,7 +109,7 @@ def tile_aftfull_pb_kernel(tc, q_bytes, q_scale, num, den, Wq, Wo, out):
         def wq_copy(G, t, eng):
             u, e = divmod(t, 2)
             if e == 0:
-                wts["q", G, u] = grouped(f"stage{2 * G + u}")
+                wts["q", G, u] = wide(1) if (G, u) == (1, 1) else grouped(f"stage{2 * G + u}")
             dst = wts["q", G, u][:, 1024 * e : 1024 * (e + 1)].bitcast(F32)
             eng(out=dst.rearrange("p (g m u) -> p g m u", g=2, u=2), in_=banks["wq", G, t][:].rearrange("p g u m -> p g m u"))
 
@@ -116,7 +119,7 @@ def tile_aftfull_pb_kernel(tc, q_bytes, q_scale, num, den, Wq, Wo, out):
             nc.vector.quantize_mx(
                 out=codes[:].rearrange("p e g m -> p (e g m)").bitcast(FP8X4),
                 scales=scales[:].rearrange("p e g m -> p (e g m)"),
-                in_=wts["q", G, u][:],
+                in_=wts["q", G, u][:, 0:2048],
             )
             wq_c[G, u] = (codes, scales)
 
@@ -131,7 +134,7 @@ def tile_aftfull_pb_kernel(tc, q_bytes, q_scale, num, den, Wq, Wo, out):
 
         def wo_copy(oh, g, h, eng):
             if h == 0:
-                wts["o", oh, g] = grouped(("stage1", "stage2", "y1", "stage3")[2 * oh + g])
+                wts["o", oh, g] = grouped(("stage1", "stage2", "y1", "stage1")[2 * oh + g])
             dst = wts["o", oh, g][:].bitcast(F32).rearrange("p (m h x) -> p m h x", h=2, x=4)
             eng(out=dst[:, :, h, :], in_=banks["wo", oh, g, h][:].rearrange("p j u m -> p m (j u)"))
 
@@ -180,7 +183,7 @@ def tile_aftfull_pb_kernel(tc, q_bytes, q_scale, num, den, Wq, Wo, out):
 
         def q_scale_up(c, g):
             if g == 0:
-                qt[c] = sb.tile([P, 2048], BF16, name="qt", tag="qt", bufs=3, align_bytes=64)
+                qt[c] = wide(c % 2)
             nc.vector.tensor_tensor(
                 out=qt[c][:, 1024 * g : 1024 * (g + 1)].rearrange("p (n u e) -> p n u e", u=2, e=2),
                 in0=banks["x", c, g][:].rearrange("p u i n -> p (u i n)").bitcast(BF16).rearrange("p (u n e) -> p n u e", u=2, e=2),
@@ -194,12 +197,14 @@ def tile_aftfull_pb_kernel(tc, q_bytes, q_scale, num, den, Wq, Wo, out):
             nc.vector.quantize_mx(
                 out=codes[:].rearrange("p g n -> p (g n)").bitcast(FP8X4),
                 scales=scales[:].rearrange("p g n -> p (g n)"),
-                in_=qt[c][:],
+                in_=qt[c][:, 0:2048],
             )
             qc[c] = (codes, scales)
 
         def rsqrt(c, i):
-            w[c, i] = sb.tile([P, DH], F32, name="w", tag="w", bufs=2 * NC)[:]
+            if i == 0:
+                w[c] = sb.tile([P, 2 * DH], F32, name="w", tag="w", bufs=NC)
+            w[c, i] = w[c][:, DH * i : DH * (i + 1)]
             nc.scalar.activation(
                 out=w[c, i].rearrange("p (g t m) -> p g t m", g=2, t=4),
                 in_=dent[c, i].rearrange("p (g m t) -> p g t m", g=2, t=4),
@@ -219,6 +224,17 @@ def tile_aftfull_pb_kernel(tc, q_bytes, q_scale, num, den, Wq, Wo, out):
                 out=dst.rearrange("p (g t m) -> p g t m", t=4, m=P),
                 in0=numt[c][:, DH * i : DH * (i + 1)].rearrange("p (g m t) -> p g t m", t=4, m=P),
                 in1=w[c, i].rearrange("p (g t m) -> p g t m", t=4, m=P),
+                op=ALU.mult,
+            )
+
+        def ratio_pair(c, freed):
+            dst = freed[:].bitcast(F32)
+            for i in range(2):
+                rr[c, i] = dst[:, DH * i : DH * (i + 1)]
+            nc.gpsimd.tensor_tensor(
+                out=dst.rearrange("p (g t m) -> p g t m", t=4, m=P),
+                in0=numt[c][:].rearrange("p (g m t) -> p g t m", t=4, m=P),
+                in1=w[c][:].rearrange("p (g t m) -> p g t m", t=4, m=P),
                 op=ALU.mult,
             )
 
@@ -418,7 +434,7 @@ def tile_aftfull_pb_kernel(tc, q_bytes, q_scale, num, den, Wq, Wo, out):
             wq_quant(1, 0)
             cast_v(2, 0, 2)
             wq_quant(1, 1)
-            ratios_g(0, wts["q", 1, 1])
+            ratio_pair(0, wts["q", 1, 1])
             for c in range(2, 4):
                 load_q(c + 2)
                 load_num(c)
@@ -447,11 +463,12 @@ def tile_aftfull_pb_kernel(tc, q_bytes, q_scale, num, den, Wq, Wo, out):
             for c in range(2):
                 for u in range(2):
                     sig(c, 1, u)
-            q_quant(2)
             cast_v(3, 0, 2)
             wo_quant(0, 0)
+            q_quant(2)
             square(1, 1)
-            ratios_g(1, wts["o", 0, 0])
+            ratio(1, 0, nc.gpsimd, words(qt[2])[:, 0:DH])
+            ratio(1, 1, nc.gpsimd, w[1, 1])
             wo_copy(0, 1, 0, on_v)
             wo_copy(0, 1, 1, on_v)
             r_transpose(0, 0, 0, 2)
@@ -466,6 +483,7 @@ def tile_aftfull_pb_kernel(tc, q_bytes, q_scale, num, den, Wq, Wo, out):
             q_transpose(3, 1, 1)
             square(2, 0)
             stage1_group(2, 1, 0)
+            square(2, 1)
             q_scales(3)
             wo_unit(1, 0, 0, 3, on_s)
             wo_unit(1, 0, 1, 0, on_s)
@@ -478,15 +496,15 @@ def tile_aftfull_pb_kernel(tc, q_bytes, q_scale, num, den, Wq, Wo, out):
             stage2(0, 0, 0, on_s)
             stage2(0, 1, 0, on_s)
             cast_v(4, 0, 2)
-            q_quant(3)
             r_transpose(1, 0, 0, 3)
             r_transpose(1, 1, 0, 0)
             r_transpose(1, 0, 1, 2)
             r_transpose(1, 1, 1, 1)
             wo_quant(1, 0)
             wo_quant(1, 1)
-            square(2, 1)
-            ratios_g(2, wts["o", 1, 1])
+            q_quant(3)
+            ratio_pair(2, qt[3])
+            square(3, 0)
             load_q(6)
             load_num(4)
             rings["turn"] = [3, 0, 2, 1]
@@ -501,15 +519,15 @@ def tile_aftfull_pb_kernel(tc, q_bytes, q_scale, num, den, Wq, Wo, out):
                 if n + 3 < NC:
                     q_transposes(n + 3)
                 if n + 2 < NC:
-                    square(n + 2, 0)
+                    square(n + 2, 1)
                 if n + 2 < NC:
                     stage1(n + 2)
                 if n + 3 < NC:
                     q_scales(n + 3)
                 if n + 4 < NC:
                     cast_s(n + 4, 0)
-                if n + 2 < NC:
-                    square(n + 2, 1)
+                if n + 3 < NC:
+                    square(n + 3, 0)
                 if n == NC - 3:
                     ratio(n + 1, 1, nc.vector, w[n + 1, 1])
                 if n + 2 < NC:
@@ -520,9 +538,10 @@ def tile_aftfull_pb_kernel(tc, q_bytes, q_scale, num, den, Wq, Wo, out):
                     cast_v(n + 4, 1, 2)
                 if n + 3 < NC:
                     q_quant(n + 3)
-                    ratio(n + 2, 0, nc.gpsimd, words(qt[n + 3]))
                     if n + 4 < NC:
-                        ratio(n + 2, 1, nc.gpsimd, w[n + 2, 1])
+                        ratio_pair(n + 2, qt[n + 3])
+                    else:
+                        ratio(n + 2, 0, nc.gpsimd, words(qt[n + 3])[:, 0:DH])
                 elif n + 2 < NC:
                     y_quant(n, 0, 2)
                     ratio(NC - 1, 0, nc.gpsimd, y[n][:].bitcast(F32))

@@ -17,6 +17,8 @@ T, DM, DH, DO = 2048, 1024, 1024, 1024
 CH = 256
 NC = T // CH
 FLOPS = 2 * T * DM * DH + 2 * T * DH * DO
+GROUP = 512
+EARLY = 3
 
 
 def tile_aftfull_pb_kernel(tc, q_bytes, q_scale, num, den, Wq, Wo, out):
@@ -35,29 +37,25 @@ def tile_aftfull_pb_kernel(tc, q_bytes, q_scale, num, den, Wq, Wo, out):
         ident = sb.tile([P, P], F32, name="ident")
         make_identity(nc, ident[:])
         sc = sb.tile([P, 2, 4], F32, name="sc")
-
         one = sb.tile([P, 1], F32, name="one")
         nc.vector.memset(one[:], 1.0)
-        sorted_words = {}
-        raw, banks, wts, wq_c, wo_c = {}, {}, {}, {}, {}
+
+        raw, banks, staged, wq_c, wo_c = {}, {}, {}, {}, {}
         qb, qx, qt, qc = {}, {}, {}, {}
+        unsorted, w2 = set(), {}
         dent, numt, w, rr, s, y, yc, o = {}, {}, {}, {}, {}, {}, {}, {}
-
-        rings = {"turn": [0, 1, 2, 3], "sum": [4, 5, 6, 7]}
-
-        def next_bank(ring):
-            k = rings[ring][0]
-            rings[ring] = rings[ring][1:] + [k]
-            return k
 
         def bank_tile(shape, k):
             return ps.tile(shape, F32, name="bank", tag=f"bank{k}", bufs=1)
 
-        def turn_bank(shape, k=None):
-            return bank_tile(shape, next_bank("turn") if k is None else k)
+        def wide(slot):
+            return sb.tile([P, 4096], BF16, name="wide", tag=f"wide{slot}", bufs=1, align_bytes=64)
 
-        def sum_bank(shape, k=None):
-            return bank_tile(shape, next_bank("sum") if k is None else k)
+        def narrow(slot):
+            return sb.tile([P, 2048], BF16, name="narrow", tag=f"narrow{slot}", bufs=1, align_bytes=64)
+
+        def words(tile):
+            return tile[:].bitcast(F32)
 
         def load_sc():
             nc.sync.dma_start(out=sc[:], in_=q_scale.rearrange("a b (g p t) -> p (a b g) t", p=P, t=4))
@@ -77,7 +75,7 @@ def tile_aftfull_pb_kernel(tc, q_bytes, q_scale, num, den, Wq, Wo, out):
             nc.sync.dma_start(out=qb[c][:], in_=q_v[c].rearrange("p i d -> p (i d)"))
 
         def load_den_half(c, i):
-            half = sb.tile([P, DH], BF16, name="den_half", tag="den_half", bufs=2)
+            half = sb.tile([P, DH], BF16, name="den_half", tag="den_half", bufs=4)
             nc.sync.dma_start(out=half[:], in_=den_v[c][:, i, :])
             dent[c, i] = half[:]
 
@@ -91,26 +89,18 @@ def tile_aftfull_pb_kernel(tc, q_bytes, q_scale, num, den, Wq, Wo, out):
             numt[c] = sb.tile([P, 2 * DH], BF16, name="numt", tag="numt", bufs=3)
             nc.sync.dma_start(out=numt[c][:], in_=num_v[c].rearrange("p i d -> p (i d)"))
 
-        def grouped(slot):
-            return sb.tile([P, 2048], BF16, name="grouped", tag=slot, bufs=1, align_bytes=64)
-
-        def wide(slot):
-            return sb.tile([P, 4096], BF16, name="wide", tag=f"wide{slot}", bufs=1, align_bytes=64)
-
-        def wq_transpose(G, t):
-            words = raw["q", G, t // 2][:].bitcast(F32)
-            bank = turn_bank([P, 2, 2, P])
+        def wq_transpose(G, t, k):
+            src = words(raw["q", G, t // 2])
+            bank = bank_tile([P, 2, 2, P], k)
             for g in range(2):
                 s0 = 512 * (t % 2) + 256 * g
                 for u in range(2):
-                    nc.tensor.transpose(bank[:, g, u, :], words[:, s0 + u : s0 + 256 : 2], ident[:])
+                    nc.tensor.transpose(bank[:, g, u, :], src[:, s0 + u : s0 + 256 : 2], ident[:])
             banks["wq", G, t] = bank
 
         def wq_copy(G, t, eng):
             u, e = divmod(t, 2)
-            if e == 0:
-                wts["q", G, u] = wide(1) if (G, u) == (1, 1) else grouped(f"stage{2 * G + u}")
-            dst = wts["q", G, u][:, 1024 * e : 1024 * (e + 1)].bitcast(F32)
+            dst = staged["q", G, u][:, 1024 * e : 1024 * (e + 1)].bitcast(F32)
             eng(out=dst.rearrange("p (g m u) -> p g m u", g=2, u=2), in_=banks["wq", G, t][:].rearrange("p g u m -> p g m u"))
 
         def wq_quant(G, u):
@@ -119,71 +109,59 @@ def tile_aftfull_pb_kernel(tc, q_bytes, q_scale, num, den, Wq, Wo, out):
             nc.vector.quantize_mx(
                 out=codes[:].rearrange("p e g m -> p (e g m)").bitcast(FP8X4),
                 scales=scales[:].rearrange("p e g m -> p (e g m)"),
-                in_=wts["q", G, u][:, 0:2048],
+                in_=staged["q", G, u][:, 0:2048],
             )
             wq_c[G, u] = (codes, scales)
 
-        def wo_transpose(oh, g, h, k=None):
-            bank = turn_bank([P, 2, 2, P], k)
-            words = raw["o", oh, h][:].bitcast(F32)
+        def wo_transpose(oh, g, h, k):
+            bank = bank_tile([P, 2, 2, P], k)
+            src = words(raw["o", oh, h])
             for j in range(2):
                 s0 = 512 * j + 256 * g
                 for u in range(2):
-                    nc.tensor.transpose(bank[:, j, u, :], words[:, s0 + u : s0 + 256 : 2], ident[:])
+                    nc.tensor.transpose(bank[:, j, u, :], src[:, s0 + u : s0 + 256 : 2], ident[:])
             banks["wo", oh, g, h] = bank
 
         def wo_copy(oh, g, h, eng):
-            if h == 0:
-                wts["o", oh, g] = grouped(("stage1", "stage2", "y1", "stage1")[2 * oh + g])
-            dst = wts["o", oh, g][:].bitcast(F32).rearrange("p (m h x) -> p m h x", h=2, x=4)
+            dst = staged["o", oh, g][:, 0:2048].bitcast(F32).rearrange("p (m h x) -> p m h x", h=2, x=4)
             eng(out=dst[:, :, h, :], in_=banks["wo", oh, g, h][:].rearrange("p j u m -> p m (j u)"))
 
         def wo_quant(oh, g):
             codes = sb.tile([P, 512], U32, name=f"woc{oh}{g}", align_bytes=64)
             scales = sb.tile([P, 512], U8, name=f"wos{oh}{g}", align_bytes=64)
-            nc.vector.quantize_mx(out=codes[:].bitcast(FP8X4), scales=scales[:], in_=wts["o", oh, g][:])
+            nc.vector.quantize_mx(out=codes[:].bitcast(FP8X4), scales=scales[:], in_=staged["o", oh, g][:, 0:2048])
             wo_c[oh, g] = (codes, scales)
 
-        def widened(c):
-            if c not in qx:
-                qx[c] = sb.tile([P, 2 * DM], BF16, name="qx", tag="qx", bufs=2)
-            return qx[c]
-
-        def cast_s(c, i):
-            cols = slice(DM * i, DM * (i + 1))
-            nc.scalar.copy(out=widened(c)[:, cols], in_=qb[c][:, cols].bitcast(FP8))
-            sorted_words[c, i] = False
-
-        def cast_v(c, i0, i1):
-            cols = slice(DM * i0, DM * i1)
+        def widen(c):
+            qx[c] = sb.tile([P, 2 * DM], BF16, name="qx", tag="qx", bufs=2)
             nc.vector.tensor_scalar(
-                out=widened(c)[:, cols].rearrange("p (u x e) -> p x u e", u=2, e=2),
-                in0=qb[c][:, cols].bitcast(FP8),
+                out=qx[c][:].rearrange("p (u x e) -> p x u e", u=2, e=2),
+                in0=qb[c][:].bitcast(FP8),
                 scalar1=one[:],
                 scalar2=None,
                 op0=ALU.mult,
             )
-            for i in range(i0, i1):
-                sorted_words[c, i] = (512 * i0 + 256 * (i - i0), 256 * (i1 - i0))
 
-        def q_transpose(c, g, k=None):
-            words = qx[c][:].bitcast(F32)
-            bank = turn_bank([P, 2, 2, P], k)
+        def widen_s(c):
+            qx[c] = sb.tile([P, 2 * DM], BF16, name="qx", tag="qx", bufs=2)
+            nc.scalar.copy(out=qx[c][:], in_=qb[c][:].bitcast(FP8))
+            unsorted.add(c)
+
+        def q_transpose(c, g, k):
+            src = words(qx[c])
+            bank = bank_tile([P, 2, 2, P], k)
             for i in range(2):
                 for u in range(2):
-                    if sorted_words[c, i]:
-                        first, plane = sorted_words[c, i]
-                        s0 = first + plane * u + P * g
-                        src = words[:, s0 : s0 + P]
-                    else:
+                    if c in unsorted:
                         s0 = 512 * i + 256 * g
-                        src = words[:, s0 + u : s0 + 256 : 2]
-                    nc.tensor.transpose(bank[:, u, i, :], src, ident[:])
+                        cols = slice(s0 + u, s0 + 256, 2)
+                    else:
+                        s0 = 512 * u + 256 * i + P * g
+                        cols = slice(s0, s0 + P)
+                    nc.tensor.transpose(bank[:, u, i, :], src[:, cols], ident[:])
             banks["x", c, g] = bank
 
         def q_scale_up(c, g):
-            if g == 0:
-                qt[c] = wide(c % 2)
             nc.vector.tensor_tensor(
                 out=qt[c][:, 1024 * g : 1024 * (g + 1)].rearrange("p (n u e) -> p n u e", u=2, e=2),
                 in0=banks["x", c, g][:].rearrange("p u i n -> p (u i n)").bitcast(BF16).rearrange("p (u n e) -> p n u e", u=2, e=2),
@@ -191,98 +169,88 @@ def tile_aftfull_pb_kernel(tc, q_bytes, q_scale, num, den, Wq, Wo, out):
                 op=ALU.mult,
             )
 
+        def code_tiles():
+            codes = sb.tile([P, 512], U32, name="codes", tag="codes", bufs=3, align_bytes=64)
+            scales = sb.tile([P, 512], U8, name="scales", tag="scales", bufs=3, align_bytes=64)
+            return codes, scales
+
         def q_quant(c):
-            codes = sb.tile([P, 2, CH], U32, name="qcod", tag="qcod", bufs=3, align_bytes=64)
-            scales = sb.tile([P, 2, CH], U8, name="qscl", tag="qscl", bufs=3, align_bytes=64)
-            nc.vector.quantize_mx(
-                out=codes[:].rearrange("p g n -> p (g n)").bitcast(FP8X4),
-                scales=scales[:].rearrange("p g n -> p (g n)"),
-                in_=qt[c][:, 0:2048],
-            )
-            qc[c] = (codes, scales)
+            qc[c] = code_tiles()
+            nc.vector.quantize_mx(out=qc[c][0][:].bitcast(FP8X4), scales=qc[c][1][:], in_=qt[c][:, 0:2048])
 
         def rsqrt(c, i):
             if i == 0:
-                w[c] = sb.tile([P, 2 * DH], F32, name="w", tag="w", bufs=NC)
-            w[c, i] = w[c][:, DH * i : DH * (i + 1)]
+                w[c] = sb.tile([P, 2 * DH], F32, name="w", tag="w", bufs=4, align_bytes=64)[:]
             nc.scalar.activation(
-                out=w[c, i].rearrange("p (g t m) -> p g t m", g=2, t=4),
+                out=w[c][:, DH * i : DH * (i + 1)].rearrange("p (g t m) -> p g t m", g=2, t=4),
                 in_=dent[c, i].rearrange("p (g m t) -> p g t m", g=2, t=4),
                 func=ACT.Abs_reciprocal_sqrt,
             )
 
-        def square(c, i):
-            nc.scalar.activation(out=w[c, i], in_=w[c, i], func=ACT.Square)
+        def square_s(c, lo, hi):
+            cols = slice(GROUP * lo, GROUP * hi)
+            nc.scalar.activation(out=w2.setdefault(c, w[c])[:, cols], in_=w[c][:, cols], func=ACT.Square)
 
-        def square_g(c, i, dst):
-            nc.gpsimd.tensor_tensor(out=dst, in0=w[c, i], in1=w[c, i], op=ALU.mult)
-            w[c, i] = dst
+        def square_g(c, lo, hi, dst=None):
+            src = w[c][:, GROUP * lo : GROUP * hi]
+            w2[c] = w[c] if dst is None else dst
+            nc.gpsimd.tensor_tensor(out=w2[c][:, GROUP * lo : GROUP * hi], in0=src, in1=src, op=ALU.mult)
 
-        def ratio(c, i, eng, dst):
-            rr[c, i] = dst
+        def ratio(c, lo, hi, eng, dst=None):
+            cols = slice(GROUP * lo, GROUP * hi)
+            dst = w2[c][:, cols] if dst is None else dst[:, 0 : GROUP * (hi - lo)]
+            for x in range(lo, hi):
+                rr[c, x] = dst[:, GROUP * (x - lo) : GROUP * (x - lo + 1)]
             eng.tensor_tensor(
-                out=dst.rearrange("p (g t m) -> p g t m", t=4, m=P),
-                in0=numt[c][:, DH * i : DH * (i + 1)].rearrange("p (g m t) -> p g t m", t=4, m=P),
-                in1=w[c, i].rearrange("p (g t m) -> p g t m", t=4, m=P),
+                out=dst.rearrange("p (x t m) -> p x t m", t=4, m=P),
+                in0=numt[c][:, cols].rearrange("p (x m t) -> p x t m", t=4, m=P),
+                in1=w2[c][:, cols].rearrange("p (x t m) -> p x t m", t=4, m=P),
                 op=ALU.mult,
             )
 
-        def ratio_pair(c, freed):
-            dst = freed[:].bitcast(F32)
-            for i in range(2):
-                rr[c, i] = dst[:, DH * i : DH * (i + 1)]
-            nc.gpsimd.tensor_tensor(
-                out=dst.rearrange("p (g t m) -> p g t m", t=4, m=P),
-                in0=numt[c][:].rearrange("p (g m t) -> p g t m", t=4, m=P),
-                in1=w[c][:].rearrange("p (g t m) -> p g t m", t=4, m=P),
-                op=ALU.mult,
-            )
-
-        def m1(c, G, u, k=None):
+        def m1(c, G, u, k):
             codes, scales = qc[c]
             wc, ws = wq_c[G, u]
-            bank = sum_bank([P, 2, CH], k)
+            bank = bank_tile([P, 2, CH], k)
             for e in range(2):
                 for g in range(2):
                     nc.tensor.matmul_mx(
                         out=bank[:, e, :],
                         lhsT=wc[:, e, g, :].bitcast(FP8X4),
                         lhsT_scale=ws[:, e, g, :],
-                        rhs=codes[:, g, :].bitcast(FP8X4),
-                        rhs_scale=scales[:, g, :],
+                        rhs=codes[:, CH * g : CH * (g + 1)].bitcast(FP8X4),
+                        rhs_scale=scales[:, CH * g : CH * (g + 1)],
                         start=(g == 0),
                         stop=(g == 1),
                     )
             banks["m1", c, G, u] = bank
 
+        def page():
+            return sb.tile([P, 1024], F32, name="page", tag="page", bufs=18)
+
         def sig(c, G, u):
             if u == 0:
-                s[c, G] = sb.tile([P, 2, CH, 2], F32, name="s", tag="s", bufs=6)
+                s[c, G] = page()[:].rearrange("p (u n e) -> p u n e", u=2, e=2)
             nc.scalar.activation(out=s[c, G][:, u, :, :], in_=banks["m1", c, G, u][:].rearrange("p e n -> p n e"), func=ACT.Sigmoid)
 
-        def r_transpose(c, G, i, k=None):
-            bank = turn_bank([P, 4, P], k)
+        def r_transpose(c, i, G, k):
+            bank = bank_tile([P, 4, P], k)
             for t in range(4):
-                s0 = 512 * G + P * t
-                nc.tensor.transpose(bank[:, t, :], rr[c, i][:, s0 : s0 + P], ident[:])
-            banks["r", c, G, i] = bank
+                nc.tensor.transpose(bank[:, t, :], rr[c, 2 * i + G][:, P * t : P * (t + 1)], ident[:])
+            banks["r", c, i, G] = bank
 
-        def fin(c, G, i):
-            if (G, i) == (0, 0):
-                y[c] = grouped(f"y{c % 2}")
+        def fin(c, i, G):
             s0 = 1024 * i + 512 * G
             nc.vector.tensor_tensor(
                 out=y[c][:, s0 : s0 + 512].rearrange("p (n u e) -> p n u e", u=2, e=2),
-                in0=banks["r", c, G, i][:].rearrange("p (u e) n -> p n u e", u=2),
+                in0=banks["r", c, i, G][:].rearrange("p (u e) n -> p n u e", u=2),
                 in1=s[c, G][:, :, i * P : (i + 1) * P, :].rearrange("p u n e -> p n u e"),
                 op=ALU.mult,
             )
 
-        def y_quant(c, i0, i1):
+        def y_quant(c, i0=0, i1=2):
             if i0 == 0:
-                codes = sb.tile([P, 512], U32, name="ycod", tag="ycod", bufs=3, align_bytes=64)
-                scales = sb.tile([P, 512], U8, name="yscl", tag="yscl", bufs=3, align_bytes=64)
-                yc[c] = (codes, scales)
+                yc[c] = code_tiles()
             codes, scales = yc[c]
             nc.vector.quantize_mx(
                 out=codes[:, 256 * i0 : 256 * i1].bitcast(FP8X4),
@@ -290,8 +258,8 @@ def tile_aftfull_pb_kernel(tc, q_bytes, q_scale, num, den, Wq, Wo, out):
                 in_=y[c][:, 1024 * i0 : 1024 * i1],
             )
 
-        def m2(c, i, oh, lo=0, hi=512):
-            bank = sum_bank([P, hi - lo])
+        def m2(c, i, oh, k):
+            bank = bank_tile([P, 512], k)
             codes, scales = yc[c]
             for G in range(2):
                 s0 = 256 * i + P * G
@@ -299,271 +267,254 @@ def tile_aftfull_pb_kernel(tc, q_bytes, q_scale, num, den, Wq, Wo, out):
                     out=bank[:],
                     lhsT=codes[:, s0 : s0 + P].bitcast(FP8X4),
                     lhsT_scale=scales[:, s0 : s0 + P],
-                    rhs=wo_c[oh, G][0][:, lo:hi].bitcast(FP8X4),
-                    rhs_scale=wo_c[oh, G][1][:, lo:hi],
+                    rhs=wo_c[oh, G][0][:].bitcast(FP8X4),
+                    rhs_scale=wo_c[oh, G][1][:],
                     start=(G == 0),
                     stop=(G == 1),
                 )
             banks["m2", c, i, oh] = bank
 
-        def copy_out(c, i, oh, eng, lo=0, hi=512):
+        def copy_out(c, i, oh, eng):
             if (c, i) not in o:
-                o[c, i] = sb.tile([P, DO], F32, name="o", tag="o", bufs=4)
-            eng(out=o[c, i][:, 512 * oh + lo : 512 * oh + hi], in_=banks["m2", c, i, oh][:])
+                o[c, i] = page()
+            eng(out=o[c, i][:, 512 * oh : 512 * (oh + 1)], in_=banks["m2", c, i, oh][:])
 
-        def store(c, i):
-            nc.sync.dma_start(out=out_v[c][:, i, :], in_=o[c, i][:])
-
-        def store_cols(c, i, lo, hi):
+        def store(c, i, lo=0, hi=DO):
             nc.sync.dma_start(out=out_v[c][:, i, lo:hi], in_=o[c, i][:, lo:hi])
 
-        def store_half(c, i, oh):
-            store_cols(c, i, 512 * oh, 512 * (oh + 1))
-
         on_v, on_s = nc.vector.tensor_copy, nc.scalar.copy
+        pairs = [(a, b) for a in range(2) for b in range(2)]
+
+        def q_transposes(c):
+            for g in range(2):
+                q_transpose(c, g, 2 * (c % 2) + g)
+
+        def q_scales(c):
+            for g in range(2):
+                q_scale_up(c, g)
+
+        def r_transposes(c):
+            for i, G in pairs:
+                r_transpose(c, i, G, 2 * i + G)
+
+        def fins(c):
+            for i, G in pairs:
+                fin(c, i, G)
+
+        def roots(c):
+            for i in range(2):
+                rsqrt(c, i)
+            for i in range(2):
+                square_s(c, 2 * i, 2 * i + 2)
+
+        ring = [4, 5, 6, 7]
+
+        def sum_bank():
+            ring.append(ring.pop(0))
+            return ring[-1]
+
+        def gate(c, G, u):
+            m1(c, G, u, sum_bank())
+            sig(c, G, u)
+
+        def gates(c):
+            for G, u in pairs:
+                gate(c, G, u)
+
+        wo_units = [(oh, g, h) for oh in range(2) for g, h in pairs]
+
+        def wo_turn(unit):
+            wo_transpose(*wo_units[unit], sum_bank())
+
+        def wo_move(unit, eng):
+            wo_copy(*wo_units[unit], eng)
+
+        def wo_unit(unit):
+            wo_turn(unit)
+            wo_move(unit, on_s)
+
+        def products(c):
+            for i, oh in pairs:
+                m2(c, i, oh, sum_bank())
+
+        def copies(c, engs):
+            for (i, oh), eng in zip(pairs, engs):
+                copy_out(c, i, oh, eng)
+                if oh == 1:
+                    store(c, i)
 
         with tc.manual_schedule():
-
-            def stage1_matmuls(c):
-                for G in range(2):
-                    for u in range(2):
-                        m1(c, G, u)
-
-            def sigmoids(c):
-                for G in range(2):
-                    for u in range(2):
-                        sig(c, G, u)
-
-            def stage1(c):
-                for G in range(2):
-                    for u in range(2):
-                        m1(c, G, u)
-                        sig(c, G, u)
-
-            def rsqrts(c):
-                rsqrt(c, 0)
-                rsqrt(c, 1)
-
-            def r_transposes(c):
-                for i in range(2):
-                    for G in range(2):
-                        r_transpose(c, G, i)
-
-            def q_transposes(c):
-                q_transpose(c, 0)
-                q_transpose(c, 1)
-
-            def q_scales(c):
-                q_scale_up(c, 0)
-                q_scale_up(c, 1)
-
-            def wq_turn(G, u):
-                for e in range(2):
-                    wq_transpose(G, 2 * u + e)
-                    wq_copy(G, 2 * u + e, on_v)
-
-            def wo_turn(oh, g, eng):
-                for h in range(2):
-                    wo_transpose(oh, g, h)
-                    wo_copy(oh, g, h, eng)
-
-
-            def stage1_half(c, G):
-                for u in range(2):
-                    m1(c, G, u)
-                    sig(c, G, u)
-
-            def stage2(c, i, oh, eng):
-                m2(c, i, oh)
-                copy_out(c, i, oh, eng)
-
-            def ratios_g(c, freed):
-                ratio(c, 0, nc.gpsimd, freed[:].bitcast(F32))
-                ratio(c, 1, nc.gpsimd, w[c, 1])
-
-            def stage1_group(c, G, u):
-                m1(c, G, u)
-                sig(c, G, u)
-
-            def words(tile):
-                return tile[:].bitcast(F32)
-
-            def ratio_g(c, i, dst=None):
-                ratio(c, i, nc.gpsimd, w[c, i] if dst is None else dst)
-
             load_q(0)
             load_den_half(0, 0)
             load_q(1)
             load_den_half(0, 1)
             load_sc()
-            load_den(1)
-            rsqrts(0)
-            cast_v(0, 0, 2)
-            cast_v(1, 0, 2)
-            square_g(0, 0, w[0, 0])
-            square_g(0, 1, w[0, 1])
+            load_den_half(1, 0)
+            load_wq(0, 0)
+            load_den_half(1, 1)
+            load_wq(0, 1)
+            load_den(2)
+            load_wq(1, 0)
+            load_wq(1, 1)
+            load_q(2)
+            load_den(3)
+            load_q(3)
+            load_wo(0, 0)
+            load_wo(0, 1)
+            widen(0)
+            widen(1)
+            for i in range(2):
+                rsqrt(0, i)
+                square_g(0, 2 * i, 2 * i + 2)
+            rsqrt(1, 0)
+            rsqrt(1, 1)
+            qt[0], qt[1] = narrow(0), narrow(1)
             for c in range(2):
                 q_transposes(c)
                 q_scales(c)
-            for n in range(4):
-                load_wq(*divmod(n, 2))
-                rsqrts(1 + n)
-                load_den(2 + n)
-            load_q(2)
-            rsqrts(5)
-            load_den(6)
+            staged["q", 0, 0], staged["q", 0, 1], staged["q", 1, 0], staged["q", 1, 1] = narrow(2), narrow(3), wide(1), wide(0)
+            for t, k in enumerate((4, 5, 0, 1)):
+                wq_transpose(0, t, k)
+                wq_copy(0, t, on_s if t < 2 else on_v)
+            rsqrt(2, 0)
+            rsqrt(2, 1)
+            for t, k in enumerate((2, 3, 6, 7)):
+                wq_transpose(1, t, k)
+                wq_copy(1, t, on_s)
+            rsqrt(3, 0)
+            rsqrt(3, 1)
+            q_quant(0)
+            wq_quant(0, 0)
+            q_quant(1)
+            wq_quant(0, 1)
+            widen(2)
+            wq_quant(1, 0)
+            widen(3)
+            wq_quant(1, 1)
+            square_g(1, 0, 3, words(staged["q", 1, 1]))
             load_num(0)
-            rsqrts(6)
-            load_den(7)
-            rsqrts(7)
-            load_wo(0, 0)
-            load_wo(0, 1)
-            load_q(3)
+            load_q(4)
+            load_q(5)
             load_wo(1, 0)
             load_wo(1, 1)
             load_num(1)
-            wq_turn(0, 0)
-            q_quant(0)
-            q_quant(1)
-            wq_quant(0, 0)
-            square_g(1, 0, words(wts["q", 0, 0]))
-            wq_turn(0, 1)
-            wq_turn(1, 0)
-            wq_turn(1, 1)
-            wq_quant(0, 1)
-            wq_quant(1, 0)
-            cast_v(2, 0, 2)
-            wq_quant(1, 1)
-            ratio_pair(0, wts["q", 1, 1])
-            for c in range(2, 4):
-                load_q(c + 2)
-                load_num(c)
-            def wo_unit(oh, g, h, k, eng):
-                wo_transpose(oh, g, h, k)
-                wo_copy(oh, g, h, eng)
-
-            m1(0, 0, 0)
-            m1(0, 0, 1)
-            m1(0, 1, 0)
-            q_transpose(2, 0, 0)
-            q_transpose(2, 1, 1)
-            m1(0, 1, 1)
+            for u in range(2):
+                for c in range(2):
+                    m1(c, 0, u, sum_bank())
+                q_transposes(2 + u)
+            qt[2], qt[3] = narrow(0), wide(1)
             q_scales(2)
-            wo_unit(0, 0, 0, 3, on_v)
-            m1(1, 0, 0, 2)
-            wo_unit(0, 0, 1, 0, on_v)
-            m1(1, 0, 1, 1)
-            wo_transpose(0, 1, 0, 3)
-            for c in range(2):
-                for u in range(2):
-                    sig(c, 0, u)
-            m1(1, 1, 0)
-            m1(1, 1, 1)
-            wo_transpose(0, 1, 1, 0)
-            for c in range(2):
-                for u in range(2):
-                    sig(c, 1, u)
-            cast_v(3, 0, 2)
-            wo_quant(0, 0)
-            q_quant(2)
-            square(1, 1)
-            ratio(1, 0, nc.gpsimd, words(qt[2])[:, 0:DH])
-            ratio(1, 1, nc.gpsimd, w[1, 1])
-            wo_copy(0, 1, 0, on_v)
-            wo_copy(0, 1, 1, on_v)
-            r_transpose(0, 0, 0, 2)
-            r_transpose(0, 1, 0, 1)
-            stage1_half(2, 0)
-            r_transpose(0, 0, 1, 3)
-            r_transpose(0, 1, 1, 0)
-            for i in range(2):
-                for G in range(2):
-                    fin(0, G, i)
-            q_transpose(3, 0, 2)
-            q_transpose(3, 1, 1)
-            square(2, 0)
-            stage1_group(2, 1, 0)
-            square(2, 1)
             q_scales(3)
-            wo_unit(1, 0, 0, 3, on_s)
-            wo_unit(1, 0, 1, 0, on_s)
-            m1(2, 1, 1)
-            wo_unit(1, 1, 0, 2, on_s)
-            wo_unit(1, 1, 1, 1, on_s)
-            sig(2, 1, 1)
-            y_quant(0, 0, 2)
-            wo_quant(0, 1)
-            stage2(0, 0, 0, on_s)
-            stage2(0, 1, 0, on_s)
-            cast_v(4, 0, 2)
-            r_transpose(1, 0, 0, 3)
-            r_transpose(1, 1, 0, 0)
-            r_transpose(1, 0, 1, 2)
-            r_transpose(1, 1, 1, 1)
-            wo_quant(1, 0)
-            wo_quant(1, 1)
-            q_quant(3)
-            ratio_pair(2, qt[3])
-            square(3, 0)
-            load_q(6)
-            load_num(4)
-            rings["turn"] = [3, 0, 2, 1]
-            halves = [(i, k) for i in range(2) for k in range(2)]
-            for n in range(1, NC - 1):
-                for k, (i, G) in enumerate(halves):
-                    fin(n, G, i)
-                    if n > 1 or k % 2 == 1:
-                        stage2(n - 1, *halves[k], on_v if k == 3 and n < NC - 2 else on_s)
-                    if k % 2 == 1:
-                        store(n - 1, k // 2)
-                if n + 3 < NC:
-                    q_transposes(n + 3)
-                if n + 2 < NC:
-                    square(n + 2, 1)
-                if n + 2 < NC:
-                    stage1(n + 2)
-                if n + 3 < NC:
-                    q_scales(n + 3)
-                if n + 4 < NC:
-                    cast_s(n + 4, 0)
-                if n + 3 < NC:
-                    square(n + 3, 0)
-                if n == NC - 3:
-                    ratio(n + 1, 1, nc.vector, w[n + 1, 1])
-                if n + 2 < NC:
-                    r_transposes(n + 1)
-                if n + 3 < NC:
-                    y_quant(n, 0, 2)
-                if n + 4 < NC:
-                    cast_v(n + 4, 1, 2)
-                if n + 3 < NC:
-                    q_quant(n + 3)
-                    if n + 4 < NC:
-                        ratio_pair(n + 2, qt[n + 3])
-                    else:
-                        ratio(n + 2, 0, nc.gpsimd, words(qt[n + 3])[:, 0:DH])
-                elif n + 2 < NC:
-                    y_quant(n, 0, 2)
-                    ratio(NC - 1, 0, nc.gpsimd, y[n][:].bitcast(F32))
-                if n + 6 < NC:
-                    load_q(n + 6)
-                if n + 4 < NC:
-                    load_num(n + 4)
+            for c in range(2):
+                m1(c, 1, 0, c)
+            for u in range(2):
+                for c in range(2):
+                    sig(c, 0, u)
+            for c in range(2):
+                sig(c, 1, 0)
+            for c in range(2):
+                gate(c, 1, 1)
+            staged["o", 0, 0], staged["o", 0, 1] = narrow(2), narrow(3)
+            staged["o", 1, 0], staged["o", 1, 1] = narrow(1), narrow(4)
+            for unit in range(2):
+                wo_unit(unit)
+            square_s(1, 3, 4)
+            for a in (2, 4):
+                b, n = a + 1, a // 2 - 1
+                widen(a + 2)
+                q_quant(a)
+                widen(b + 2)
+                q_quant(b)
+                ratio(n, 0, 4, nc.gpsimd, words(qt[b]))
+                if a == 2:
+                    load_q(6)
+                    load_q(7)
+                    load_num(2)
+                    load_den(4)
+                    load_den(5)
+                    load_den(6)
+                load_num(3 + n)
+                q_transposes(a + 2)
+                gates(a)
+                q_transposes(b + 2)
+                qt[a + 2], qt[b + 2] = narrow(0), wide(2) if a == 2 else w[1].bitcast(BF16)
+                q_scales(a + 2)
+                wo_transpose(*wo_units[2 + 3 * n], 0)
+                q_scales(b + 2)
+                wo_move(2 + 3 * n, on_v)
+                square_s(2, 2 * n, 2 * n + 2)
+                gates(b)
+                wo_unit(3 + 3 * n)
+                wo_unit(4 + 3 * n)
+            q_quant(6)
+            q_quant(7)
+            for oh, g in pairs:
+                wo_quant(oh, g)
+            ratio(2, 0, 2, nc.gpsimd, words(staged["o", 1, 1]))
+            r_transposes(0)
+            square_s(3, 0, 2)
+            gates(6)
+            y[0] = narrow(2)
+            fins(0)
+            y_quant(0)
+            ratio(2, 2, 4, nc.gpsimd, words(y[0]))
+            load_num(5)
+            y[1] = wide(1)
+            r_transposes(1)
+            square_s(3, 2, 4)
+            gates(7)
+            products(0)
+            fins(1)
+            copy_out(0, 0, 0, on_v)
+            y_quant(1)
+            ratio(3, 0, 3, nc.gpsimd, words(y[1]))
+            copy_out(0, 0, 1, on_v)
+            store(0, 0)
+            for oh in range(2):
+                copy_out(0, 1, oh, on_v)
+            store(0, 1)
+            y[2] = wide(0)
+            r_transposes(2)
+            products(1)
+            fins(2)
+            for c in range(2, NC - 2):
+                for i in range(2):
+                    rsqrt(c + 2, i)
+                if c == 2:
+                    load_den(7)
+                square_s(c + 2, 0, 2)
+                square_s(c + 2, 2, 4)
+                ratio(c + 1, 3, 4, nc.vector)
+                y_quant(c)
+                ratio(c + 2, 0, 3 if c + 3 < NC else 2, nc.gpsimd, words(y[c]))
+                r_transposes(c + 1)
+                y[c + 1] = wide((2, 1, 0)[c - 2]) if c + 3 < NC else narrow(0)
+                late = c + 3 == NC
+                for i in range(2):
+                    for oh in range(2):
+                        copy_out(c - 1, i, oh, on_s if late or (i, oh) == (1, 1) else on_v)
+                        m2(c, i, oh, sum_bank())
+                    store(c - 1, i)
+                    for G in range(2):
+                        fin(c + 1, i, G)
+                if c in (2, 3):
+                    load_num(c + 4)
             a, b = NC - 2, NC - 1
-            y_quant(a, 0, 2)
-            ratio(b, 1, nc.vector, w[b, 1])
+            y[b] = narrow(1)
+            copies(a - 1, [on_s] * 4)
+            y_quant(a)
+            ratio(b, 2, 4, nc.vector)
             for i in range(2):
                 for G in range(2):
-                    r_transpose(b, G, i)
-                    fin(b, G, i)
+                    r_transpose(b, i, G, 2 * i + G)
                 for oh in range(2):
-                    stage2(a, i, oh, on_s)
+                    m2(a, i, oh, sum_bank())
+                    copy_out(a, i, oh, on_s)
                 store(a, i)
+                for G in range(2):
+                    fin(b, i, G)
                 y_quant(b, i, i + 1)
-            for i in range(2):
-                for oh in range(2):
-                    stage2(b, i, oh, (on_s, on_v)[oh])
-                    if i == 1:
-                        store_half(b, i, oh)
-                if i == 0:
-                    store(b, 0)
+            for i, oh in pairs:
+                m2(b, i, oh, sum_bank())
+                copy_out(b, i, oh, (on_s, on_v)[oh])
+                store(b, i, 512 * oh, 512 * (oh + 1))

@@ -389,9 +389,9 @@ def tile_aftfull_pb_kernel(tc, q_bytes, q_scale, num, den, Wq, Wo, out):
             wq_quant(0, 1)
             widen(2)
             wq_quant(1, 0)
-            widen(3)
             wq_quant(1, 1)
             square_g(1, 0, 3, words(staged["q", 1, 1]))
+            widen(3)
             load_num(0)
             load_q(4)
             load_q(5)
@@ -423,9 +423,9 @@ def tile_aftfull_pb_kernel(tc, q_bytes, q_scale, num, den, Wq, Wo, out):
                 b, n = a + 1, a // 2 - 1
                 widen(a + 2)
                 q_quant(a)
-                widen(b + 2)
                 q_quant(b)
                 ratio(n, 0, 4, nc.gpsimd, words(qt[b]))
+                widen(b + 2)
                 if a == 2:
                     load_q(6)
                     load_q(7)
@@ -450,7 +450,7 @@ def tile_aftfull_pb_kernel(tc, q_bytes, q_scale, num, den, Wq, Wo, out):
             q_quant(7)
             for oh, g in pairs:
                 wo_quant(oh, g)
-            ratio(2, 0, 2, nc.gpsimd, words(staged["o", 1, 1]))
+            ratio(2, 0, 2, nc.gpsimd, words(staged["o", 1, 0]))
             r_transposes(0)
             square_s(3, 0, 2)
             gates(6)
@@ -467,50 +467,49 @@ def tile_aftfull_pb_kernel(tc, q_bytes, q_scale, num, den, Wq, Wo, out):
             fins(1)
             copy_out(0, 0, 0, on_v)
             y_quant(1)
-            ratio(3, 0, 3, nc.gpsimd, words(y[1]))
+            ratio(3, 1, 4, nc.gpsimd, words(y[1]))
+            ratio(3, 0, 1, nc.vector)
             copy_out(0, 0, 1, on_v)
             store(0, 0)
-            for oh in range(2):
-                copy_out(0, 1, oh, on_v)
-            store(0, 1)
+            copy_out(0, 1, 0, on_v)
             y[2] = wide(0)
             r_transposes(2)
-            products(1)
             fins(2)
+            copy_out(0, 1, 1, on_v)
+            store(0, 1)
+            products(1)
             for c in range(2, NC - 2):
-                for i in range(2):
-                    rsqrt(c + 2, i)
+                last = c + 3 == NC
+                roots(c + 2)
                 if c == 2:
                     load_den(7)
-                square_s(c + 2, 0, 2)
-                square_s(c + 2, 2, 4)
-                ratio(c + 1, 3, 4, nc.vector)
                 y_quant(c)
-                ratio(c + 2, 0, 3 if c + 3 < NC else 2, nc.gpsimd, words(y[c]))
+                share = 2 if last else 1
+                ratio(c + 2, share, 4, nc.gpsimd, words(y[c]))
+                ratio(c + 2, 0, share, nc.vector)
                 r_transposes(c + 1)
-                y[c + 1] = wide((2, 1, 0)[c - 2]) if c + 3 < NC else narrow(0)
-                late = c + 3 == NC
-                for i in range(2):
-                    for oh in range(2):
-                        copy_out(c - 1, i, oh, on_s if late or (i, oh) == (1, 1) else on_v)
-                        m2(c, i, oh, sum_bank())
-                    store(c - 1, i)
-                    for G in range(2):
-                        fin(c + 1, i, G)
+                y[c + 1] = narrow(0) if last else wide((2, 1, 0)[c - 2])
+                for oh in range(2):
+                    copy_out(c - 1, 0, oh, on_s if last else on_v)
+                    m2(c, 0, oh, sum_bank())
+                store(c - 1, 0)
+                fins(c + 1)
+                for oh in range(2):
+                    copy_out(c - 1, 1, oh, on_s if last or oh == 0 else on_v)
+                    m2(c, 1, oh, sum_bank())
+                store(c - 1, 1)
                 if c in (2, 3):
                     load_num(c + 4)
             a, b = NC - 2, NC - 1
-            y[b] = narrow(1)
+            y[b] = narrow(4)
             copies(a - 1, [on_s] * 4)
+            r_transposes(b)
             y_quant(a)
-            ratio(b, 2, 4, nc.vector)
             for i in range(2):
-                for G in range(2):
-                    r_transpose(b, i, G, 2 * i + G)
                 for oh in range(2):
                     m2(a, i, oh, sum_bank())
                     copy_out(a, i, oh, on_s)
-                store(a, i)
+                    store(a, i, 512 * oh, 512 * (oh + 1))
                 for G in range(2):
                     fin(b, i, G)
                 y_quant(b, i, i + 1)

@@ -18,7 +18,6 @@ CH = 256
 NC = T // CH
 FLOPS = 2 * T * DM * DH + 2 * T * DH * DO
 GROUP = 512
-EARLY = 3
 
 
 def tile_aftfull_pb_kernel(tc, q_bytes, q_scale, num, den, Wq, Wo, out):
@@ -42,7 +41,7 @@ def tile_aftfull_pb_kernel(tc, q_bytes, q_scale, num, den, Wq, Wo, out):
 
         raw, banks, staged, wq_c, wo_c = {}, {}, {}, {}, {}
         qb, qx, qt, qc = {}, {}, {}, {}
-        unsorted, w2 = set(), {}
+        w2 = {}
         dent, numt, w, rr, s, y, yc, o = {}, {}, {}, {}, {}, {}, {}, {}
 
         def bank_tile(shape, k):
@@ -51,8 +50,8 @@ def tile_aftfull_pb_kernel(tc, q_bytes, q_scale, num, den, Wq, Wo, out):
         def wide(slot):
             return sb.tile([P, 4096], BF16, name="wide", tag=f"wide{slot}", bufs=1, align_bytes=64)
 
-        def narrow(slot):
-            return sb.tile([P, 2048], BF16, name="narrow", tag=f"narrow{slot}", bufs=1, align_bytes=64)
+        def halves(tile):
+            return tile[:, 0:2048], tile[:, 2048:4096]
 
         def words(tile):
             return tile[:].bitcast(F32)
@@ -80,7 +79,7 @@ def tile_aftfull_pb_kernel(tc, q_bytes, q_scale, num, den, Wq, Wo, out):
             dent[c, i] = half[:]
 
         def load_den(c):
-            both = sb.tile([P, 2 * DH], BF16, name="den_both", tag="den_both", bufs=3)
+            both = sb.tile([P, 2 * DH], BF16, name="den_both", tag="den_both", bufs=2)
             nc.sync.dma_start(out=both[:], in_=den_v[c].rearrange("p i d -> p (i d)"))
             for i in range(2):
                 dent[c, i] = both[:, DH * i : DH * (i + 1)]
@@ -99,19 +98,19 @@ def tile_aftfull_pb_kernel(tc, q_bytes, q_scale, num, den, Wq, Wo, out):
             banks["wq", G, t] = bank
 
         def wq_copy(G, t, eng):
-            u, e = divmod(t, 2)
-            dst = staged["q", G, u][:, 1024 * e : 1024 * (e + 1)].bitcast(F32)
+            dst = staged["q", G][:, 1024 * t : 1024 * (t + 1)].bitcast(F32)
             eng(out=dst.rearrange("p (g m u) -> p g m u", g=2, u=2), in_=banks["wq", G, t][:].rearrange("p g u m -> p g m u"))
 
-        def wq_quant(G, u):
-            codes = sb.tile([P, 2, 2, P], U32, name=f"wqc{G}{u}", align_bytes=64)
-            scales = sb.tile([P, 2, 2, P], U8, name=f"wqs{G}{u}", align_bytes=64)
+        def wq_quant(G):
+            codes = sb.tile([P, 2, 2, 2, P], U32, name=f"wqc{G}", align_bytes=64)
+            scales = sb.tile([P, 2, 2, 2, P], U8, name=f"wqs{G}", align_bytes=64)
             nc.vector.quantize_mx(
-                out=codes[:].rearrange("p e g m -> p (e g m)").bitcast(FP8X4),
-                scales=scales[:].rearrange("p e g m -> p (e g m)"),
-                in_=staged["q", G, u][:, 0:2048],
+                out=codes[:].rearrange("p u e g m -> p (u e g m)").bitcast(FP8X4),
+                scales=scales[:].rearrange("p u e g m -> p (u e g m)"),
+                in_=staged["q", G][:],
             )
-            wq_c[G, u] = (codes, scales)
+            for u in range(2):
+                wq_c[G, u] = (codes[:, u], scales[:, u])
 
         def wo_transpose(oh, g, h, k):
             bank = bank_tile([P, 2, 2, P], k)
@@ -123,14 +122,15 @@ def tile_aftfull_pb_kernel(tc, q_bytes, q_scale, num, den, Wq, Wo, out):
             banks["wo", oh, g, h] = bank
 
         def wo_copy(oh, g, h, eng):
-            dst = staged["o", oh, g][:, 0:2048].bitcast(F32).rearrange("p (m h x) -> p m h x", h=2, x=4)
+            dst = staged["o", oh][:, 2048 * g : 2048 * (g + 1)].bitcast(F32).rearrange("p (m h x) -> p m h x", h=2, x=4)
             eng(out=dst[:, :, h, :], in_=banks["wo", oh, g, h][:].rearrange("p j u m -> p m (j u)"))
 
-        def wo_quant(oh, g):
-            codes = sb.tile([P, 512], U32, name=f"woc{oh}{g}", align_bytes=64)
-            scales = sb.tile([P, 512], U8, name=f"wos{oh}{g}", align_bytes=64)
-            nc.vector.quantize_mx(out=codes[:].bitcast(FP8X4), scales=scales[:], in_=staged["o", oh, g][:, 0:2048])
-            wo_c[oh, g] = (codes, scales)
+        def wo_quant(oh):
+            codes = sb.tile([P, 1024], U32, name=f"woc{oh}", align_bytes=64)
+            scales = sb.tile([P, 1024], U8, name=f"wos{oh}", align_bytes=64)
+            nc.vector.quantize_mx(out=codes[:].bitcast(FP8X4), scales=scales[:], in_=staged["o", oh][:])
+            for g in range(2):
+                wo_c[oh, g] = (codes[:, 512 * g : 512 * (g + 1)], scales[:, 512 * g : 512 * (g + 1)])
 
         def widen(c):
             qx[c] = sb.tile([P, 2 * DM], BF16, name="qx", tag="qx", bufs=2)
@@ -142,22 +142,13 @@ def tile_aftfull_pb_kernel(tc, q_bytes, q_scale, num, den, Wq, Wo, out):
                 op0=ALU.mult,
             )
 
-        def widen_s(c):
-            qx[c] = sb.tile([P, 2 * DM], BF16, name="qx", tag="qx", bufs=2)
-            nc.scalar.copy(out=qx[c][:], in_=qb[c][:].bitcast(FP8))
-            unsorted.add(c)
-
         def q_transpose(c, g, k):
             src = words(qx[c])
             bank = bank_tile([P, 2, 2, P], k)
             for i in range(2):
                 for u in range(2):
-                    if c in unsorted:
-                        s0 = 512 * i + 256 * g
-                        cols = slice(s0 + u, s0 + 256, 2)
-                    else:
-                        s0 = 512 * u + 256 * i + P * g
-                        cols = slice(s0, s0 + P)
+                    s0 = 512 * u + 256 * i + P * g
+                    cols = slice(s0, s0 + P)
                     nc.tensor.transpose(bank[:, u, i, :], src[:, cols], ident[:])
             banks["x", c, g] = bank
 
@@ -170,13 +161,20 @@ def tile_aftfull_pb_kernel(tc, q_bytes, q_scale, num, den, Wq, Wo, out):
             )
 
         def code_tiles():
-            codes = sb.tile([P, 512], U32, name="codes", tag="codes", bufs=3, align_bytes=64)
-            scales = sb.tile([P, 512], U8, name="scales", tag="scales", bufs=3, align_bytes=64)
+            codes = sb.tile([P, 512], U32, name="codes", tag="codes", bufs=2, align_bytes=64)
+            scales = sb.tile([P, 512], U8, name="scales", tag="scales", bufs=2, align_bytes=64)
             return codes, scales
 
-        def q_quant(c):
-            qc[c] = code_tiles()
-            nc.vector.quantize_mx(out=qc[c][0][:].bitcast(FP8X4), scales=qc[c][1][:], in_=qt[c][:, 0:2048])
+        def q_quant(a, src, n):
+            if a % 2 == 0:
+                codes = sb.tile([P, 1024], U32, name="qcodes", tag="qcodes", bufs=2, align_bytes=64)
+                scales = sb.tile([P, 1024], U8, name="qscales", tag="qscales", bufs=2, align_bytes=64)
+                for j in range(2):
+                    qc[a + j] = (codes[:, 512 * j : 512 * (j + 1)], scales[:, 512 * j : 512 * (j + 1)])
+                qc["pair"] = (codes, scales)
+            codes, scales = qc["pair"]
+            cols = slice(512 * (a % 2), 512 * (a % 2 + n))
+            nc.vector.quantize_mx(out=codes[:, cols].bitcast(FP8X4), scales=scales[:, cols], in_=src)
 
         def rsqrt(c, i):
             if i == 0:
@@ -189,22 +187,23 @@ def tile_aftfull_pb_kernel(tc, q_bytes, q_scale, num, den, Wq, Wo, out):
 
         def square_s(c, lo, hi):
             cols = slice(GROUP * lo, GROUP * hi)
-            nc.scalar.activation(out=w2.setdefault(c, w[c])[:, cols], in_=w[c][:, cols], func=ACT.Square)
+            nc.scalar.activation(out=w[c][:, cols], in_=w[c][:, cols], func=ACT.Square)
+            w2[c, lo] = w[c][:, cols]
 
         def square_g(c, lo, hi, dst=None):
             src = w[c][:, GROUP * lo : GROUP * hi]
-            w2[c] = w[c] if dst is None else dst
-            nc.gpsimd.tensor_tensor(out=w2[c][:, GROUP * lo : GROUP * hi], in0=src, in1=src, op=ALU.mult)
+            w2[c, lo] = src if dst is None else dst[:, GROUP * lo : GROUP * hi]
+            nc.gpsimd.tensor_tensor(out=w2[c, lo], in0=src, in1=src, op=ALU.mult)
 
-        def ratio(c, lo, hi, eng, dst=None):
+        def ratio(c, lo, hi, eng, src, dst=None):
             cols = slice(GROUP * lo, GROUP * hi)
-            dst = w2[c][:, cols] if dst is None else dst[:, 0 : GROUP * (hi - lo)]
+            dst = src[:, cols] if dst is None else dst[:, 0 : GROUP * (hi - lo)]
             for x in range(lo, hi):
                 rr[c, x] = dst[:, GROUP * (x - lo) : GROUP * (x - lo + 1)]
             eng.tensor_tensor(
                 out=dst.rearrange("p (x t m) -> p x t m", t=4, m=P),
                 in0=numt[c][:, cols].rearrange("p (x m t) -> p x t m", t=4, m=P),
-                in1=w2[c][:, cols].rearrange("p (x t m) -> p x t m", t=4, m=P),
+                in1=src[:, cols].rearrange("p (x t m) -> p x t m", t=4, m=P),
                 op=ALU.mult,
             )
 
@@ -226,7 +225,7 @@ def tile_aftfull_pb_kernel(tc, q_bytes, q_scale, num, den, Wq, Wo, out):
             banks["m1", c, G, u] = bank
 
         def page():
-            return sb.tile([P, 1024], F32, name="page", tag="page", bufs=18)
+            return sb.tile([P, 1024], F32, name="page", tag="page", bufs=16)
 
         def sig(c, G, u):
             if u == 0:
@@ -267,8 +266,8 @@ def tile_aftfull_pb_kernel(tc, q_bytes, q_scale, num, den, Wq, Wo, out):
                     out=bank[:],
                     lhsT=codes[:, s0 : s0 + P].bitcast(FP8X4),
                     lhsT_scale=scales[:, s0 : s0 + P],
-                    rhs=wo_c[oh, G][0][:].bitcast(FP8X4),
-                    rhs_scale=wo_c[oh, G][1][:],
+                    rhs=wo_c[oh, G][0].bitcast(FP8X4),
+                    rhs_scale=wo_c[oh, G][1],
                     start=(G == 0),
                     stop=(G == 1),
                 )
@@ -285,36 +284,43 @@ def tile_aftfull_pb_kernel(tc, q_bytes, q_scale, num, den, Wq, Wo, out):
         on_v, on_s = nc.vector.tensor_copy, nc.scalar.copy
         pairs = [(a, b) for a in range(2) for b in range(2)]
 
+        turned, summed = [0, 1, 2, 3], [4, 5, 6, 7]
+
+        def next_bank(ring):
+            ring.append(ring.pop(0))
+            return ring[-1]
+
         def q_transposes(c):
             for g in range(2):
-                q_transpose(c, g, 2 * (c % 2) + g)
+                q_transpose(c, g, next_bank(turned))
 
         def q_scales(c):
             for g in range(2):
                 q_scale_up(c, g)
 
-        def r_transposes(c):
-            for i, G in pairs:
-                r_transpose(c, i, G, 2 * i + G)
+        def r_transposes(c, tiles=(0, 1)):
+            for i in tiles:
+                for G in range(2):
+                    r_transpose(c, i, G, next_bank(turned))
 
-        def fins(c):
-            for i, G in pairs:
-                fin(c, i, G)
+        def r_turn(c, x):
+            r_transpose(c, x // 2, x % 2, next_bank(turned))
+
+        def fins(c, tiles=(0, 1)):
+            for i in tiles:
+                for G in range(2):
+                    fin(c, i, G)
 
         def roots(c):
             for i in range(2):
                 rsqrt(c, i)
+
+        def squares(c):
             for i in range(2):
                 square_s(c, 2 * i, 2 * i + 2)
 
-        ring = [4, 5, 6, 7]
-
-        def sum_bank():
-            ring.append(ring.pop(0))
-            return ring[-1]
-
         def gate(c, G, u):
-            m1(c, G, u, sum_bank())
+            m1(c, G, u, next_bank(summed))
             sig(c, G, u)
 
         def gates(c):
@@ -323,25 +329,29 @@ def tile_aftfull_pb_kernel(tc, q_bytes, q_scale, num, den, Wq, Wo, out):
 
         wo_units = [(oh, g, h) for oh in range(2) for g, h in pairs]
 
-        def wo_turn(unit):
-            wo_transpose(*wo_units[unit], sum_bank())
+        def wq_unit(G, t, eng, ring):
+            wq_transpose(G, t, next_bank(ring))
+            wq_copy(G, t, eng)
+
+        def wo_unit(unit, eng, ring):
+            wo_transpose(*wo_units[unit], next_bank(ring))
+            wo_copy(*wo_units[unit], eng)
+
+        def wo_turn(unit, ring):
+            wo_transpose(*wo_units[unit], next_bank(ring))
 
         def wo_move(unit, eng):
             wo_copy(*wo_units[unit], eng)
 
-        def wo_unit(unit):
-            wo_turn(unit)
-            wo_move(unit, on_s)
+        def product(c, i, oh):
+            m2(c, i, oh, next_bank(summed))
 
-        def products(c):
-            for i, oh in pairs:
-                m2(c, i, oh, sum_bank())
-
-        def copies(c, engs):
-            for (i, oh), eng in zip(pairs, engs):
-                copy_out(c, i, oh, eng)
-                if oh == 1:
-                    store(c, i)
+        def result(c, i, oh, eng):
+            copy_out(c, i, oh, eng)
+            if c >= 3:
+                store(c, i, 512 * oh, 512 * (oh + 1))
+            elif oh == 1:
+                store(c, i)
 
         with tc.manual_schedule():
             load_q(0)
@@ -359,72 +369,71 @@ def tile_aftfull_pb_kernel(tc, q_bytes, q_scale, num, den, Wq, Wo, out):
             load_q(2)
             load_den(3)
             load_q(3)
+            load_num(0)
             load_wo(0, 0)
             load_wo(0, 1)
             widen(0)
             widen(1)
+            pair = wide(0)
+            qt[0], qt[1] = halves(pair)
+            staged["q", 0], staged["q", 1] = wide(1), wide(2)
             for i in range(2):
                 rsqrt(0, i)
                 square_g(0, 2 * i, 2 * i + 2)
-            rsqrt(1, 0)
-            rsqrt(1, 1)
-            qt[0], qt[1] = narrow(0), narrow(1)
+            roots(1)
             for c in range(2):
                 q_transposes(c)
                 q_scales(c)
-            staged["q", 0, 0], staged["q", 0, 1], staged["q", 1, 0], staged["q", 1, 1] = narrow(2), narrow(3), wide(1), wide(0)
-            for t, k in enumerate((4, 5, 0, 1)):
-                wq_transpose(0, t, k)
-                wq_copy(0, t, on_s if t < 2 else on_v)
-            rsqrt(2, 0)
-            rsqrt(2, 1)
-            for t, k in enumerate((2, 3, 6, 7)):
-                wq_transpose(1, t, k)
-                wq_copy(1, t, on_s)
-            rsqrt(3, 0)
-            rsqrt(3, 1)
-            q_quant(0)
-            wq_quant(0, 0)
-            q_quant(1)
-            wq_quant(0, 1)
+            wq_unit(0, 0, on_s, summed)
+            wq_unit(0, 1, on_s, summed)
+            wq_unit(0, 2, on_v, turned)
+            wq_unit(0, 3, on_v, turned)
+            roots(2)
+            wq_unit(1, 0, on_s, turned)
+            wq_unit(1, 1, on_s, turned)
+            wq_unit(1, 2, on_s, summed)
+            wq_unit(1, 3, on_s, summed)
+            roots(3)
+            q_quant(0, pair[:], 2)
+            wq_quant(0)
             widen(2)
-            wq_quant(1, 0)
-            wq_quant(1, 1)
-            square_g(1, 0, 3, words(staged["q", 1, 1]))
+            wq_quant(1)
+            ratio(0, 0, 4, nc.gpsimd, w[0], words(staged["q", 1]))
             widen(3)
-            load_num(0)
             load_q(4)
             load_q(5)
             load_wo(1, 0)
             load_wo(1, 1)
             load_num(1)
+            pair = wide(0)
+            qt[2], qt[3] = halves(pair)
             for u in range(2):
                 for c in range(2):
-                    m1(c, 0, u, sum_bank())
+                    m1(c, 0, u, next_bank(summed))
                 q_transposes(2 + u)
-            qt[2], qt[3] = narrow(0), wide(1)
+            staged["o", 0], staged["o", 1] = wide(4), wide(5)
             q_scales(2)
-            q_scales(3)
-            for c in range(2):
-                m1(c, 1, 0, c)
             for u in range(2):
                 for c in range(2):
                     sig(c, 0, u)
-            for c in range(2):
-                sig(c, 1, 0)
-            for c in range(2):
-                gate(c, 1, 1)
-            staged["o", 0, 0], staged["o", 0, 1] = narrow(2), narrow(3)
-            staged["o", 1, 0], staged["o", 1, 1] = narrow(1), narrow(4)
-            for unit in range(2):
-                wo_unit(unit)
-            square_s(1, 3, 4)
+            gate(0, 1, 0)
+            wo_unit(0, on_s, summed)
+            q_scales(3)
+            gate(1, 1, 0)
+            wo_unit(1, on_s, summed)
+            wo_unit(2, on_s, summed)
+            gate(0, 1, 1)
+            square_s(1, 0, 2)
+            held = (1, 1, 1)
             for a in (2, 4):
                 b, n = a + 1, a // 2 - 1
                 widen(a + 2)
-                q_quant(a)
-                q_quant(b)
-                ratio(n, 0, 4, nc.gpsimd, words(qt[b]))
+                q_quant(a, pair[:], 2)
+                if a == 2:
+                    square_g(2, 0, 4, words(pair))
+                    sq2 = words(pair)
+                else:
+                    ratio(1, 0, 4, nc.gpsimd, w[1], words(pair))
                 widen(b + 2)
                 if a == 2:
                     load_q(6)
@@ -432,88 +441,129 @@ def tile_aftfull_pb_kernel(tc, q_bytes, q_scale, num, den, Wq, Wo, out):
                     load_num(2)
                     load_den(4)
                     load_den(5)
-                    load_den(6)
-                load_num(3 + n)
                 q_transposes(a + 2)
-                gates(a)
+                gate(*held)
+                for G, u in pairs[:3]:
+                    gate(a, G, u)
                 q_transposes(b + 2)
-                qt[a + 2], qt[b + 2] = narrow(0), wide(2) if a == 2 else w[1].bitcast(BF16)
+                pair = wide(1 if a == 2 else 3)
+                qt[a + 2], qt[b + 2] = halves(pair)
                 q_scales(a + 2)
-                wo_transpose(*wo_units[2 + 3 * n], 0)
                 q_scales(b + 2)
-                wo_move(2 + 3 * n, on_v)
-                square_s(2, 2 * n, 2 * n + 2)
-                gates(b)
-                wo_unit(3 + 3 * n)
-                wo_unit(4 + 3 * n)
-            q_quant(6)
-            q_quant(7)
-            for oh, g in pairs:
-                wo_quant(oh, g)
-            ratio(2, 0, 2, nc.gpsimd, words(staged["o", 1, 0]))
-            r_transposes(0)
-            square_s(3, 0, 2)
-            gates(6)
-            y[0] = narrow(2)
+                if a == 2:
+                    gate(a, 1, 1)
+                    wo_unit(3, on_s, summed)
+                    square_s(1, 2, 4)
+                    gate(b, 0, 0)
+                    wo_unit(4, on_s, summed)
+                    gate(b, 0, 1)
+                    wo_unit(5, on_s, summed)
+                    gate(b, 1, 0)
+                    held = (b, 1, 1)
+                else:
+                    wo_unit(6, on_s, summed)
+                    gate(a, 1, 1)
+                    square_s(3, 0, 2)
+                    gate(b, 0, 0)
+                    gate(b, 0, 1)
+                    wo_unit(7, on_s, summed)
+                    r_transposes(0, (0,))
+                    gate(b, 1, 0)
+                    gate(b, 1, 1)
+            load_num(3)
+            q_quant(6, pair[:], 2)
+            ratio(2, 0, 2, nc.gpsimd, sq2, words(pair))
+            wo_quant(0)
+            r_transposes(0, (1,))
+            y[0] = wide(4)
             fins(0)
-            y_quant(0)
-            ratio(2, 2, 4, nc.gpsimd, words(y[0]))
-            load_num(5)
-            y[1] = wide(1)
-            r_transposes(1)
             square_s(3, 2, 4)
+            gates(6)
             gates(7)
-            products(0)
+            wo_quant(1)
+            y_quant(0)
+            ratio(2, 2, 4, nc.gpsimd, sq2, words(y[0]))
+            ratio(3, 0, 1, nc.vector, w[3])
+            load_num(4)
+            y[1] = wide(2)
+            r_transposes(1, (0,))
+            product(0, 0, 0)
+            r_transposes(1, (1,))
             fins(1)
-            copy_out(0, 0, 0, on_v)
-            y_quant(1)
-            ratio(3, 1, 4, nc.gpsimd, words(y[1]))
-            ratio(3, 0, 1, nc.vector)
-            copy_out(0, 0, 1, on_v)
-            store(0, 0)
-            copy_out(0, 1, 0, on_v)
-            y[2] = wide(0)
-            r_transposes(2)
-            fins(2)
-            copy_out(0, 1, 1, on_v)
-            store(0, 1)
-            products(1)
-            for c in range(2, NC - 2):
-                last = c + 3 == NC
-                roots(c + 2)
-                if c == 2:
-                    load_den(7)
+            product(0, 0, 1)
+            product(0, 1, 0)
+            product(0, 1, 1)
+            result(0, 0, 0, on_v)
+            roots(4)
+            load_den(6)
+            r_turn(2, 0)
+            for c in range(1, NC - 3):
+                last = c + 4 == NC
                 y_quant(c)
                 share = 2 if last else 1
-                ratio(c + 2, share, 4, nc.gpsimd, words(y[c]))
-                ratio(c + 2, 0, share, nc.vector)
-                r_transposes(c + 1)
-                y[c + 1] = narrow(0) if last else wide((2, 1, 0)[c - 2])
-                for oh in range(2):
-                    copy_out(c - 1, 0, oh, on_s if last else on_v)
-                    m2(c, 0, oh, sum_bank())
-                store(c - 1, 0)
-                fins(c + 1)
-                for oh in range(2):
-                    copy_out(c - 1, 1, oh, on_s if last or oh == 0 else on_v)
-                    m2(c, 1, oh, sum_bank())
-                store(c - 1, 1)
-                if c in (2, 3):
+                ratio(c + 2, share, 4, nc.gpsimd, w[c + 2], words(y[c]))
+                if c > 1:
+                    ratio(c + 2, 0, share, nc.vector, w[c + 2])
+                if c < 4:
                     load_num(c + 4)
-            a, b = NC - 2, NC - 1
-            y[b] = narrow(4)
-            copies(a - 1, [on_s] * 4)
-            r_transposes(b)
-            y_quant(a)
-            for i in range(2):
-                for oh in range(2):
-                    m2(a, i, oh, sum_bank())
-                    copy_out(a, i, oh, on_s)
-                    store(a, i, 512 * oh, 512 * (oh + 1))
-                for G in range(2):
-                    fin(b, i, G)
-                y_quant(b, i, i + 1)
+                if c == 2:
+                    load_den(7)
+                y[c + 1] = wide((5, 1, 0, 3)[c - 1])
+                if c == 1:
+                    result(0, 0, 1, on_v)
+                if last:
+                    result(c - 1, 1, 0, on_s)
+                    roots(7)
+                r_turn(c + 1, 1)
+                product(c, 0, 0)
+                fins(c + 1, (0,))
+                r_transposes(c + 1, (1,))
+                product(c, 0, 1)
+                if not last:
+                    result(c - 1, 1, 0, on_v)
+                product(c, 1, 0)
+                r_turn(c + 2, 0)
+                if last:
+                    r_turn(c + 2, 1)
+                fins(c + 1, (1,))
+                result(c - 1, 1, 1, on_v)
+                if last:
+                    r_transposes(c + 2, (1,))
+                product(c, 1, 1)
+                square_s(c + 3, 0, 2)
+                result(c, 0, 0, on_s)
+                if not last:
+                    square_s(c + 3, 2, 4)
+                result(c, 0, 1, on_s)
+                if c + 5 < NC:
+                    roots(c + 4)
+            y_quant(5)
+            ratio(7, 0, 2, nc.gpsimd, w[7], words(y[5]))
+            y[6], y[7] = wide(4), wide(2)
+            product(5, 0, 0)
+            product(5, 0, 1)
+            fins(6, (0,))
+            result(4, 1, 0, on_v)
+            fins(6, (1,))
+            result(4, 1, 1, on_s)
+            square_s(7, 2, 4)
+            product(5, 1, 0)
+            product(5, 1, 1)
+            r_transposes(7, (0,))
+            y_quant(6)
+            ratio(7, 2, 4, nc.vector, w[7])
             for i, oh in pairs:
-                m2(b, i, oh, sum_bank())
-                copy_out(b, i, oh, (on_s, on_v)[oh])
-                store(b, i, 512 * oh, 512 * (oh + 1))
+                result(5, i, oh, on_s)
+            product(6, 0, 0)
+            product(6, 0, 1)
+            r_transposes(7, (1,))
+            product(6, 1, 0)
+            product(6, 1, 1)
+            for i in range(2):
+                fins(7, (i,))
+                y_quant(7, i, i + 1)
+            for i, oh in pairs:
+                result(6, i, oh, on_s)
+            for i, oh in pairs:
+                product(7, i, oh)
+                result(7, i, oh, (on_v, on_s)[(i + oh) % 2])

@@ -41,7 +41,6 @@ def tile_aftfull_pb_kernel(tc, q_bytes, q_scale, num, den, Wq, Wo, out):
 
         raw, banks, staged, wq_c, wo_c = {}, {}, {}, {}, {}
         qb, qx, qt, qc = {}, {}, {}, {}
-        w2 = {}
         dent, numt, w, rr, s, y, yc, o = {}, {}, {}, {}, {}, {}, {}, {}
 
         def bank_tile(shape, k):
@@ -99,7 +98,10 @@ def tile_aftfull_pb_kernel(tc, q_bytes, q_scale, num, den, Wq, Wo, out):
 
         def wq_copy(G, t, eng):
             dst = staged["q", G][:, 1024 * t : 1024 * (t + 1)].bitcast(F32)
-            eng(out=dst.rearrange("p (g m u) -> p g m u", g=2, u=2), in_=banks["wq", G, t][:].rearrange("p g u m -> p g m u"))
+            eng(
+                out=dst.rearrange("p (g m j u) -> p g m u j", g=2, j=2, u=2),
+                in_=banks["wq", G, t][:].rearrange("p g u (m j) -> p g m u j", j=2),
+            )
 
         def wq_quant(G):
             codes = sb.tile([P, 2, 2, 2, P], U32, name=f"wqc{G}", align_bytes=64)
@@ -123,7 +125,10 @@ def tile_aftfull_pb_kernel(tc, q_bytes, q_scale, num, den, Wq, Wo, out):
 
         def wo_copy(oh, g, h, eng):
             dst = staged["o", oh][:, 2048 * g : 2048 * (g + 1)].bitcast(F32).rearrange("p (m h x) -> p m h x", h=2, x=4)
-            eng(out=dst[:, :, h, :], in_=banks["wo", oh, g, h][:].rearrange("p j u m -> p m (j u)"))
+            eng(
+                out=dst[:, :, h, :].rearrange("p (m r) x -> p m x r", r=2),
+                in_=banks["wo", oh, g, h][:].rearrange("p j u (m r) -> p m (j u) r", r=2),
+            )
 
         def wo_quant(oh):
             codes = sb.tile([P, 1024], U32, name=f"woc{oh}", align_bytes=64)
@@ -176,34 +181,33 @@ def tile_aftfull_pb_kernel(tc, q_bytes, q_scale, num, den, Wq, Wo, out):
             cols = slice(512 * (a % 2), 512 * (a % 2 + n))
             nc.vector.quantize_mx(out=codes[:, cols].bitcast(FP8X4), scales=scales[:, cols], in_=src)
 
+        def by_plane(flat, lo, hi):
+            return flat.rearrange("p (t n) -> p t n", t=4)[:, :, P * lo : P * hi]
+
         def rsqrt(c, i):
             if i == 0:
                 w[c] = sb.tile([P, 2 * DH], F32, name="w", tag="w", bufs=4, align_bytes=64)[:]
             nc.scalar.activation(
-                out=w[c][:, DH * i : DH * (i + 1)].rearrange("p (g t m) -> p g t m", g=2, t=4),
-                in_=dent[c, i].rearrange("p (g m t) -> p g t m", g=2, t=4),
+                out=by_plane(w[c], 2 * i, 2 * i + 2).rearrange("p t (q j) -> p q t j", j=4),
+                in_=dent[c, i].rearrange("p (q j t) -> p q t j", j=4, t=4),
                 func=ACT.Abs_reciprocal_sqrt,
             )
 
         def square_s(c, lo, hi):
-            cols = slice(GROUP * lo, GROUP * hi)
-            nc.scalar.activation(out=w[c][:, cols], in_=w[c][:, cols], func=ACT.Square)
-            w2[c, lo] = w[c][:, cols]
+            nc.scalar.activation(out=by_plane(w[c], lo, hi), in_=by_plane(w[c], lo, hi), func=ACT.Square)
 
         def square_g(c, lo, hi, dst=None):
-            src = w[c][:, GROUP * lo : GROUP * hi]
-            w2[c, lo] = src if dst is None else dst[:, GROUP * lo : GROUP * hi]
-            nc.gpsimd.tensor_tensor(out=w2[c, lo], in0=src, in1=src, op=ALU.mult)
+            src = by_plane(w[c], lo, hi)
+            nc.gpsimd.tensor_tensor(out=src if dst is None else by_plane(dst, lo, hi), in0=src, in1=src, op=ALU.mult)
 
         def ratio(c, lo, hi, eng, src, dst=None):
-            cols = slice(GROUP * lo, GROUP * hi)
-            dst = src[:, cols] if dst is None else dst[:, 0 : GROUP * (hi - lo)]
+            dst = by_plane(src, lo, hi) if dst is None else dst[:, 0 : GROUP * (hi - lo)].rearrange("p (t n) -> p t n", t=4)
             for x in range(lo, hi):
-                rr[c, x] = dst[:, GROUP * (x - lo) : GROUP * (x - lo + 1)]
+                rr[c, x] = dst[:, :, P * (x - lo) : P * (x - lo + 1)]
             eng.tensor_tensor(
-                out=dst.rearrange("p (x t m) -> p x t m", t=4, m=P),
-                in0=numt[c][:, cols].rearrange("p (x m t) -> p x t m", t=4, m=P),
-                in1=src[:, cols].rearrange("p (x t m) -> p x t m", t=4, m=P),
+                out=dst.rearrange("p t (q j) -> p q t j", j=4),
+                in0=numt[c][:, GROUP * lo : GROUP * hi].rearrange("p (q j t) -> p q t j", j=4, t=4),
+                in1=by_plane(src, lo, hi).rearrange("p t (q j) -> p q t j", j=4),
                 op=ALU.mult,
             )
 
@@ -229,21 +233,23 @@ def tile_aftfull_pb_kernel(tc, q_bytes, q_scale, num, den, Wq, Wo, out):
 
         def sig(c, G, u):
             if u == 0:
-                s[c, G] = page()[:].rearrange("p (u n e) -> p u n e", u=2, e=2)
-            nc.scalar.activation(out=s[c, G][:, u, :, :], in_=banks["m1", c, G, u][:].rearrange("p e n -> p n e"), func=ACT.Sigmoid)
+                s[c, G] = page()[:]
+            nc.scalar.activation(
+                out=s[c, G][:, 512 * u : 512 * (u + 1)], in_=banks["m1", c, G, u][:].rearrange("p e n -> p (e n)"), func=ACT.Sigmoid
+            )
 
         def r_transpose(c, i, G, k):
             bank = bank_tile([P, 4, P], k)
             for t in range(4):
-                nc.tensor.transpose(bank[:, t, :], rr[c, 2 * i + G][:, P * t : P * (t + 1)], ident[:])
+                nc.tensor.transpose(bank[:, t, :], rr[c, 2 * i + G][:, t, :], ident[:])
             banks["r", c, i, G] = bank
 
         def fin(c, i, G):
             s0 = 1024 * i + 512 * G
             nc.vector.tensor_tensor(
-                out=y[c][:, s0 : s0 + 512].rearrange("p (n u e) -> p n u e", u=2, e=2),
-                in0=banks["r", c, i, G][:].rearrange("p (u e) n -> p n u e", u=2),
-                in1=s[c, G][:, :, i * P : (i + 1) * P, :].rearrange("p u n e -> p n u e"),
+                out=y[c][:, s0 : s0 + 512].rearrange("p (n j t) -> p n t j", j=2, t=4),
+                in0=banks["r", c, i, G][:].rearrange("p t (n j) -> p n t j", j=2),
+                in1=s[c, G].rearrange("p (t n) -> p t n", t=4)[:, :, i * P : (i + 1) * P].rearrange("p t (n j) -> p n t j", j=2),
                 op=ALU.mult,
             )
 

@@ -263,6 +263,26 @@ def tile_aftfull_pb_kernel(tc, q_bytes, q_scale, num, den, Wq, Wo, out):
                 in_=y[c][:, 1024 * i0 : 1024 * i1],
             )
 
+        def group_quant(c, i, G):
+            codes, scales = yc[c]
+            s0 = 256 * i + P * G
+            nc.vector.quantize_mx(
+                out=codes[:, s0 : s0 + P].bitcast(FP8X4), scales=scales[:, s0 : s0 + P], in_=y[c][:, 4 * s0 : 4 * (s0 + P)]
+            )
+
+        def half_pass(c, i, oh, G, bank):
+            codes, scales = yc[c]
+            s0 = 256 * i + P * G
+            nc.tensor.matmul_mx(
+                out=bank[:],
+                lhsT=codes[:, s0 : s0 + P].bitcast(FP8X4),
+                lhsT_scale=scales[:, s0 : s0 + P],
+                rhs=wo_c[oh, G][0].bitcast(FP8X4),
+                rhs_scale=wo_c[oh, G][1],
+                start=(G == 0),
+                stop=(G == 1),
+            )
+
         def m2(c, i, oh, k):
             bank = bank_tile([P, 512], k)
             codes, scales = yc[c]
@@ -413,26 +433,29 @@ def tile_aftfull_pb_kernel(tc, q_bytes, q_scale, num, den, Wq, Wo, out):
             load_num(1)
             pair = wide(0)
             qt[2], qt[3] = halves(pair)
-            for u in range(2):
-                for c in range(2):
-                    m1(c, 0, u, next_bank(summed))
-                q_transposes(2 + u)
+            m1(0, 0, 0, next_bank(summed))
+            m1(1, 0, 0, next_bank(summed))
+            for c in range(2):
+                q_transposes(2 + c)
+                m1(c, 0, 1, next_bank(summed))
             staged["o", 0], staged["o", 1] = wide(4), wide(5)
             q_scales(2)
             for u in range(2):
                 for c in range(2):
                     sig(c, 0, u)
             gate(0, 1, 0)
-            wo_unit(0, on_s, summed)
+            wo_turn(0, turned)
             q_scales(3)
+            wo_move(0, on_v)
             gate(1, 1, 0)
             wo_unit(1, on_s, summed)
             wo_unit(2, on_s, summed)
             gate(0, 1, 1)
+            wo_unit(3, on_s, summed)
             square_s(1, 0, 2)
             held = (1, 1, 1)
             for a in (2, 4):
-                b, n = a + 1, a // 2 - 1
+                b = a + 1
                 widen(a + 2)
                 q_quant(a, pair[:], 2)
                 if a == 2:
@@ -455,24 +478,26 @@ def tile_aftfull_pb_kernel(tc, q_bytes, q_scale, num, den, Wq, Wo, out):
                 pair = wide(1 if a == 2 else 3)
                 qt[a + 2], qt[b + 2] = halves(pair)
                 q_scales(a + 2)
+                if a == 2:
+                    wo_turn(4, turned)
                 q_scales(b + 2)
                 if a == 2:
-                    gate(a, 1, 1)
-                    wo_unit(3, on_s, summed)
+                    wo_move(4, on_v)
                     square_s(1, 2, 4)
-                    gate(b, 0, 0)
-                    wo_unit(4, on_s, summed)
-                    gate(b, 0, 1)
+                else:
+                    square_s(3, 2, 4)
+                gate(a, 1, 1)
+                gate(b, 0, 0)
+                if a == 2:
                     wo_unit(5, on_s, summed)
+                    wo_unit(6, on_s, summed)
+                    gate(b, 0, 1)
                     gate(b, 1, 0)
+                    wo_unit(7, on_s, summed)
+                    square_s(3, 0, 2)
                     held = (b, 1, 1)
                 else:
-                    wo_unit(6, on_s, summed)
-                    gate(a, 1, 1)
-                    square_s(3, 0, 2)
-                    gate(b, 0, 0)
                     gate(b, 0, 1)
-                    wo_unit(7, on_s, summed)
                     r_transposes(0, (0,))
                     gate(b, 1, 0)
                     gate(b, 1, 1)
@@ -483,7 +508,6 @@ def tile_aftfull_pb_kernel(tc, q_bytes, q_scale, num, den, Wq, Wo, out):
             r_transposes(0, (1,))
             y[0] = wide(4)
             fins(0)
-            square_s(3, 2, 4)
             gates(6)
             gates(7)
             wo_quant(1)
@@ -525,17 +549,17 @@ def tile_aftfull_pb_kernel(tc, q_bytes, q_scale, num, den, Wq, Wo, out):
                 fins(c + 1, (0,))
                 r_transposes(c + 1, (1,))
                 product(c, 0, 1)
-                if not last:
-                    result(c - 1, 1, 0, on_v)
+                result(c - 1, 1, 1 if last else 0, on_v)
                 product(c, 1, 0)
                 r_turn(c + 2, 0)
                 if last:
                     r_turn(c + 2, 1)
                 fins(c + 1, (1,))
-                result(c - 1, 1, 1, on_v)
+                if not last:
+                    result(c - 1, 1, 1, on_v)
+                product(c, 1, 1)
                 if last:
                     r_transposes(c + 2, (1,))
-                product(c, 1, 1)
                 square_s(c + 3, 0, 2)
                 result(c, 0, 0, on_s)
                 if not last:
@@ -565,11 +589,21 @@ def tile_aftfull_pb_kernel(tc, q_bytes, q_scale, num, den, Wq, Wo, out):
             r_transposes(7, (1,))
             product(6, 1, 0)
             product(6, 1, 1)
+            yc[7] = code_tiles()
             for i in range(2):
                 fins(7, (i,))
-                y_quant(7, i, i + 1)
+                for G in range(2):
+                    group_quant(7, i, G)
             for i, oh in pairs:
                 result(6, i, oh, on_s)
-            for i, oh in pairs:
-                product(7, i, oh)
-                result(7, i, oh, (on_v, on_s)[(i + oh) % 2])
+            for oh in range(2):
+                product(7, 0, oh)
+            last = [bank_tile([P, 512], next_bank(summed)) for oh in range(2)]
+            for G in range(2):
+                for oh in range(2):
+                    half_pass(7, 1, oh, G, last[oh])
+            result(7, 0, 0, on_s)
+            result(7, 0, 1, on_v)
+            for oh in range(2):
+                banks["m2", 7, 1, oh] = last[oh]
+                result(7, 1, oh, (on_s, on_v)[oh])

@@ -511,9 +511,8 @@ def tile_aftfull_pb_kernel(tc, q_bytes, q_scale, num, den, Wq, Wo, out):
             gates(6)
             gates(7)
             wo_quant(1)
+            ratio(2, 2, 4, nc.gpsimd, sq2, words(staged["o", 1]))
             y_quant(0)
-            ratio(2, 2, 4, nc.gpsimd, sq2, words(y[0]))
-            ratio(3, 0, 1, nc.vector, w[3])
             load_num(4)
             y[1] = wide(2)
             r_transposes(1, (0,))
@@ -532,13 +531,15 @@ def tile_aftfull_pb_kernel(tc, q_bytes, q_scale, num, den, Wq, Wo, out):
                 y_quant(c)
                 share = 2 if last else 1
                 ratio(c + 2, share, 4, nc.gpsimd, w[c + 2], words(y[c]))
-                if c > 1:
-                    ratio(c + 2, 0, share, nc.vector, w[c + 2])
+                ratio(c + 2, 0, share, nc.vector, w[c + 2])
                 if c < 4:
                     load_num(c + 4)
                 if c == 2:
                     load_den(7)
-                y[c + 1] = wide((5, 1, 0, 3)[c - 1])
+                y[c + 1] = wide((4, 1, 0, 3)[c - 1])
+                if last:
+                    around_y5 = y[5]
+                    y[5] = around_y5[:, 1024:3072]
                 if c == 1:
                     result(0, 0, 1, on_v)
                 if last:
@@ -567,9 +568,10 @@ def tile_aftfull_pb_kernel(tc, q_bytes, q_scale, num, den, Wq, Wo, out):
                 result(c, 0, 1, on_s)
                 if c + 5 < NC:
                     roots(c + 4)
-            y_quant(5)
-            ratio(7, 0, 2, nc.gpsimd, w[7], words(y[5]))
-            y[6], y[7] = wide(4), wide(2)
+            y_quant(5, 0, 1)
+            ratio(7, 0, 2, nc.gpsimd, w[7], words(around_y5))
+            y_quant(5, 1, 2)
+            y[6], y[7] = wide(5), wide(2)
             product(5, 0, 0)
             product(5, 0, 1)
             fins(6, (0,))

from contextlib import ExitStack

import concourse.mybir as mybir
from concourse.masks import make_identity

F32 = mybir.dt.float32
BF16 = mybir.dt.bfloat16
U32 = mybir.dt.uint32
U8 = mybir.dt.uint8
FP8 = mybir.dt.float8_e4m3fn
FP8X4 = mybir.dt.float8_e4m3fn_x4
ACT = mybir.ActivationFunctionType
ALU = mybir.AluOpType

P = 128
T, DM, DH, DO = 2048, 1024, 1024, 1024
CH = 256
NC = T // CH
FLOPS = 2 * T * DM * DH + 2 * T * DH * DO
GROUP = 512


def tile_aftfull_pb_kernel(tc, q_bytes, q_scale, num, den, Wq, Wo, out):
    nc = tc.nc
    with ExitStack() as ctx:
        sb = ctx.enter_context(tc.tile_pool(name="sb", bufs=1))
        ps = ctx.enter_context(tc.psum_pool(name="ps", bufs=1))

        q_v = q_bytes.flatten_outer_dims().rearrange("(c p i) d -> c p i d", p=P, i=2)
        num_v = num.flatten_outer_dims().rearrange("(c p i) d -> c p i d", p=P, i=2)
        den_v = den.flatten_outer_dims().rearrange("(c p i) d -> c p i d", p=P, i=2)
        out_v = out.flatten_outer_dims().rearrange("(c p i) d -> c p i d", p=P, i=2)
        wq_v = Wq.rearrange("(g m u e) k -> g u m e k", m=P, u=2, e=2)
        wo_v = Wo.rearrange("(oh m h j) k -> oh h m j k", m=P, h=2, j=2)

        ident = sb.tile([P, P], F32, name="ident")
        make_identity(nc, ident[:])
        sc = sb.tile([P, 2, 4], F32, name="sc")
        one = sb.tile([P, 1], F32, name="one")
        nc.vector.memset(one[:], 1.0)

        raw, banks, staged, wq_c, wo_c = {}, {}, {}, {}, {}
        qb, qx, qt, qc = {}, {}, {}, {}
        dent, numt, w, rr, s, y, yc, o = {}, {}, {}, {}, {}, {}, {}, {}

        def bank_tile(shape, k):
            return ps.tile(shape, F32, name="bank", tag=f"bank{k}", bufs=1)

        def wide(slot):
            return sb.tile([P, 4096], BF16, name="wide", tag=f"wide{slot}", bufs=1, align_bytes=64)

        def halves(tile):
            return tile[:, 0:2048], tile[:, 2048:4096]

        def words(tile):
            return tile[:].bitcast(F32)

        def load_sc():
            nc.sync.dma_start(out=sc[:], in_=q_scale.rearrange("a b (g p t) -> p (a b g) t", p=P, t=4))

        def load_w(key, src):
            raw[key] = sb.tile([P, 2 * DM], BF16, name="wraw", tag="wraw", bufs=4)
            nc.sync.dma_start(out=raw[key][:], in_=src.rearrange("m j k -> m (j k)"))

        def load_wq(G, u):
            load_w(("q", G, u), wq_v[G][u])

        def load_wo(oh, h):
            load_w(("o", oh, h), wo_v[oh][h])

        def load_q(c):
            qb[c] = sb.tile([P, 2 * DM], U8, name="qb", tag="qb", bufs=3)
            nc.sync.dma_start(out=qb[c][:], in_=q_v[c].rearrange("p i d -> p (i d)"))

        def load_den_half(c, i):
            half = sb.tile([P, DH], BF16, name="den_half", tag="den_half", bufs=4)
            nc.sync.dma_start(out=half[:], in_=den_v[c][:, i, :])
            dent[c, i] = half[:]

        def load_den(c):
            both = sb.tile([P, 2 * DH], BF16, name="den_both", tag="den_both", bufs=2)
            nc.sync.dma_start(out=both[:], in_=den_v[c].rearrange("p i d -> p (i d)"))
            for i in range(2):
                dent[c, i] = both[:, DH * i : DH * (i + 1)]

        def load_num(c):
            numt[c] = sb.tile([P, 2 * DH], BF16, name="numt", tag="numt", bufs=3)
            nc.sync.dma_start(out=numt[c][:], in_=num_v[c].rearrange("p i d -> p (i d)"))

        def wq_transpose(G, t, k):
            src = words(raw["q", G, t // 2])
            bank = bank_tile([P, 2, 2, P], k)
            for g in range(2):
                s0 = 512 * (t % 2) + 256 * g
                for u in range(2):
                    nc.tensor.transpose(bank[:, g, u, :], src[:, s0 + u : s0 + 256 : 2], ident[:])
            banks["wq", G, t] = bank

        def wq_copy(G, t, eng):
            dst = staged["q", G][:, 1024 * t : 1024 * (t + 1)].bitcast(F32)
            eng(
                out=dst.rearrange("p (g m j u) -> p g m u j", g=2, j=2, u=2),
                in_=banks["wq", G, t][:].rearrange("p g u (m j) -> p g m u j", j=2),
            )

        def wq_quant(G):
            codes = sb.tile([P, 2, 2, 2, P], U32, name=f"wqc{G}", align_bytes=64)
            scales = sb.tile([P, 2, 2, 2, P], U8, name=f"wqs{G}", align_bytes=64)
            nc.vector.quantize_mx(
                out=codes[:].rearrange("p u e g m -> p (u e g m)").bitcast(FP8X4),
                scales=scales[:].rearrange("p u e g m -> p (u e g m)"),
                in_=staged["q", G][:],
            )
            for u in range(2):
                wq_c[G, u] = (codes[:, u], scales[:, u])

        def wo_transpose(oh, g, h, k):
            bank = bank_tile([P, 2, 2, P], k)
            src = words(raw["o", oh, h])
            for j in range(2):
                s0 = 512 * j + 256 * g
                for u in range(2):
                    nc.tensor.transpose(bank[:, j, u, :], src[:, s0 + u : s0 + 256 : 2], ident[:])
            banks["wo", oh, g, h] = bank

        def wo_copy(oh, g, h, eng):
            dst = staged["o", oh][:, 2048 * g : 2048 * (g + 1)].bitcast(F32).rearrange("p (m h x) -> p m h x", h=2, x=4)
            eng(
                out=dst[:, :, h, :].rearrange("p (m r) x -> p m x r", r=2),
                in_=banks["wo", oh, g, h][:].rearrange("p j u (m r) -> p m (j u) r", r=2),
            )

        def wo_quant(oh):
            codes = sb.tile([P, 1024], U32, name=f"woc{oh}", align_bytes=64)
            scales = sb.tile([P, 1024], U8, name=f"wos{oh}", align_bytes=64)
            nc.vector.quantize_mx(out=codes[:].bitcast(FP8X4), scales=scales[:], in_=staged["o", oh][:])
            for g in range(2):
                wo_c[oh, g] = (codes[:, 512 * g : 512 * (g + 1)], scales[:, 512 * g : 512 * (g + 1)])

        def widen(c):
            qx[c] = sb.tile([P, 2 * DM], BF16, name="qx", tag="qx", bufs=2)
            nc.vector.tensor_scalar(
                out=qx[c][:].rearrange("p (u x e) -> p x u e", u=2, e=2),
                in0=qb[c][:].bitcast(FP8),
                scalar1=one[:],
                scalar2=None,
                op0=ALU.mult,
            )

        def q_transpose(c, g, k):
            src = words(qx[c])
            bank = bank_tile([P, 2, 2, P], k)
            for i in range(2):
                for u in range(2):
                    s0 = 512 * u + 256 * i + P * g
                    cols = slice(s0, s0 + P)
                    nc.tensor.transpose(bank[:, u, i, :], src[:, cols], ident[:])
            banks["x", c, g] = bank

        def q_scale_up(c, g):
            nc.vector.tensor_tensor(
                out=qt[c][:, 1024 * g : 1024 * (g + 1)].rearrange("p (n u e) -> p n u e", u=2, e=2),
                in0=banks["x", c, g][:].rearrange("p u i n -> p (u i n)").bitcast(BF16).rearrange("p (u n e) -> p n u e", u=2, e=2),
                in1=sc[:, g, :].rearrange("p (u e) -> p u e", u=2).unsqueeze(1).to_broadcast([P, CH, 2, 2]),
                op=ALU.mult,
            )

        def code_tiles():
            codes = sb.tile([P, 512], U32, name="codes", tag="codes", bufs=2, align_bytes=64)
            scales = sb.tile([P, 512], U8, name="scales", tag="scales", bufs=2, align_bytes=64)
            return codes, scales

        def q_quant(a, src, n):
            if a % 2 == 0:
                codes = sb.tile([P, 1024], U32, name="qcodes", tag="qcodes", bufs=2, align_bytes=64)
                scales = sb.tile([P, 1024], U8, name="qscales", tag="qscales", bufs=2, align_bytes=64)
                for j in range(2):
                    qc[a + j] = (codes[:, 512 * j : 512 * (j + 1)], scales[:, 512 * j : 512 * (j + 1)])
                qc["pair"] = (codes, scales)
            codes, scales = qc["pair"]
            cols = slice(512 * (a % 2), 512 * (a % 2 + n))
            nc.vector.quantize_mx(out=codes[:, cols].bitcast(FP8X4), scales=scales[:, cols], in_=src)

        def by_plane(flat, lo, hi):
            return flat.rearrange("p (t n) -> p t n", t=4)[:, :, P * lo : P * hi]

        def rsqrt(c, i):
            if i == 0:
                w[c] = sb.tile([P, 2 * DH], F32, name="w", tag="w", bufs=4, align_bytes=64)[:]
            nc.scalar.activation(
                out=by_plane(w[c], 2 * i, 2 * i + 2).rearrange("p t (q j) -> p q t j", j=4),
                in_=dent[c, i].rearrange("p (q j t) -> p q t j", j=4, t=4),
                func=ACT.Abs_reciprocal_sqrt,
            )

        def square_s(c, lo, hi):
            nc.scalar.activation(out=by_plane(w[c], lo, hi), in_=by_plane(w[c], lo, hi), func=ACT.Square)

        def square_g(c, lo, hi, dst=None):
            src = by_plane(w[c], lo, hi)
            nc.gpsimd.tensor_tensor(out=src if dst is None else by_plane(dst, lo, hi), in0=src, in1=src, op=ALU.mult)

        def ratio(c, lo, hi, eng, src, dst=None):
            dst = by_plane(src, lo, hi) if dst is None else dst[:, 0 : GROUP * (hi - lo)].rearrange("p (t n) -> p t n", t=4)
            for x in range(lo, hi):
                rr[c, x] = dst[:, :, P * (x - lo) : P * (x - lo + 1)]
            eng.tensor_tensor(
                out=dst.rearrange("p t (q j) -> p q t j", j=4),
                in0=numt[c][:, GROUP * lo : GROUP * hi].rearrange("p (q j t) -> p q t j", j=4, t=4),
                in1=by_plane(src, lo, hi).rearrange("p t (q j) -> p q t j", j=4),
                op=ALU.mult,
            )

        def m1(c, G, u, k):
            codes, scales = qc[c]
            wc, ws = wq_c[G, u]
            bank = bank_tile([P, 2, CH], k)
            for e in range(2):
                for g in range(2):
                    nc.tensor.matmul_mx(
                        out=bank[:, e, :],
                        lhsT=wc[:, e, g, :].bitcast(FP8X4),
                        lhsT_scale=ws[:, e, g, :],
                        rhs=codes[:, CH * g : CH * (g + 1)].bitcast(FP8X4),
                        rhs_scale=scales[:, CH * g : CH * (g + 1)],
                        start=(g == 0),
                        stop=(g == 1),
                    )
            banks["m1", c, G, u] = bank

        def page():
            return sb.tile([P, 1024], F32, name="page", tag="page", bufs=16)

        def sig(c, G, u):
            if u == 0:
                s[c, G] = page()[:]
            nc.scalar.activation(
                out=s[c, G][:, 512 * u : 512 * (u + 1)], in_=banks["m1", c, G, u][:].rearrange("p e n -> p (e n)"), func=ACT.Sigmoid
            )

        def r_transpose(c, i, G, k):
            bank = bank_tile([P, 4, P], k)
            for t in range(4):
                nc.tensor.transpose(bank[:, t, :], rr[c, 2 * i + G][:, t, :], ident[:])
            banks["r", c, i, G] = bank

        def fin(c, i, G):
            s0 = 1024 * i + 512 * G
            nc.vector.tensor_tensor(
                out=y[c][:, s0 : s0 + 512].rearrange("p (n j t) -> p n t j", j=2, t=4),
                in0=banks["r", c, i, G][:].rearrange("p t (n j) -> p n t j", j=2),
                in1=s[c, G].rearrange("p (t n) -> p t n", t=4)[:, :, i * P : (i + 1) * P].rearrange("p t (n j) -> p n t j", j=2),
                op=ALU.mult,
            )

        def y_quant(c, i0=0, i1=2):
            if i0 == 0:
                yc[c] = code_tiles()
            codes, scales = yc[c]
            nc.vector.quantize_mx(
                out=codes[:, 256 * i0 : 256 * i1].bitcast(FP8X4),
                scales=scales[:, 256 * i0 : 256 * i1],
                in_=y[c][:, 1024 * i0 : 1024 * i1],
            )

        def group_quant(c, i, G):
            codes, scales = yc[c]
            s0 = 256 * i + P * G
            nc.vector.quantize_mx(
                out=codes[:, s0 : s0 + P].bitcast(FP8X4), scales=scales[:, s0 : s0 + P], in_=y[c][:, 4 * s0 : 4 * (s0 + P)]
            )

        def half_pass(c, i, oh, G, bank):
            codes, scales = yc[c]
            s0 = 256 * i + P * G
            nc.tensor.matmul_mx(
                out=bank[:],
                lhsT=codes[:, s0 : s0 + P].bitcast(FP8X4),
                lhsT_scale=scales[:, s0 : s0 + P],
                rhs=wo_c[oh, G][0].bitcast(FP8X4),
                rhs_scale=wo_c[oh, G][1],
                start=(G == 0),
                stop=(G == 1),
            )

        def m2(c, i, oh, k):
            bank = bank_tile([P, 512], k)
            codes, scales = yc[c]
            for G in range(2):
                s0 = 256 * i + P * G
                nc.tensor.matmul_mx(
                    out=bank[:],
                    lhsT=codes[:, s0 : s0 + P].bitcast(FP8X4),
                    lhsT_scale=scales[:, s0 : s0 + P],
                    rhs=wo_c[oh, G][0].bitcast(FP8X4),
                    rhs_scale=wo_c[oh, G][1],
                    start=(G == 0),
                    stop=(G == 1),
                )
            banks["m2", c, i, oh] = bank

        def copy_out(c, i, oh, eng):
            if (c, i) not in o:
                o[c, i] = page()
            eng(out=o[c, i][:, 512 * oh : 512 * (oh + 1)], in_=banks["m2", c, i, oh][:])

        def store(c, i, lo=0, hi=DO):
            nc.sync.dma_start(out=out_v[c][:, i, lo:hi], in_=o[c, i][:, lo:hi])

        on_v, on_s = nc.vector.tensor_copy, nc.scalar.copy
        pairs = [(a, b) for a in range(2) for b in range(2)]

        turned, summed = [0, 1, 2, 3], [4, 5, 6, 7]

        def next_bank(ring):
            ring.append(ring.pop(0))
            return ring[-1]

        def q_transposes(c):
            for g in range(2):
                q_transpose(c, g, next_bank(turned))

        def q_scales(c):
            for g in range(2):
                q_scale_up(c, g)

        def r_transposes(c, tiles=(0, 1)):
            for i in tiles:
                for G in range(2):
                    r_transpose(c, i, G, next_bank(turned))

        def r_turn(c, x):
            r_transpose(c, x // 2, x % 2, next_bank(turned))

        def fins(c, tiles=(0, 1)):
            for i in tiles:
                for G in range(2):
                    fin(c, i, G)

        def roots(c):
            for i in range(2):
                rsqrt(c, i)

        def squares(c):
            for i in range(2):
                square_s(c, 2 * i, 2 * i + 2)

        def gate(c, G, u):
            m1(c, G, u, next_bank(summed))
            sig(c, G, u)

        def gates(c):
            for G, u in pairs:
                gate(c, G, u)

        wo_units = [(oh, g, h) for oh in range(2) for g, h in pairs]

        def wq_unit(G, t, eng, ring):
            wq_transpose(G, t, next_bank(ring))
            wq_copy(G, t, eng)

        def wo_unit(unit, eng, ring):
            wo_transpose(*wo_units[unit], next_bank(ring))
            wo_copy(*wo_units[unit], eng)

        def wo_turn(unit, ring):
            wo_transpose(*wo_units[unit], next_bank(ring))

        def wo_move(unit, eng):
            wo_copy(*wo_units[unit], eng)

        def product(c, i, oh):
            m2(c, i, oh, next_bank(summed))

        def result(c, i, oh, eng):
            copy_out(c, i, oh, eng)
            if c >= 3:
                store(c, i, 512 * oh, 512 * (oh + 1))
            elif oh == 1:
                store(c, i)

        with tc.manual_schedule():
            load_q(0)
            load_den_half(0, 0)
            load_q(1)
            load_den_half(0, 1)
            load_sc()
            load_den_half(1, 0)
            load_wq(0, 0)
            load_den_half(1, 1)
            load_wq(0, 1)
            load_den(2)
            load_wq(1, 0)
            load_wq(1, 1)
            load_q(2)
            load_den(3)
            load_q(3)
            load_num(0)
            load_wo(0, 0)
            load_wo(0, 1)
            widen(0)
            widen(1)
            pair = wide(0)
            qt[0], qt[1] = halves(pair)
            staged["q", 0], staged["q", 1] = wide(1), wide(2)
            for i in range(2):
                rsqrt(0, i)
                square_g(0, 2 * i, 2 * i + 2)
            roots(1)
            for c in range(2):
                q_transposes(c)
                q_scales(c)
            wq_unit(0, 0, on_s, summed)
            wq_unit(0, 1, on_s, summed)
            wq_unit(0, 2, on_v, turned)
            wq_unit(0, 3, on_v, turned)
            roots(2)
            wq_unit(1, 0, on_s, turned)
            wq_unit(1, 1, on_s, turned)
            wq_unit(1, 2, on_s, summed)
            wq_unit(1, 3, on_s, summed)
            roots(3)
            q_quant(0, pair[:], 2)
            wq_quant(0)
            widen(2)
            wq_quant(1)
            ratio(0, 0, 4, nc.gpsimd, w[0], words(staged["q", 1]))
            widen(3)
            load_q(4)
            load_q(5)
            load_wo(1, 0)
            load_wo(1, 1)
            load_num(1)
            pair = wide(0)
            qt[2], qt[3] = halves(pair)
            m1(0, 0, 0, next_bank(summed))
            m1(1, 0, 0, next_bank(summed))
            for c in range(2):
                q_transposes(2 + c)
                m1(c, 0, 1, next_bank(summed))
            staged["o", 0], staged["o", 1] = wide(4), wide(5)
            q_scales(2)
            for u in range(2):
                for c in range(2):
                    sig(c, 0, u)
            gate(0, 1, 0)
            wo_turn(0, turned)
            q_scales(3)
            wo_move(0, on_v)
            gate(1, 1, 0)
            wo_unit(1, on_s, summed)
            wo_unit(2, on_s, summed)
            gate(0, 1, 1)
            wo_unit(3, on_s, summed)
            square_s(1, 0, 2)
            held = (1, 1, 1)
            for a in (2, 4):
                b = a + 1
                widen(a + 2)
                q_quant(a, pair[:], 2)
                if a == 2:
                    square_g(2, 0, 4, words(pair))
                    sq2 = words(pair)
                else:
                    ratio(1, 0, 4, nc.gpsimd, w[1], words(pair))
                widen(b + 2)
                if a == 2:
                    load_q(6)
                    load_q(7)
                    load_num(2)
                    load_den(4)
                    load_den(5)
                q_transposes(a + 2)
                gate(*held)
                for G, u in pairs[:3]:
                    gate(a, G, u)
                q_transposes(b + 2)
                pair = wide(1 if a == 2 else 3)
                qt[a + 2], qt[b + 2] = halves(pair)
                q_scales(a + 2)
                if a == 2:
                    wo_turn(4, turned)
                q_scales(b + 2)
                if a == 2:
                    wo_move(4, on_v)
                    square_s(1, 2, 4)
                else:
                    square_s(3, 2, 4)
                gate(a, 1, 1)
                gate(b, 0, 0)
                if a == 2:
                    wo_unit(5, on_s, summed)
                    wo_unit(6, on_s, summed)
                    gate(b, 0, 1)
                    gate(b, 1, 0)
                    wo_unit(7, on_s, summed)
                    square_s(3, 0, 2)
                    held = (b, 1, 1)
                else:
                    gate(b, 0, 1)
                    r_transposes(0, (0,))
                    gate(b, 1, 0)
                    gate(b, 1, 1)
            load_num(3)
            q_quant(6, pair[:], 2)
            ratio(2, 0, 2, nc.gpsimd, sq2, words(pair))
            wo_quant(0)
            r_transposes(0, (1,))
            y[0] = wide(4)
            fins(0)
            gates(6)
            gates(7)
            wo_quant(1)
            ratio(2, 2, 4, nc.gpsimd, sq2, words(staged["o", 1]))
            y_quant(0)
            load_num(4)
            y[1] = wide(2)
            r_transposes(1, (0,))
            product(0, 0, 0)
            r_transposes(1, (1,))
            fins(1)
            product(0, 0, 1)
            product(0, 1, 0)
            product(0, 1, 1)
            result(0, 0, 0, on_v)
            roots(4)
            load_den(6)
            r_turn(2, 0)
            for c in range(1, NC - 3):
                last = c + 4 == NC
                y_quant(c)
                share = 2 if last else 1
                ratio(c + 2, share, 4, nc.gpsimd, w[c + 2], words(y[c]))
                ratio(c + 2, 0, share, nc.vector, w[c + 2])
                if c < 4:
                    load_num(c + 4)
                if c == 2:
                    load_den(7)
                y[c + 1] = wide((4, 1, 0, 3)[c - 1])
                if last:
                    around_y5 = y[5]
                    y[5] = around_y5[:, 1024:3072]
                if c == 1:
                    result(0, 0, 1, on_v)
                if last:
                    result(c - 1, 1, 0, on_s)
                    roots(7)
                r_turn(c + 1, 1)
                product(c, 0, 0)
                fins(c + 1, (0,))
                r_transposes(c + 1, (1,))
                product(c, 0, 1)
                result(c - 1, 1, 1 if last else 0, on_v)
                product(c, 1, 0)
                r_turn(c + 2, 0)
                if last:
                    r_turn(c + 2, 1)
                fins(c + 1, (1,))
                if not last:
                    result(c - 1, 1, 1, on_v)
                product(c, 1, 1)
                if last:
                    r_transposes(c + 2, (1,))
                square_s(c + 3, 0, 2)
                result(c, 0, 0, on_s)
                if not last:
                    square_s(c + 3, 2, 4)
                result(c, 0, 1, on_s)
                if c + 5 < NC:
                    roots(c + 4)
            y_quant(5, 0, 1)
            ratio(7, 0, 2, nc.gpsimd, w[7], words(around_y5))
            y_quant(5, 1, 2)
            y[6], y[7] = wide(5), wide(2)
            product(5, 0, 0)
            product(5, 0, 1)
            fins(6, (0,))
            result(4, 1, 0, on_v)
            fins(6, (1,))
            result(4, 1, 1, on_s)
            square_s(7, 2, 4)
            product(5, 1, 0)
            product(5, 1, 1)
            r_transposes(7, (0,))
            y_quant(6)
            ratio(7, 2, 4, nc.vector, w[7])
            for i, oh in pairs:
                result(5, i, oh, on_s)
            product(6, 0, 0)
            product(6, 0, 1)
            r_transposes(7, (1,))
            product(6, 1, 0)
            product(6, 1, 1)
            yc[7] = code_tiles()
            for i in range(2):
                fins(7, (i,))
                for G in range(2):
                    group_quant(7, i, G)
            for i, oh in pairs:
                result(6, i, oh, on_s)
            for oh in range(2):
                product(7, 0, oh)
            last = [bank_tile([P, 512], next_bank(summed)) for oh in range(2)]
            for G in range(2):
                for oh in range(2):
                    half_pass(7, 1, oh, G, last[oh])
            result(7, 0, 0, on_s)
            result(7, 0, 1, on_v)
            for oh in range(2):
                banks["m2", 7, 1, oh] = last[oh]
                result(7, 1, oh, (on_s, on_v)[oh])
